import numpy as np
import ml_dtypes


def mxq(x, axis, fmt="e4m3"):
    dtype, down = {"e4m3": (ml_dtypes.float8_e4m3fn, 7), "e5m2": (ml_dtypes.float8_e5m2, 14)}[fmt]
    v = np.moveaxis(np.asarray(x, np.float32).astype(ml_dtypes.bfloat16).astype(np.float64), axis, -1)
    blocks = v.reshape(v.shape[:-1] + (-1, 32))
    amax = np.abs(blocks).max(-1, keepdims=True)
    byte = np.maximum(np.where(amax > 0, np.frexp(amax)[1] - 1 + 127, 0) - down, 1)
    scale = np.exp2(byte - 127.0)
    codes = (blocks / scale).astype(np.float32).astype(dtype).astype(np.float64)
    return np.moveaxis((codes * scale).reshape(v.shape), -1, axis)


WIDE = False


def mx_kscale(k):
    if not WIDE:
        return np.ones(k)
    levels = np.array([10, -10, 5, -5, 0])
    a = np.random.permutation(np.resize(levels, k // 512 * 4)).reshape(k // 512, 4)
    idx = np.arange(k)
    return np.exp2(a[idx // 512, idx % 128 // 32])


BF16 = ml_dtypes.bfloat16


def bf(x):
    return np.asarray(x, np.float32).astype(BF16)


def f64(x):
    return np.asarray(x).astype(np.float64)


B, S, L, C, K0, K1, K2, NC = 8, 512, 1024, 2, 512, 128, 16, 10
T = S * L
R = B * S


def setup_inputs():
    t = mx_kscale(K0)
    level = np.random.standard_normal((B, S, C))
    x = np.random.standard_normal((B, S, L, C)) + 0.5 * level[:, :, None, :]
    return {"x": bf(x.reshape(B, T, C)),
            "W0": bf(np.random.standard_normal((C, L, K0)) / np.sqrt(L) * t),
            "b0": bf(np.random.standard_normal((C, K0)) * 0.3 * t),
            "W1": bf(np.random.standard_normal((C, K0, K1)) * 1.4 / np.sqrt(K0) / t[:, None]),
            "b1": bf(np.random.standard_normal((C, K1)) * 0.3)}


def reference(x, W0, b0, W1, b1):
    xc = f64(x).reshape(B, S, L, C)
    mid = (xc.min(axis=2) + xc.max(axis=2)) * 0.5
    norm = xc - mid[:, :, None, :]
    nt = norm.transpose(3, 0, 1, 2).reshape(C, R, L)
    h0 = np.maximum((mxq(nt, 2, "e4m3") @ mxq(f64(W0), 1, "e4m3")) + f64(b0)[:, None, :], 0.0)
    h1 = np.maximum((mxq(h0, 2, "e4m3") @ mxq(f64(W1), 1, "e4m3")) + f64(b1)[:, None, :], 0.0)
    return h1.reshape(C, B, S, K1).transpose(1, 2, 0, 3)

@@ -1,0 +1,251 @@
+from contextlib import ExitStack
+
+import concourse.mybir as mybir
+from concourse.masks import make_identity
+
+BF16 = mybir.dt.bfloat16
+F32 = mybir.dt.float32
+U32 = mybir.dt.uint32
+U8 = mybir.dt.uint8
+FP8X4 = mybir.dt.float8_e4m3fn_x4
+ALU = mybir.AluOpType
+ACT = mybir.ActivationFunctionType
+AX = mybir.AxisListType
+
+P = 128
+NB = 8
+CELLS = 512
+L = 1024
+C = 2
+K0 = 512
+K1 = 128
+NA = 16
+SEG = 256
+FLOPS = 2 * C * NB * CELLS * L * K0 + 2 * C * NB * CELLS * K0 * K1
+
+D_ON_VECTOR = (7,)
+
+
+def tile_shapeletencoder_pa_t_kernel(tc, x, W0, b0, W1, b1, out):
+    nc = tc.nc
+    with ExitStack() as ctx:
+        const = ctx.enter_context(tc.tile_pool(name="const", bufs=1))
+        xpool = ctx.enter_context(tc.tile_pool(name="xpool", bufs=3))
+        scr = ctx.enter_context(tc.tile_pool(name="scr", bufs=1))
+        small = ctx.enter_context(tc.tile_pool(name="small", bufs=2))
+        npool = ctx.enter_context(tc.tile_pool(name="npool", bufs=2))
+        gpool = ctx.enter_context(tc.tile_pool(name="gpool", bufs=3))
+        hpool = ctx.enter_context(tc.tile_pool(name="hpool", bufs=3))
+        opool = ctx.enter_context(tc.tile_pool(name="opool", bufs=2))
+        wstage = ctx.enter_context(tc.tile_pool(name="wstage", bufs=2))
+        ps_tp = ctx.enter_context(tc.psum_pool(name="ps_tp", bufs=2))
+        ps_acc = ctx.enter_context(tc.psum_pool(name="ps_acc", bufs=3))
+        ps_o = ctx.enter_context(tc.psum_pool(name="ps_o", bufs=2))
+        ps_ch = ctx.enter_context(tc.psum_pool(name="ps_ch", bufs=1))
+
+        def load_x(g):
+            xg = xpool.tile([P, NA, 2 * SEG], BF16, name="xg", tag="xg")
+            nc.sync.dma_start(
+                out=xg[:],
+                in_=x[g].rearrange("(a p s) c -> p a (s c)", a=NA, p=P, s=SEG),
+            )
+            return xg
+
+        xs = {}
+        xs[0] = load_x(0)
+
+        w0raw = const.tile([P, 16, K0], BF16, name="w0raw", tag="w0raw")
+        nc.sync.dma_start(out=w0raw[:], in_=W0.rearrange("c (u q) f -> q (c u) f", u=8, q=P))
+        w1raw = const.tile([P, 8, K1], BF16, name="w1raw", tag="w1raw")
+        nc.sync.dma_start(out=w1raw[:], in_=W1.rearrange("c (t p) k -> p (c t) k", t=4, p=P))
+        bz = const.tile([P, P], BF16, name="bz", tag="bz")
+        nc.vector.memset(bz[:], 0.0)
+        nc.sync.dma_start(out=bz[0:8, :], in_=b0.rearrange("c (t p) -> (c t) p", t=4, p=P))
+        b1b = const.tile([P, C * K1], BF16, name="b1b", tag="b1b")
+        nc.sync.dma_start(out=b1b[:], in_=b1.rearrange("c k -> (c k)").partition_broadcast(P))
+        xs[1] = load_x(1)
+
+        identf = const.tile([P, P], F32, name="identf", tag="identf")
+        make_identity(nc, identf[:])
+        identb = const.tile([P, P], BF16, name="identb", tag="identb")
+        make_identity(nc, identb[:])
+        stx = const.tile([P, P], F32, name="stx", tag="stx")
+        nc.vector.memset(stx[:], 0.0)
+        stn = const.tile([P, P], F32, name="stn", tag="stn")
+        nc.vector.memset(stn[:], 0.0)
+
+        bzt = ps_ch.tile([P, P], BF16, name="bzt", tag="ch")
+        nc.tensor.transpose(out=bzt[:], in_=bz[:], identity=identb[:])
+        b0col = const.tile([P, 8], F32, name="b0col", tag="b0col")
+        nc.vector.tensor_copy(out=b0col[:], in_=bzt[:, 0:8])
+
+        w0codes = const.tile([P, C, 2, K0], U32, name="w0codes", tag="w0codes", align_bytes=64)
+        w0sc = const.tile([P, C, 2, K0], U8, name="w0sc", tag="w0sc", align_bytes=64)
+        w0v = w0raw[:].rearrange("q (c t g) f -> q c t g f", c=C, t=4, g=2)
+        for c in range(C):
+            for gk in range(2):
+                w0g = wstage.tile([P, K0, 4], BF16, name="w0g", tag="w0g", align_bytes=64)
+                nc.scalar.copy(
+                    out=w0g[:].rearrange("q (w i) t -> q w t i", i=4),
+                    in_=w0v[:, c, :, gk, :].rearrange("q t (w i) -> q w t i", i=4),
+                )
+                nc.vector.quantize_mx(
+                    out=w0codes[:, c, gk, :].bitcast(FP8X4),
+                    scales=w0sc[:, c, gk, :],
+                    in_=w0g[:].rearrange("q w t -> q (w t)"),
+                )
+        w1codes = const.tile([P, C, K1], U32, name="w1codes", tag="w1codes", align_bytes=64)
+        w1sc = const.tile([P, C, K1], U8, name="w1sc", tag="w1sc", align_bytes=64)
+        w1g = const.tile([P, C, K1, 4], BF16, name="w1g", tag="w1g", align_bytes=64)
+        nc.scalar.copy(
+            out=w1g[:],
+            in_=w1raw[:].rearrange("p (c t) k -> p c k t", c=C, t=4),
+        )
+        nc.vector.quantize_mx(
+            out=w1codes[:].rearrange("p c k -> p (c k)").bitcast(FP8X4),
+            scales=w1sc[:].rearrange("p c k -> p (c k)"),
+            in_=w1g[:].rearrange("p c k t -> p (c k t)"),
+        )
+
+        def stats(xg):
+            hi = scr.tile([P, NA, SEG], BF16, name="hi", tag="hi")
+            lo = scr.tile([P, NA, SEG], BF16, name="lo", tag="lo")
+            nc.vector.tensor_tensor(out=hi[:], in0=xg[:, :, 0:SEG], in1=xg[:, :, SEG : 2 * SEG], op=ALU.max)
+            nc.vector.tensor_tensor(out=lo[:], in0=xg[:, :, 0:SEG], in1=xg[:, :, SEG : 2 * SEG], op=ALU.min)
+            w = SEG
+            while w > 16:
+                h = w // 2
+                nc.vector.tensor_tensor(out=hi[:, :, 0:h], in0=hi[:, :, 0:h], in1=hi[:, :, h:w], op=ALU.max)
+                nc.vector.tensor_tensor(out=lo[:, :, 0:h], in0=lo[:, :, 0:h], in1=lo[:, :, h:w], op=ALU.min)
+                w = h
+            nc.vector.tensor_reduce(
+                out=stx[:, 0:32].rearrange("p (a c) -> p a c", c=C),
+                in_=hi[:, :, 0:16].rearrange("p a (s c) -> p a c s", c=C),
+                axis=AX.X,
+                op=ALU.max,
+            )
+            nc.vector.tensor_reduce(
+                out=stn[:, 0:32].rearrange("p (a c) -> p a c", c=C),
+                in_=lo[:, :, 0:16].rearrange("p a (s c) -> p a c s", c=C),
+                axis=AX.X,
+                op=ALU.min,
+                negate=True,
+            )
+            p1 = ps_ch.tile([P, 2, P], F32, name="p1", tag="ch")
+            nc.tensor.transpose(out=p1[:, 0, :], in_=stx[:], identity=identf[:])
+            nc.tensor.transpose(out=p1[:, 1, :], in_=stn[:], identity=identf[:])
+            red = small.tile([P, 2, 32], F32, name="red", tag="red")
+            nc.vector.tensor_reduce(
+                out=red[:],
+                in_=p1[:].rearrange("q s (e t) -> q s e t", t=4),
+                axis=AX.X,
+                op=ALU.max,
+            )
+            nsum = small.tile([P, 32, 4], F32, name="nsum", tag="nsum")
+            nc.vector.tensor_tensor(
+                out=nsum[:],
+                in0=red[:, 1, :].unsqueeze(2).to_broadcast([P, 32, 4]),
+                in1=red[:, 0, :].unsqueeze(2).to_broadcast([P, 32, 4]),
+                op=ALU.subtract,
+            )
+            p2 = ps_ch.tile([P, P], F32, name="p2", tag="ch")
+            nc.tensor.transpose(out=p2[:], in_=nsum[:].rearrange("q e t -> q (e t)"), identity=identf[:])
+            negmid = small.tile([P, 32], F32, name="negmid", tag="negmid")
+            nc.vector.tensor_scalar(out=negmid[:], in0=p2[:, 0:32], scalar1=0.5, scalar2=None, op0=ALU.mult)
+            return negmid
+
+        for g in range(NB):
+            if g + 2 < NB:
+                xs[g + 2] = load_x(g + 2)
+            xg = xs[g]
+            negmid = stats(xg)
+            nt = npool.tile([P, NA, C, SEG], BF16, name="nt", tag="nt")
+            o_ps = [ps_o.tile([P, 2, C, K1], F32, name="o_ps%d" % jp, tag="o") for jp in range(2)]
+            osb = opool.tile([P, 4, C, K1], F32, name="osb", tag="osb")
+            for c in range(C):
+                gn = gpool.tile([P, 2, 4 * CELLS], BF16, name="gn", tag="gn", align_bytes=64)
+                for h in range(2):
+                    for i in range(8):
+                        a = 8 * h + i
+                        nc.scalar.activation(
+                            out=nt[:, a, c, :],
+                            in_=xg[:, a, :].rearrange("p (s c) -> p s c", c=C)[:, :, c],
+                            func=ACT.Identity,
+                            bias=negmid[:, 2 * a + c : 2 * a + c + 1],
+                            scale=1.0,
+                        )
+                    for gk in range(2):
+                        tp = ps_tp.tile([P, 8 * P], BF16, name="tp", tag="tp")
+                        for i in range(8):
+                            nc.tensor.transpose(
+                                out=tp[:, P * i : P * (i + 1)],
+                                in_=nt[:, 8 * h + i, c, P * gk : P * (gk + 1)],
+                                identity=identb[:],
+                            )
+                        dst = gn[:, gk, 1024 * h : 1024 * (h + 1)]
+                        if 4 * c + 2 * h + gk in D_ON_VECTOR:
+                            nc.vector.tensor_copy(out=dst, in_=tp[:])
+                        else:
+                            nc.scalar.copy(out=dst, in_=tp[:])
+                ncodes = gpool.tile([P, 2, CELLS], U32, name="ncodes", tag="ncodes", align_bytes=64)
+                nsc = gpool.tile([P, 2, CELLS], U8, name="nsc", tag="nsc", align_bytes=64)
+                nc.vector.quantize_mx(
+                    out=ncodes[:].rearrange("p g w -> p (g w)").bitcast(FP8X4),
+                    scales=nsc[:].rearrange("p g w -> p (g w)"),
+                    in_=gn[:].rearrange("p g w -> p (g w)"),
+                )
+                hp = hpool.tile([P, 4, CELLS], BF16, name="hp", tag="hp")
+                for m in range(4):
+                    acc = ps_acc.tile([P, CELLS], F32, name="acc", tag="acc")
+                    for gk in range(2):
+                        nc.tensor.matmul_mx(
+                            out=acc[:],
+                            lhsT=w0codes[:, c, gk, P * m : P * (m + 1)].bitcast(FP8X4),
+                            lhsT_scale=w0sc[:, c, gk, P * m : P * (m + 1)],
+                            rhs=ncodes[:, gk, :].bitcast(FP8X4),
+                            rhs_scale=nsc[:, gk, :],
+                            start=(gk == 0),
+                            stop=(gk == 1),
+                        )
+                    nc.scalar.activation(
+                        out=hp[:, m, :],
+                        in_=acc[:],
+                        func=ACT.Relu,
+                        bias=b0col[:, 4 * c + m : 4 * c + m + 1],
+                        scale=1.0,
+                    )
+                hg = hpool.tile([P, CELLS, 4], BF16, name="hg", tag="hg", align_bytes=64)
+                nc.vector.tensor_copy(
+                    out=hg[:].rearrange("p (w i) t -> p w t i", i=4),
+                    in_=hp[:].rearrange("p t (w i) -> p w t i", i=4),
+                )
+                hcodes = hpool.tile([P, CELLS], U32, name="hcodes", tag="hcodes", align_bytes=64)
+                hsc = hpool.tile([P, CELLS], U8, name="hsc", tag="hsc", align_bytes=64)
+                nc.vector.quantize_mx(
+                    out=hcodes[:].bitcast(FP8X4),
+                    scales=hsc[:],
+                    in_=hg[:].rearrange("p w t -> p (w t)"),
+                )
+                for jj in range(4):
+                    nc.tensor.matmul_mx(
+                        out=o_ps[jj // 2][:, jj % 2, c, :],
+                        lhsT=hcodes[:, P * jj : P * (jj + 1)].bitcast(FP8X4),
+                        lhsT_scale=hsc[:, P * jj : P * (jj + 1)],
+                        rhs=w1codes[:, c, :].bitcast(FP8X4),
+                        rhs_scale=w1sc[:, c, :],
+                        start=True,
+                        stop=True,
+                    )
+            for jp in range(2):
+                nc.vector.tensor_tensor(
+                    out=osb[:, 2 * jp : 2 * jp + 2, :, :].rearrange("p j c k -> p j (c k)"),
+                    in0=o_ps[jp][:].rearrange("p j c k -> p j (c k)"),
+                    in1=b1b[:].unsqueeze(1).to_broadcast([P, 2, C * K1]),
+                    op=ALU.add,
+                )
+            flat = osb[:].rearrange("p j c k -> p (j c k)")
+            nc.vector.tensor_scalar_max(out=flat, in0=flat, scalar1=0.0)
+            nc.sync.dma_start(
+                out=out[g].rearrange("(j p) c k -> p j (c k)", p=P),
+                in_=osb[:].rearrange("p j c k -> p j (c k)"),
+            )

@@ -13,7 +13,7 @@ ACT = mybir.ActivationFunctionType
 AX = mybir.AxisListType
 
 P = 128
-NB = 8
+NG = 8
 CELLS = 512
 L = 1024
 C = 2
@@ -21,9 +21,23 @@ K0 = 512
 K1 = 128
 NA = 16
 SEG = 256
-FLOPS = 2 * C * NB * CELLS * L * K0 + 2 * C * NB * CELLS * K0 * K1
+FLOPS = 2 * C * NG * CELLS * L * K0 + 2 * C * NG * CELLS * K0 * K1
 
-D_ON_VECTOR = (7,)
+NSLOT = 4 * NG
+LAG_A = 5
+LAG_Q = 3
+LAG_U = 3
+LAG_F = 4
+LAG_G = 6
+LAG_L1 = 7
+LAG_I = 8
+A_PARTS = ((0,), (1,), (2, 3, 4), (5, 6, 7, 8, 9, 10, 11))
+W_REGROUP_SLOTS = (-2, -1, 1, 2)
+W_QUANT_SLOTS = (-1, 0, 2, 3)
+
+
+def b_on_vector(k):
+    return 6 if k >= 28 else 1
 
 
 def tile_shapeletencoder_pa_t_kernel(tc, x, W0, b0, W1, b1, out):
@@ -35,35 +49,60 @@ def tile_shapeletencoder_pa_t_kernel(tc, x, W0, b0, W1, b1, out):
         small = ctx.enter_context(tc.tile_pool(name="small", bufs=2))
         npool = ctx.enter_context(tc.tile_pool(name="npool", bufs=2))
         gpool = ctx.enter_context(tc.tile_pool(name="gpool", bufs=3))
-        hpool = ctx.enter_context(tc.tile_pool(name="hpool", bufs=3))
+        hpool = ctx.enter_context(tc.tile_pool(name="hpool", bufs=2))
         opool = ctx.enter_context(tc.tile_pool(name="opool", bufs=2))
         wstage = ctx.enter_context(tc.tile_pool(name="wstage", bufs=2))
         ps_tp = ctx.enter_context(tc.psum_pool(name="ps_tp", bufs=2))
-        ps_acc = ctx.enter_context(tc.psum_pool(name="ps_acc", bufs=3))
-        ps_o = ctx.enter_context(tc.psum_pool(name="ps_o", bufs=2))
+        ps_acc = ctx.enter_context(tc.psum_pool(name="ps_acc", bufs=4))
+        ps_o = ctx.enter_context(tc.psum_pool(name="ps_o", bufs=1))
         ps_ch = ctx.enter_context(tc.psum_pool(name="ps_ch", bufs=1))
-
-        def load_x(g):
-            xg = xpool.tile([P, NA, 2 * SEG], BF16, name="xg", tag="xg")
-            nc.sync.dma_start(
-                out=xg[:],
-                in_=x[g].rearrange("(a p s) c -> p a (s c)", a=NA, p=P, s=SEG),
-            )
-            return xg
+        ctx.enter_context(tc.manual_schedule())
 
         xs = {}
-        xs[0] = load_x(0)
+        his = {}
+        los = {}
+        p1s = {}
+        nsums = {}
+        p2s = {}
+        negmids = {}
+        nts = {}
+        tps = {}
+        gns = {}
+        ncs = {}
+        accs = {}
+        hps = {}
+        hgs = {}
+        hcs = {}
+        ops_ = {}
+        osbs = {}
+        w0gs = {}
 
-        w0raw = const.tile([P, 16, K0], BF16, name="w0raw", tag="w0raw")
-        nc.sync.dma_start(out=w0raw[:], in_=W0.rearrange("c (u q) f -> q (c u) f", u=8, q=P))
-        w1raw = const.tile([P, 8, K1], BF16, name="w1raw", tag="w1raw")
-        nc.sync.dma_start(out=w1raw[:], in_=W1.rearrange("c (t p) k -> p (c t) k", t=4, p=P))
+        def x_view(g):
+            return x[g].rearrange("(a p s) c -> p a (s c)", a=NA, p=P, s=SEG)
+
+        def load_x(g):
+            xs[g] = xpool.tile([P, NA, 2 * SEG], BF16, name="xg", tag="xg")
+            nc.sync.dma_start(out=xs[g][:], in_=x_view(g))
+
+        xs[0] = xpool.tile([P, NA, 2 * SEG], BF16, name="xg", tag="xg")
+        for i in range(4):
+            nc.sync.dma_start(out=xs[0][:, 4 * i : 4 * i + 4, :], in_=x_view(0)[:, 4 * i : 4 * i + 4, :])
+        w0raw = const.tile([P, C, 8, K0], BF16, name="w0raw", tag="w0raw")
+        w0dram = W0.rearrange("c (u q) f -> q c u f", u=8, q=P)
+        nc.sync.dma_start(out=w0raw[:, 0, :, :], in_=w0dram[:, 0, :, :])
+        load_x(1)
         bz = const.tile([P, P], BF16, name="bz", tag="bz")
         nc.vector.memset(bz[:], 0.0)
         nc.sync.dma_start(out=bz[0:8, :], in_=b0.rearrange("c (t p) -> (c t) p", t=4, p=P))
-        b1b = const.tile([P, C * K1], BF16, name="b1b", tag="b1b")
-        nc.sync.dma_start(out=b1b[:], in_=b1.rearrange("c k -> (c k)").partition_broadcast(P))
-        xs[1] = load_x(1)
+        nc.sync.dma_start(out=w0raw[:, 1, :, :], in_=w0dram[:, 1, :, :])
+        w1raw = const.tile([P, 8, K1], BF16, name="w1raw", tag="w1raw")
+        nc.sync.dma_start(out=w1raw[:], in_=W1.rearrange("c (t p) k -> p (c t) k", t=4, p=P))
+        load_x(2)
+        b1b = const.tile([P, C, K1], BF16, name="b1b", tag="b1b")
+        nc.sync.dma_start(
+            out=b1b[:].rearrange("p c k -> p (c k)"),
+            in_=b1.rearrange("c k -> (c k)").partition_broadcast(P),
+        )
 
         identf = const.tile([P, P], F32, name="identf", tag="identf")
         make_identity(nc, identf[:])
@@ -73,179 +112,271 @@ def tile_shapeletencoder_pa_t_kernel(tc, x, W0, b0, W1, b1, out):
         nc.vector.memset(stx[:], 0.0)
         stn = const.tile([P, P], F32, name="stn", tag="stn")
         nc.vector.memset(stn[:], 0.0)
-
-        bzt = ps_ch.tile([P, P], BF16, name="bzt", tag="ch")
-        nc.tensor.transpose(out=bzt[:], in_=bz[:], identity=identb[:])
         b0col = const.tile([P, 8], F32, name="b0col", tag="b0col")
-        nc.vector.tensor_copy(out=b0col[:], in_=bzt[:, 0:8])
-
         w0codes = const.tile([P, C, 2, K0], U32, name="w0codes", tag="w0codes", align_bytes=64)
         w0sc = const.tile([P, C, 2, K0], U8, name="w0sc", tag="w0sc", align_bytes=64)
-        w0v = w0raw[:].rearrange("q (c t g) f -> q c t g f", c=C, t=4, g=2)
-        for c in range(C):
-            for gk in range(2):
-                w0g = wstage.tile([P, K0, 4], BF16, name="w0g", tag="w0g", align_bytes=64)
-                nc.scalar.copy(
-                    out=w0g[:].rearrange("q (w i) t -> q w t i", i=4),
-                    in_=w0v[:, c, :, gk, :].rearrange("q t (w i) -> q w t i", i=4),
-                )
-                nc.vector.quantize_mx(
-                    out=w0codes[:, c, gk, :].bitcast(FP8X4),
-                    scales=w0sc[:, c, gk, :],
-                    in_=w0g[:].rearrange("q w t -> q (w t)"),
-                )
         w1codes = const.tile([P, C, K1], U32, name="w1codes", tag="w1codes", align_bytes=64)
         w1sc = const.tile([P, C, K1], U8, name="w1sc", tag="w1sc", align_bytes=64)
         w1g = const.tile([P, C, K1, 4], BF16, name="w1g", tag="w1g", align_bytes=64)
-        nc.scalar.copy(
-            out=w1g[:],
-            in_=w1raw[:].rearrange("p (c t) k -> p c k t", c=C, t=4),
-        )
-        nc.vector.quantize_mx(
-            out=w1codes[:].rearrange("p c k -> p (c k)").bitcast(FP8X4),
-            scales=w1sc[:].rearrange("p c k -> p (c k)"),
-            in_=w1g[:].rearrange("p c k t -> p (c k t)"),
-        )
 
-        def stats(xg):
-            hi = scr.tile([P, NA, SEG], BF16, name="hi", tag="hi")
-            lo = scr.tile([P, NA, SEG], BF16, name="lo", tag="lo")
-            nc.vector.tensor_tensor(out=hi[:], in0=xg[:, :, 0:SEG], in1=xg[:, :, SEG : 2 * SEG], op=ALU.max)
-            nc.vector.tensor_tensor(out=lo[:], in0=xg[:, :, 0:SEG], in1=xg[:, :, SEG : 2 * SEG], op=ALU.min)
-            w = SEG
-            while w > 16:
-                h = w // 2
-                nc.vector.tensor_tensor(out=hi[:, :, 0:h], in0=hi[:, :, 0:h], in1=hi[:, :, h:w], op=ALU.max)
-                nc.vector.tensor_tensor(out=lo[:, :, 0:h], in0=lo[:, :, 0:h], in1=lo[:, :, h:w], op=ALU.min)
-                w = h
-            nc.vector.tensor_reduce(
-                out=stx[:, 0:32].rearrange("p (a c) -> p a c", c=C),
-                in_=hi[:, :, 0:16].rearrange("p a (s c) -> p a c s", c=C),
-                axis=AX.X,
-                op=ALU.max,
-            )
-            nc.vector.tensor_reduce(
-                out=stn[:, 0:32].rearrange("p (a c) -> p a c", c=C),
-                in_=lo[:, :, 0:16].rearrange("p a (s c) -> p a c s", c=C),
-                axis=AX.X,
-                op=ALU.min,
-                negate=True,
-            )
-            p1 = ps_ch.tile([P, 2, P], F32, name="p1", tag="ch")
-            nc.tensor.transpose(out=p1[:, 0, :], in_=stx[:], identity=identf[:])
-            nc.tensor.transpose(out=p1[:, 1, :], in_=stn[:], identity=identf[:])
+        def a_op(g, idx):
+            xg = xs[g]
+            if idx == 0:
+                his[g] = scr.tile([P, NA, SEG], BF16, name="hi", tag="hi")
+                los[g] = scr.tile([P, NA, SEG], BF16, name="lo", tag="lo")
+            t = his[g] if idx % 2 == 0 else los[g]
+            op = ALU.max if idx % 2 == 0 else ALU.min
+            if idx < 2 and g == 0:
+                for i in range(4 if idx == 0 else 0):
+                    for tt, oo in ((his[g], ALU.max), (los[g], ALU.min)):
+                        nc.vector.tensor_tensor(
+                            out=tt[:, 4 * i : 4 * i + 4, :],
+                            in0=xg[:, 4 * i : 4 * i + 4, 0:SEG],
+                            in1=xg[:, 4 * i : 4 * i + 4, SEG : 2 * SEG],
+                            op=oo,
+                        )
+            elif idx < 2:
+                nc.vector.tensor_tensor(out=t[:], in0=xg[:, :, 0:SEG], in1=xg[:, :, SEG : 2 * SEG], op=op)
+            elif idx < 10:
+                h = SEG >> (idx // 2)
+                nc.vector.tensor_tensor(out=t[:, :, 0:h], in0=t[:, :, 0:h], in1=t[:, :, h : 2 * h], op=op)
+            else:
+                st = stx if idx == 10 else stn
+                nc.vector.tensor_reduce(
+                    out=st[:, 0:32].rearrange("p (a c) -> p a c", c=C),
+                    in_=t[:, :, 0:16].rearrange("p a (s c) -> p a c s", c=C),
+                    axis=AX.X,
+                    op=op,
+                    negate=(idx == 11),
+                )
+
+        def chain1(g):
+            p1s[g] = ps_ch.tile([P, 2, P], F32, name="p1", tag="ch")
+            nc.tensor.transpose(out=p1s[g][:, 0, :], in_=stx[:], identity=identf[:])
+            nc.tensor.transpose(out=p1s[g][:, 1, :], in_=stn[:], identity=identf[:])
+
+        def chain2(g):
             red = small.tile([P, 2, 32], F32, name="red", tag="red")
             nc.vector.tensor_reduce(
-                out=red[:],
-                in_=p1[:].rearrange("q s (e t) -> q s e t", t=4),
-                axis=AX.X,
-                op=ALU.max,
+                out=red[:], in_=p1s[g][:].rearrange("q s (e t) -> q s e t", t=4), axis=AX.X, op=ALU.max
             )
-            nsum = small.tile([P, 32, 4], F32, name="nsum", tag="nsum")
+            nsums[g] = small.tile([P, 32, 4], F32, name="nsum", tag="nsum")
             nc.vector.tensor_tensor(
-                out=nsum[:],
+                out=nsums[g][:],
                 in0=red[:, 1, :].unsqueeze(2).to_broadcast([P, 32, 4]),
                 in1=red[:, 0, :].unsqueeze(2).to_broadcast([P, 32, 4]),
                 op=ALU.subtract,
             )
-            p2 = ps_ch.tile([P, P], F32, name="p2", tag="ch")
-            nc.tensor.transpose(out=p2[:], in_=nsum[:].rearrange("q e t -> q (e t)"), identity=identf[:])
-            negmid = small.tile([P, 32], F32, name="negmid", tag="negmid")
-            nc.vector.tensor_scalar(out=negmid[:], in0=p2[:, 0:32], scalar1=0.5, scalar2=None, op0=ALU.mult)
-            return negmid
 
-        for g in range(NB):
-            if g + 2 < NB:
-                xs[g + 2] = load_x(g + 2)
-            xg = xs[g]
-            negmid = stats(xg)
-            nt = npool.tile([P, NA, C, SEG], BF16, name="nt", tag="nt")
-            o_ps = [ps_o.tile([P, 2, C, K1], F32, name="o_ps%d" % jp, tag="o") for jp in range(2)]
-            osb = opool.tile([P, 4, C, K1], F32, name="osb", tag="osb")
-            for c in range(C):
-                gn = gpool.tile([P, 2, 4 * CELLS], BF16, name="gn", tag="gn", align_bytes=64)
-                for h in range(2):
-                    for i in range(8):
-                        a = 8 * h + i
-                        nc.scalar.activation(
-                            out=nt[:, a, c, :],
-                            in_=xg[:, a, :].rearrange("p (s c) -> p s c", c=C)[:, :, c],
-                            func=ACT.Identity,
-                            bias=negmid[:, 2 * a + c : 2 * a + c + 1],
-                            scale=1.0,
-                        )
-                    for gk in range(2):
-                        tp = ps_tp.tile([P, 8 * P], BF16, name="tp", tag="tp")
-                        for i in range(8):
-                            nc.tensor.transpose(
-                                out=tp[:, P * i : P * (i + 1)],
-                                in_=nt[:, 8 * h + i, c, P * gk : P * (gk + 1)],
-                                identity=identb[:],
-                            )
-                        dst = gn[:, gk, 1024 * h : 1024 * (h + 1)]
-                        if 4 * c + 2 * h + gk in D_ON_VECTOR:
-                            nc.vector.tensor_copy(out=dst, in_=tp[:])
-                        else:
-                            nc.scalar.copy(out=dst, in_=tp[:])
-                ncodes = gpool.tile([P, 2, CELLS], U32, name="ncodes", tag="ncodes", align_bytes=64)
-                nsc = gpool.tile([P, 2, CELLS], U8, name="nsc", tag="nsc", align_bytes=64)
-                nc.vector.quantize_mx(
-                    out=ncodes[:].rearrange("p g w -> p (g w)").bitcast(FP8X4),
-                    scales=nsc[:].rearrange("p g w -> p (g w)"),
-                    in_=gn[:].rearrange("p g w -> p (g w)"),
-                )
-                hp = hpool.tile([P, 4, CELLS], BF16, name="hp", tag="hp")
-                for m in range(4):
-                    acc = ps_acc.tile([P, CELLS], F32, name="acc", tag="acc")
-                    for gk in range(2):
-                        nc.tensor.matmul_mx(
-                            out=acc[:],
-                            lhsT=w0codes[:, c, gk, P * m : P * (m + 1)].bitcast(FP8X4),
-                            lhsT_scale=w0sc[:, c, gk, P * m : P * (m + 1)],
-                            rhs=ncodes[:, gk, :].bitcast(FP8X4),
-                            rhs_scale=nsc[:, gk, :],
-                            start=(gk == 0),
-                            stop=(gk == 1),
-                        )
+        def chain3(g):
+            p2s[g] = ps_ch.tile([P, P], F32, name="p2", tag="ch")
+            nc.tensor.transpose(out=p2s[g][:], in_=nsums[g][:].rearrange("q e t -> q (e t)"), identity=identf[:])
+
+        def chain4(g):
+            negmids[g] = small.tile([P, 32], F32, name="negmid", tag="negmid")
+            nc.vector.tensor_scalar(
+                out=negmids[g][:], in0=p2s[g][:, 0:32], scalar1=0.5, scalar2=None, op0=ALU.mult
+            )
+
+        def subtract(k):
+            g, c, h = k // 4, (k // 2) % 2, k % 2
+            if k % 4 == 0:
+                nts[g] = npool.tile([P, NA, C, SEG], BF16, name="nt", tag="nt")
+            nv = b_on_vector(k)
+            for i in range(8):
+                a = 8 * h + i
+                src = xs[g][:, a, :].rearrange("p (s c) -> p s c", c=C)[:, :, c]
+                bias = negmids[g][:, 2 * a + c : 2 * a + c + 1]
+                if i < nv:
+                    nc.vector.tensor_scalar(
+                        out=nts[g][:, a, c, :], in0=src, scalar1=bias, scalar2=None, op0=ALU.add
+                    )
+                else:
                     nc.scalar.activation(
-                        out=hp[:, m, :],
-                        in_=acc[:],
-                        func=ACT.Relu,
-                        bias=b0col[:, 4 * c + m : 4 * c + m + 1],
-                        scale=1.0,
+                        out=nts[g][:, a, c, :], in_=src, func=ACT.Identity, bias=bias, scale=1.0
                     )
-                hg = hpool.tile([P, CELLS, 4], BF16, name="hg", tag="hg", align_bytes=64)
-                nc.vector.tensor_copy(
-                    out=hg[:].rearrange("p (w i) t -> p w t i", i=4),
-                    in_=hp[:].rearrange("p t (w i) -> p w t i", i=4),
+
+        def transposes(k, gk):
+            g, c, h = k // 4, (k // 2) % 2, k % 2
+            tp = ps_tp.tile([P, 8 * P], BF16, name="tp", tag="tp")
+            tps[(k, gk)] = tp
+            for i in range(8):
+                nc.tensor.transpose(
+                    out=tp[:, P * i : P * (i + 1)],
+                    in_=nts[g][:, 8 * h + i, c, P * gk : P * (gk + 1)],
+                    identity=identb[:],
                 )
-                hcodes = hpool.tile([P, CELLS], U32, name="hcodes", tag="hcodes", align_bytes=64)
-                hsc = hpool.tile([P, CELLS], U8, name="hsc", tag="hsc", align_bytes=64)
-                nc.vector.quantize_mx(
-                    out=hcodes[:].bitcast(FP8X4),
-                    scales=hsc[:],
-                    in_=hg[:].rearrange("p w t -> p (w t)"),
+
+        def evacuate(k, gk):
+            chi, h = k // 2, k % 2
+            if h == 0 and gk == 0:
+                gns[chi] = gpool.tile([P, 2, 4 * CELLS], BF16, name="gn", tag="gn", align_bytes=64)
+            nc.scalar.copy(out=gns[chi][:, gk, 1024 * h : 1024 * (h + 1)], in_=tps[(k, gk)][:])
+
+        def quantise_n(chi):
+            codes = gpool.tile([P, 2, CELLS], U32, name="ncodes", tag="ncodes", align_bytes=64)
+            sc = gpool.tile([P, 2, CELLS], U8, name="nsc", tag="nsc", align_bytes=64)
+            ncs[chi] = (codes, sc)
+            nc.vector.quantize_mx(
+                out=codes[:].rearrange("p g w -> p (g w)").bitcast(FP8X4),
+                scales=sc[:].rearrange("p g w -> p (g w)"),
+                in_=gns[chi][:].rearrange("p g w -> p (g w)"),
+            )
+
+        def layer0(u):
+            chi, m = u // 4, u % 4
+            c = chi % 2
+            codes, sc = ncs[chi]
+            accs[u] = ps_acc.tile([P, CELLS], F32, name="acc", tag="acc")
+            for gk in range(2):
+                nc.tensor.matmul_mx(
+                    out=accs[u][:],
+                    lhsT=w0codes[:, c, gk, P * m : P * (m + 1)].bitcast(FP8X4),
+                    lhsT_scale=w0sc[:, c, gk, P * m : P * (m + 1)],
+                    rhs=codes[:, gk, :].bitcast(FP8X4),
+                    rhs_scale=sc[:, gk, :],
+                    start=(gk == 0),
+                    stop=(gk == 1),
                 )
-                for jj in range(4):
-                    nc.tensor.matmul_mx(
-                        out=o_ps[jj // 2][:, jj % 2, c, :],
-                        lhsT=hcodes[:, P * jj : P * (jj + 1)].bitcast(FP8X4),
-                        lhsT_scale=hsc[:, P * jj : P * (jj + 1)],
-                        rhs=w1codes[:, c, :].bitcast(FP8X4),
-                        rhs_scale=w1sc[:, c, :],
-                        start=True,
-                        stop=True,
-                    )
-            for jp in range(2):
-                nc.vector.tensor_tensor(
-                    out=osb[:, 2 * jp : 2 * jp + 2, :, :].rearrange("p j c k -> p j (c k)"),
-                    in0=o_ps[jp][:].rearrange("p j c k -> p j (c k)"),
-                    in1=b1b[:].unsqueeze(1).to_broadcast([P, 2, C * K1]),
-                    op=ALU.add,
+
+        def relu0(u):
+            chi, m = u // 4, u % 4
+            c = chi % 2
+            if m == 0:
+                hps[chi] = hpool.tile([P, 4, CELLS], BF16, name="hp", tag="hp")
+            nc.scalar.activation(
+                out=hps[chi][:, m, :],
+                in_=accs[u][:],
+                func=ACT.Relu,
+                bias=b0col[:, 4 * c + m : 4 * c + m + 1],
+                scale=1.0,
+            )
+
+        def regroup_h(chi):
+            hgs[chi] = hpool.tile([P, CELLS, 4], BF16, name="hg", tag="hg", align_bytes=64)
+            nc.vector.tensor_copy(
+                out=hgs[chi][:].rearrange("p (w i) t -> p w t i", i=4),
+                in_=hps[chi][:].rearrange("p t (w i) -> p w t i", i=4),
+            )
+
+        def quantise_h(chi):
+            codes = hpool.tile([P, CELLS], U32, name="hcodes", tag="hcodes", align_bytes=64)
+            sc = hpool.tile([P, CELLS], U8, name="hsc", tag="hsc", align_bytes=64)
+            hcs[chi] = (codes, sc)
+            nc.vector.quantize_mx(
+                out=codes[:].bitcast(FP8X4), scales=sc[:], in_=hgs[chi][:].rearrange("p w t -> p (w t)")
+            )
+
+        def layer1(chi):
+            c = chi % 2
+            codes, sc = hcs[chi]
+            ops_[chi] = ps_o.tile([P, 4, K1], F32, name="o_ps", tag="o")
+            for jj in range(4):
+                nc.tensor.matmul_mx(
+                    out=ops_[chi][:, jj, :],
+                    lhsT=codes[:, P * jj : P * (jj + 1)].bitcast(FP8X4),
+                    lhsT_scale=sc[:, P * jj : P * (jj + 1)],
+                    rhs=w1codes[:, c, :].bitcast(FP8X4),
+                    rhs_scale=w1sc[:, c, :],
+                    start=True,
+                    stop=True,
                 )
-            flat = osb[:].rearrange("p j c k -> p (j c k)")
+
+        def bias1(chi):
+            g, c = chi // 2, chi % 2
+            if c == 0:
+                osbs[g] = opool.tile([P, 4, C, K1], F32, name="osb", tag="osb")
+            nc.vector.tensor_tensor(
+                out=osbs[g][:, :, c, :],
+                in0=ops_[chi][:],
+                in1=b1b[:, c, :].unsqueeze(1).to_broadcast([P, 4, K1]),
+                op=ALU.add,
+            )
+
+        def finish(g):
+            flat = osbs[g][:].rearrange("p j c k -> p (j c k)")
             nc.vector.tensor_scalar_max(out=flat, in0=flat, scalar1=0.0)
             nc.sync.dma_start(
                 out=out[g].rearrange("(j p) c k -> p j (c k)", p=P),
-                in_=osb[:].rearrange("p j c k -> p j (c k)"),
+                in_=osbs[g][:].rearrange("p j c k -> p j (c k)"),
             )
+
+        def regroup_w0(i):
+            c, gk = i // 2, i % 2
+            w0gs[i] = wstage.tile([P, K0, 4], BF16, name="w0g", tag="w0g", align_bytes=64)
+            src = w0raw[:, c, :, :].rearrange("q (t g) f -> q t g f", t=4, g=2)[:, :, gk, :]
+            nc.scalar.copy(
+                out=w0gs[i][:].rearrange("q (w i) t -> q w t i", i=4),
+                in_=src.rearrange("q t (w i) -> q w t i", i=4),
+            )
+
+        def quantise_w0(i):
+            c, gk = i // 2, i % 2
+            nc.vector.quantize_mx(
+                out=w0codes[:, c, gk, :].bitcast(FP8X4),
+                scales=w0sc[:, c, gk, :],
+                in_=w0gs[i][:].rearrange("q w t -> q (w t)"),
+            )
+
+        for k in range(-LAG_A, NSLOT + LAG_I + 3):
+            if k % 4 == 0 and 3 <= k // 4 + 2 < NG:
+                load_x(k // 4 + 2)
+            if 0 <= k < NSLOT:
+                subtract(k)
+            if 0 <= k - 1 < NSLOT:
+                transposes(k - 1, 1)
+            if k in W_REGROUP_SLOTS:
+                regroup_w0(W_REGROUP_SLOTS.index(k))
+            if k == 0:
+                bzt = ps_ch.tile([P, P], BF16, name="bzt", tag="ch")
+                nc.tensor.transpose(out=bzt[:], in_=bz[:], identity=identb[:])
+            if k == 3:
+                nc.scalar.copy(out=w1g[:], in_=w1raw[:].rearrange("p (c t) k -> p c k t", c=C, t=4))
+            gc = (k + 1) // 4
+            chain_now = (k + 1) % 4 == 0 and 0 <= gc < NG
+            if chain_now:
+                chain2(gc)
+                chain3(gc)
+            if (k - LAG_Q) % 2 == 0 and 0 <= (k - LAG_Q) // 2 < 2 * NG:
+                quantise_n((k - LAG_Q) // 2)
+            if (k - LAG_G) % 2 == 0 and 0 <= (k - LAG_G) // 2 < 2 * NG:
+                regroup_h((k - LAG_G) // 2)
+            if chain_now:
+                chain4(gc)
+            if 0 <= 2 * (k - LAG_U) < 8 * NG:
+                layer0(2 * (k - LAG_U))
+            if 0 <= k - 1 < NSLOT:
+                evacuate(k - 1, 0)
+                evacuate(k - 1, 1)
+            ga, j = (k + LAG_A) // 4, (k + LAG_A) % 4
+            if ga < NG:
+                for idx in A_PARTS[j]:
+                    a_op(ga, idx)
+                if j == 3:
+                    chain1(ga)
+            if k == 0:
+                nc.vector.tensor_copy(out=b0col[:], in_=bzt[:, 0:8])
+            if k in W_QUANT_SLOTS:
+                quantise_w0(W_QUANT_SLOTS.index(k))
+            if k == 4:
+                nc.vector.quantize_mx(
+                    out=w1codes[:].rearrange("p c k -> p (c k)").bitcast(FP8X4),
+                    scales=w1sc[:].rearrange("p c k -> p (c k)"),
+                    in_=w1g[:].rearrange("p c k t -> p (c k t)"),
+                )
+            if 0 <= k < NSLOT:
+                transposes(k, 0)
+            if 0 <= 2 * (k - LAG_U) < 8 * NG:
+                layer0(2 * (k - LAG_U) + 1)
+            if (k - LAG_L1) % 2 == 0 and 0 <= (k - LAG_L1) // 2 < 2 * NG:
+                layer1((k - LAG_L1) // 2)
+            if 0 <= 2 * (k - LAG_F) < 8 * NG:
+                relu0(2 * (k - LAG_F))
+                relu0(2 * (k - LAG_F) + 1)
+            if (k - LAG_G) % 2 == 0 and 0 <= (k - LAG_G) // 2 < 2 * NG:
+                quantise_h((k - LAG_G) // 2)
+            if (k - LAG_I) % 2 == 0 and 0 <= (k - LAG_I) // 2 < 2 * NG:
+                chi = (k - LAG_I) // 2
+                bias1(chi)
+                if chi % 2 == 1:
+                    finish(chi // 2)

@@ -31,6 +31,7 @@ LAG_F = 4
 LAG_G = 6
 LAG_L1 = 7
 LAG_I = 8
+LAG_I2 = 9
 A_PARTS = ((0,), (1,), (2, 3, 4), (5, 6, 7, 8, 9, 10, 11))
 W_REGROUP_SLOTS = (-2, -1, 1, 2)
 W_QUANT_SLOTS = (-1, 0, 2, 3)
@@ -62,6 +63,7 @@ def tile_shapeletencoder_pa_t_kernel(tc, x, W0, b0, W1, b1, out):
         his = {}
         los = {}
         p1s = {}
+        reds = {}
         nsums = {}
         p2s = {}
         negmids = {}
@@ -155,11 +157,14 @@ def tile_shapeletencoder_pa_t_kernel(tc, x, W0, b0, W1, b1, out):
             nc.tensor.transpose(out=p1s[g][:, 0, :], in_=stx[:], identity=identf[:])
             nc.tensor.transpose(out=p1s[g][:, 1, :], in_=stn[:], identity=identf[:])
 
-        def chain2(g):
-            red = small.tile([P, 2, 32], F32, name="red", tag="red")
+        def chain2a(g):
+            reds[g] = small.tile([P, 2, 32], F32, name="red", tag="red")
             nc.vector.tensor_reduce(
-                out=red[:], in_=p1s[g][:].rearrange("q s (e t) -> q s e t", t=4), axis=AX.X, op=ALU.max
+                out=reds[g][:], in_=p1s[g][:].rearrange("q s (e t) -> q s e t", t=4), axis=AX.X, op=ALU.max
             )
+
+        def chain2b(g):
+            red = reds[g]
             nsums[g] = small.tile([P, 32, 4], F32, name="nsum", tag="nsum")
             nc.vector.tensor_tensor(
                 out=nsums[g][:],
@@ -318,36 +323,48 @@ def tile_shapeletencoder_pa_t_kernel(tc, x, W0, b0, W1, b1, out):
                 in_=w0gs[i][:].rearrange("q w t -> q (w t)"),
             )
 
-        for k in range(-LAG_A, NSLOT + LAG_I + 3):
+        for k in range(-LAG_A, NSLOT + LAG_I2 + 1):
+            gc = (k + 1) // 4
+            chain_now = (k + 1) % 4 == 0 and 0 <= gc < NG
+            chi_q, chi_g, chi_l1, chi_i, chi_i2 = (
+                (k - LAG_Q) // 2,
+                (k - LAG_G) // 2,
+                (k - LAG_L1) // 2,
+                (k - LAG_I) // 2,
+                (k - LAG_I2) // 2,
+            )
+            u0 = 2 * (k - LAG_U)
+            f0 = 2 * (k - LAG_F)
             if k % 4 == 0 and 3 <= k // 4 + 2 < NG:
                 load_x(k // 4 + 2)
+            if chain_now:
+                chain2a(gc)
             if 0 <= k < NSLOT:
                 subtract(k)
+            if 0 <= f0 < 8 * NG:
+                relu0(f0)
             if 0 <= k - 1 < NSLOT:
                 transposes(k - 1, 1)
-            if k in W_REGROUP_SLOTS:
-                regroup_w0(W_REGROUP_SLOTS.index(k))
             if k == 0:
                 bzt = ps_ch.tile([P, P], BF16, name="bzt", tag="ch")
                 nc.tensor.transpose(out=bzt[:], in_=bz[:], identity=identb[:])
-            if k == 3:
-                nc.scalar.copy(out=w1g[:], in_=w1raw[:].rearrange("p (c t) k -> p c k t", c=C, t=4))
-            gc = (k + 1) // 4
-            chain_now = (k + 1) % 4 == 0 and 0 <= gc < NG
             if chain_now:
-                chain2(gc)
+                chain2b(gc)
                 chain3(gc)
-            if (k - LAG_Q) % 2 == 0 and 0 <= (k - LAG_Q) // 2 < 2 * NG:
-                quantise_n((k - LAG_Q) // 2)
-            if (k - LAG_G) % 2 == 0 and 0 <= (k - LAG_G) // 2 < 2 * NG:
-                regroup_h((k - LAG_G) // 2)
+            if (k - LAG_Q) % 2 == 0 and 0 <= chi_q < 2 * NG:
+                quantise_n(chi_q)
+            if (k - LAG_L1) % 2 == 0 and 0 <= chi_l1 < 2 * NG:
+                layer1(chi_l1)
             if chain_now:
                 chain4(gc)
-            if 0 <= 2 * (k - LAG_U) < 8 * NG:
-                layer0(2 * (k - LAG_U))
+            if k in W_REGROUP_SLOTS:
+                regroup_w0(W_REGROUP_SLOTS.index(k))
+            if k == 3:
+                nc.scalar.copy(out=w1g[:], in_=w1raw[:].rearrange("p (c t) k -> p c k t", c=C, t=4))
+            if 0 <= u0 < 8 * NG:
+                layer0(u0)
             if 0 <= k - 1 < NSLOT:
                 evacuate(k - 1, 0)
-                evacuate(k - 1, 1)
             ga, j = (k + LAG_A) // 4, (k + LAG_A) % 4
             if ga < NG:
                 for idx in A_PARTS[j]:
@@ -356,6 +373,20 @@ def tile_shapeletencoder_pa_t_kernel(tc, x, W0, b0, W1, b1, out):
                     chain1(ga)
             if k == 0:
                 nc.vector.tensor_copy(out=b0col[:], in_=bzt[:, 0:8])
+            if 0 <= k < NSLOT:
+                transposes(k, 0)
+            if 0 <= u0 < 8 * NG:
+                layer0(u0 + 1)
+            if (k - LAG_G) % 2 == 0 and 0 <= chi_g < 2 * NG:
+                regroup_h(chi_g)
+            if 0 <= k - 1 < NSLOT:
+                evacuate(k - 1, 1)
+            if 0 <= f0 < 8 * NG:
+                relu0(f0 + 1)
+            if (k - LAG_I) % 2 == 0 and 0 <= chi_i < 2 * NG:
+                bias1(chi_i)
+            if (k - LAG_G) % 2 == 0 and 0 <= chi_g < 2 * NG:
+                quantise_h(chi_g)
             if k in W_QUANT_SLOTS:
                 quantise_w0(W_QUANT_SLOTS.index(k))
             if k == 4:
@@ -364,19 +395,5 @@ def tile_shapeletencoder_pa_t_kernel(tc, x, W0, b0, W1, b1, out):
                     scales=w1sc[:].rearrange("p c k -> p (c k)"),
                     in_=w1g[:].rearrange("p c k t -> p (c k t)"),
                 )
-            if 0 <= k < NSLOT:
-                transposes(k, 0)
-            if 0 <= 2 * (k - LAG_U) < 8 * NG:
-                layer0(2 * (k - LAG_U) + 1)
-            if (k - LAG_L1) % 2 == 0 and 0 <= (k - LAG_L1) // 2 < 2 * NG:
-                layer1((k - LAG_L1) // 2)
-            if 0 <= 2 * (k - LAG_F) < 8 * NG:
-                relu0(2 * (k - LAG_F))
-                relu0(2 * (k - LAG_F) + 1)
-            if (k - LAG_G) % 2 == 0 and 0 <= (k - LAG_G) // 2 < 2 * NG:
-                quantise_h((k - LAG_G) // 2)
-            if (k - LAG_I) % 2 == 0 and 0 <= (k - LAG_I) // 2 < 2 * NG:
-                chi = (k - LAG_I) // 2
-                bias1(chi)
-                if chi % 2 == 1:
-                    finish(chi // 2)
+            if (k - LAG_I2) % 2 == 0 and 0 <= chi_i2 < 2 * NG and chi_i2 % 2 == 1:
+                finish(chi_i2 // 2)

@@ -35,6 +35,7 @@ LAG_I2 = 9
 A_PARTS = ((0,), (1,), (2, 3, 4), (5, 6, 7, 8, 9, 10, 11))
 W_REGROUP_SLOTS = (-2, -1, 1, 2)
 W_QUANT_SLOTS = (-1, 0, 2, 3)
+FIRST_PIECES = ((0, 4), (4, 8), (8, 12), (12, 14), (14, 16))
 
 
 def b_on_vector(k):
@@ -87,8 +88,8 @@ def tile_shapeletencoder_pa_t_kernel(tc, x, W0, b0, W1, b1, out):
             nc.sync.dma_start(out=xs[g][:], in_=x_view(g))
 
         xs[0] = xpool.tile([P, NA, 2 * SEG], BF16, name="xg", tag="xg")
-        for i in range(4):
-            nc.sync.dma_start(out=xs[0][:, 4 * i : 4 * i + 4, :], in_=x_view(0)[:, 4 * i : 4 * i + 4, :])
+        for lo_a, hi_a in FIRST_PIECES:
+            nc.sync.dma_start(out=xs[0][:, lo_a:hi_a, :], in_=x_view(0)[:, lo_a:hi_a, :])
         w0raw = const.tile([P, C, 8, K0], BF16, name="w0raw", tag="w0raw")
         w0dram = W0.rearrange("c (u q) f -> q c u f", u=8, q=P)
         nc.sync.dma_start(out=w0raw[:, 0, :, :], in_=w0dram[:, 0, :, :])
@@ -106,6 +107,9 @@ def tile_shapeletencoder_pa_t_kernel(tc, x, W0, b0, W1, b1, out):
             in_=b1.rearrange("c k -> (c k)").partition_broadcast(P),
         )
 
+        warm = const.tile([P, 1], F32, name="warm", tag="warm")
+        nc.vector.memset(warm[:], 0.0)
+        nc.scalar.activation(out=warm[:], in_=warm[:], func=ACT.Identity)
         identf = const.tile([P, P], F32, name="identf", tag="identf")
         make_identity(nc, identf[:])
         identb = const.tile([P, P], BF16, name="identb", tag="identb")
@@ -129,12 +133,12 @@ def tile_shapeletencoder_pa_t_kernel(tc, x, W0, b0, W1, b1, out):
             t = his[g] if idx % 2 == 0 else los[g]
             op = ALU.max if idx % 2 == 0 else ALU.min
             if idx < 2 and g == 0:
-                for i in range(4 if idx == 0 else 0):
+                for lo_a, hi_a in FIRST_PIECES if idx == 0 else ():
                     for tt, oo in ((his[g], ALU.max), (los[g], ALU.min)):
                         nc.vector.tensor_tensor(
-                            out=tt[:, 4 * i : 4 * i + 4, :],
-                            in0=xg[:, 4 * i : 4 * i + 4, 0:SEG],
-                            in1=xg[:, 4 * i : 4 * i + 4, SEG : 2 * SEG],
+                            out=tt[:, lo_a:hi_a, :],
+                            in0=xg[:, lo_a:hi_a, 0:SEG],
+                            in1=xg[:, lo_a:hi_a, SEG : 2 * SEG],
                             op=oo,
                         )
             elif idx < 2:
@@ -298,13 +302,11 @@ def tile_shapeletencoder_pa_t_kernel(tc, x, W0, b0, W1, b1, out):
                 op=ALU.add,
             )
 
-        def finish(g):
-            flat = osbs[g][:].rearrange("p j c k -> p (j c k)")
-            nc.vector.tensor_scalar_max(out=flat, in0=flat, scalar1=0.0)
-            nc.sync.dma_start(
-                out=out[g].rearrange("(j p) c k -> p j (c k)", p=P),
-                in_=osbs[g][:].rearrange("p j c k -> p j (c k)"),
-            )
+        def finish(chi):
+            g, c = chi // 2, chi % 2
+            part = osbs[g][:, :, c, :]
+            nc.vector.tensor_scalar_max(out=part, in0=part, scalar1=0.0)
+            nc.sync.dma_start(out=out[g].rearrange("(j p) c k -> p j c k", p=P)[:, :, c, :], in_=part)
 
         def regroup_w0(i):
             c, gk = i // 2, i % 2
@@ -395,5 +397,5 @@ def tile_shapeletencoder_pa_t_kernel(tc, x, W0, b0, W1, b1, out):
                     scales=w1sc[:].rearrange("p c k -> p (c k)"),
                     in_=w1g[:].rearrange("p c k t -> p (c k t)"),
                 )
-            if (k - LAG_I2) % 2 == 0 and 0 <= chi_i2 < 2 * NG and chi_i2 % 2 == 1:
-                finish(chi_i2 // 2)
+            if (k - LAG_I2) % 2 == 0 and 0 <= chi_i2 < 2 * NG:
+                finish(chi_i2)

@@ -39,7 +39,7 @@ FIRST_PIECES = ((0, 4), (4, 8), (8, 12), (12, 14), (14, 16))
 
 
 def b_on_vector(k):
-    return 6 if k >= 28 else 1
+    return 6 if k >= 28 else 2
 
 
 def tile_shapeletencoder_pa_t_kernel(tc, x, W0, b0, W1, b1, out):

@@ -39,7 +39,11 @@ FIRST_PIECES = ((0, 4), (4, 8), (8, 12), (12, 14), (14, 16))
 
 
 def b_on_vector(k):
-    return 6 if k >= 28 else 2
+    return 7 if k >= 28 else 0
+
+
+def pe_rows(k):
+    return 4 if k < NSLOT - 4 else 0
 
 
 def tile_shapeletencoder_pa_t_kernel(tc, x, W0, b0, W1, b1, out):
@@ -54,8 +58,8 @@ def tile_shapeletencoder_pa_t_kernel(tc, x, W0, b0, W1, b1, out):
         hpool = ctx.enter_context(tc.tile_pool(name="hpool", bufs=2))
         opool = ctx.enter_context(tc.tile_pool(name="opool", bufs=2))
         wstage = ctx.enter_context(tc.tile_pool(name="wstage", bufs=2))
-        ps_tp = ctx.enter_context(tc.psum_pool(name="ps_tp", bufs=2))
-        ps_acc = ctx.enter_context(tc.psum_pool(name="ps_acc", bufs=4))
+        ps_tp = ctx.enter_context(tc.psum_pool(name="ps_tp", bufs=3))
+        ps_acc = ctx.enter_context(tc.psum_pool(name="ps_acc", bufs=3))
         ps_o = ctx.enter_context(tc.psum_pool(name="ps_o", bufs=1))
         ps_ch = ctx.enter_context(tc.psum_pool(name="ps_ch", bufs=1))
         ctx.enter_context(tc.manual_schedule())
@@ -192,7 +196,7 @@ def tile_shapeletencoder_pa_t_kernel(tc, x, W0, b0, W1, b1, out):
             if k % 4 == 0:
                 nts[g] = npool.tile([P, NA, C, SEG], BF16, name="nt", tag="nt")
             nv = b_on_vector(k)
-            for i in range(8):
+            for i in range(8 - pe_rows(k)):
                 a = 8 * h + i
                 src = xs[g][:, a, :].rearrange("p (s c) -> p s c", c=C)[:, :, c]
                 bias = negmids[g][:, 2 * a + c : 2 * a + c + 1]
@@ -205,22 +209,61 @@ def tile_shapeletencoder_pa_t_kernel(tc, x, W0, b0, W1, b1, out):
                         out=nts[g][:, a, c, :], in_=src, func=ACT.Identity, bias=bias, scale=1.0
                     )
 
-        def transposes(k, gk):
+        def fill(k, j):
             g, c, h = k // 4, (k // 2) % 2, k % 2
-            tp = ps_tp.tile([P, 8 * P], BF16, name="tp", tag="tp")
-            tps[(k, gk)] = tp
-            for i in range(8):
-                nc.tensor.transpose(
-                    out=tp[:, P * i : P * (i + 1)],
-                    in_=nts[g][:, 8 * h + i, c, P * gk : P * (gk + 1)],
-                    identity=identb[:],
-                )
+            if pe_rows(k) == 0:
+                tp = ps_tp.tile([P, 8 * P], BF16, name="tp", tag="tp")
+                for i in range(8):
+                    nc.tensor.transpose(
+                        out=tp[:, P * i : P * (i + 1)],
+                        in_=nts[g][:, 8 * h + i, c, P * j : P * (j + 1)],
+                        identity=identb[:],
+                    )
+            elif j < 2:
+                tp = ps_tp.tile([P, 4, P], F32, name="pb", tag="tp")
+                for i in range(4):
+                    a = 8 * h + 4 + i
+                    nc.tensor.matmul(
+                        out=tp[:, i, :],
+                        lhsT=xs[g][:, a, :].rearrange("p (s c) -> p s c", c=C)[:, P * j : P * (j + 1), c],
+                        rhs=identb[:],
+                        start=True,
+                        stop=False,
+                    )
+                    nc.tensor.matmul(
+                        out=tp[:, i, :],
+                        lhsT=negmids[g][:, 2 * a + c : 2 * a + c + 1].to_broadcast([P, P]),
+                        rhs=identf[:],
+                        start=False,
+                        stop=True,
+                        is_transpose=True,
+                    )
+            else:
+                tp = ps_tp.tile([P, 2, 4, P], BF16, name="tq", tag="tp")
+                for gk in range(2):
+                    for i in range(4):
+                        nc.tensor.transpose(
+                            out=tp[:, gk, i, :],
+                            in_=nts[g][:, 8 * h + i, c, P * gk : P * (gk + 1)],
+                            identity=identb[:],
+                        )
+            tps[(k, j)] = tp
 
-        def evacuate(k, gk):
+        def evacuate(k, j):
             chi, h = k // 2, k % 2
-            if h == 0 and gk == 0:
+            if h == 0 and j == 0:
                 gns[chi] = gpool.tile([P, 2, 4 * CELLS], BF16, name="gn", tag="gn", align_bytes=64)
-            nc.scalar.copy(out=gns[chi][:, gk, 1024 * h : 1024 * (h + 1)], in_=tps[(k, gk)][:])
+            tp = tps[(k, j)]
+            if pe_rows(k) == 0:
+                nc.scalar.copy(out=gns[chi][:, j, 1024 * h : 1024 * (h + 1)], in_=tp[:])
+            elif j < 2:
+                nc.scalar.copy(
+                    out=gns[chi][:, j, 1024 * h + 512 : 1024 * (h + 1)], in_=tp[:].rearrange("p i w -> p (i w)")
+                )
+            else:
+                nc.scalar.copy(
+                    out=gns[chi][:, :, 1024 * h : 1024 * h + 512], in_=tp[:].rearrange("p g i w -> p g (i w)")
+                )
 
         def quantise_n(chi):
             codes = gpool.tile([P, 2, CELLS], U32, name="ncodes", tag="ncodes", align_bytes=64)
@@ -341,50 +384,56 @@ def tile_shapeletencoder_pa_t_kernel(tc, x, W0, b0, W1, b1, out):
                 load_x(k // 4 + 2)
             if chain_now:
                 chain2a(gc)
-            if 0 <= k < NSLOT:
-                subtract(k)
-            if 0 <= f0 < 8 * NG:
-                relu0(f0)
-            if 0 <= k - 1 < NSLOT:
-                transposes(k - 1, 1)
-            if k == 0:
-                bzt = ps_ch.tile([P, P], BF16, name="bzt", tag="ch")
-                nc.tensor.transpose(out=bzt[:], in_=bz[:], identity=identb[:])
+            if (k - LAG_I2) % 2 == 0 and 0 <= chi_i2 < 2 * NG:
+                finish(chi_i2)
             if chain_now:
                 chain2b(gc)
                 chain3(gc)
+            if k == 1:
+                bzt = ps_ch.tile([P, P], BF16, name="bzt", tag="ch")
+                nc.tensor.transpose(out=bzt[:], in_=bz[:], identity=identb[:])
+            if 0 <= k - 1 < NSLOT:
+                evacuate(k - 1, 0)
+            if 0 <= k < NSLOT:
+                subtract(k)
             if (k - LAG_Q) % 2 == 0 and 0 <= chi_q < 2 * NG:
                 quantise_n(chi_q)
             if (k - LAG_L1) % 2 == 0 and 0 <= chi_l1 < 2 * NG:
                 layer1(chi_l1)
             if chain_now:
                 chain4(gc)
-            if k in W_REGROUP_SLOTS:
-                regroup_w0(W_REGROUP_SLOTS.index(k))
-            if k == 3:
-                nc.scalar.copy(out=w1g[:], in_=w1raw[:].rearrange("p (c t) k -> p c k t", c=C, t=4))
+            if 0 <= k < NSLOT:
+                fill(k, 0)
             if 0 <= u0 < 8 * NG:
                 layer0(u0)
-            if 0 <= k - 1 < NSLOT:
-                evacuate(k - 1, 0)
             ga, j = (k + LAG_A) // 4, (k + LAG_A) % 4
             if ga < NG:
                 for idx in A_PARTS[j]:
                     a_op(ga, idx)
-                if j == 3:
-                    chain1(ga)
-            if k == 0:
+            if 0 <= f0 < 8 * NG:
+                relu0(f0)
+            if ga < NG and j == 3:
+                chain1(ga)
+            if k == 1:
                 nc.vector.tensor_copy(out=b0col[:], in_=bzt[:, 0:8])
+            if 0 <= k - 1 < NSLOT:
+                evacuate(k - 1, 1)
             if 0 <= k < NSLOT:
-                transposes(k, 0)
+                fill(k, 1)
+            if 0 <= f0 < 8 * NG:
+                relu0(f0 + 1)
             if 0 <= u0 < 8 * NG:
                 layer0(u0 + 1)
             if (k - LAG_G) % 2 == 0 and 0 <= chi_g < 2 * NG:
                 regroup_h(chi_g)
-            if 0 <= k - 1 < NSLOT:
-                evacuate(k - 1, 1)
-            if 0 <= f0 < 8 * NG:
-                relu0(f0 + 1)
+            if 0 <= k - 1 < NSLOT and pe_rows(k - 1) > 0:
+                evacuate(k - 1, 2)
+            if k in W_REGROUP_SLOTS:
+                regroup_w0(W_REGROUP_SLOTS.index(k))
+            if k == 3:
+                nc.scalar.copy(out=w1g[:], in_=w1raw[:].rearrange("p (c t) k -> p c k t", c=C, t=4))
+            if 0 <= k < NSLOT and pe_rows(k) > 0:
+                fill(k, 2)
             if (k - LAG_I) % 2 == 0 and 0 <= chi_i < 2 * NG:
                 bias1(chi_i)
             if (k - LAG_G) % 2 == 0 and 0 <= chi_g < 2 * NG:
@@ -397,5 +446,3 @@ def tile_shapeletencoder_pa_t_kernel(tc, x, W0, b0, W1, b1, out):
                     scales=w1sc[:].rearrange("p c k -> p (c k)"),
                     in_=w1g[:].rearrange("p c k t -> p (c k t)"),
                 )
-            if (k - LAG_I2) % 2 == 0 and 0 <= chi_i2 < 2 * NG:
-                finish(chi_i2)

@@ -24,7 +24,8 @@ SEG = 256
 FLOPS = 2 * C * NG * CELLS * L * K0 + 2 * C * NG * CELLS * K0 * K1
 
 NSLOT = 4 * NG
-LAG_A = 5
+LAST = 2 * NG - 1
+LAG_A = 6
 LAG_Q = 3
 LAG_U = 3
 LAG_F = 4
@@ -32,10 +33,9 @@ LAG_G = 6
 LAG_L1 = 7
 LAG_I = 8
 LAG_I2 = 9
-A_PARTS = ((0,), (1,), (2, 3, 4), (5, 6, 7, 8, 9, 10, 11))
-W_REGROUP_SLOTS = (-2, -1, 1, 2)
-W_QUANT_SLOTS = (-1, 0, 2, 3)
-FIRST_PIECES = ((0, 4), (4, 8), (8, 12), (12, 14), (14, 16))
+LEVELS = 14
+A_PARTS = ((0,), (1, 2), (3,), tuple(range(4, LEVELS)))
+PIECES0 = (((0, 2), (2, 4), (4, 8)), ((8, 12), (12, 16)))
 
 
 def b_on_vector(k):
@@ -44,6 +44,10 @@ def b_on_vector(k):
 
 def pe_rows(k):
     return 4 if k < NSLOT - 4 else 0
+
+
+def relu1_on_scalar(chi):
+    return chi % 2 == 0 or chi < 4
 
 
 def tile_shapeletencoder_pa_t_kernel(tc, x, W0, b0, W1, b1, out):
@@ -87,21 +91,30 @@ def tile_shapeletencoder_pa_t_kernel(tc, x, W0, b0, W1, b1, out):
         def x_view(g):
             return x[g].rearrange("(a p s) c -> p a (s c)", a=NA, p=P, s=SEG)
 
-        def load_x(g):
-            xs[g] = xpool.tile([P, NA, 2 * SEG], BF16, name="xg", tag="xg")
-            nc.sync.dma_start(out=xs[g][:], in_=x_view(g))
+        def load_x(g, pieces=((0, NA),)):
+            if g not in xs:
+                xs[g] = xpool.tile([P, NA, 2 * SEG], BF16, name="xg", tag="xg")
+            for lo, hi in pieces:
+                nc.sync.dma_start(out=xs[g][:, lo:hi, :], in_=x_view(g)[:, lo:hi, :])
 
-        xs[0] = xpool.tile([P, NA, 2 * SEG], BF16, name="xg", tag="xg")
-        for lo_a, hi_a in FIRST_PIECES:
-            nc.sync.dma_start(out=xs[0][:, lo_a:hi_a, :], in_=x_view(0)[:, lo_a:hi_a, :])
         w0raw = const.tile([P, C, 8, K0], BF16, name="w0raw", tag="w0raw")
-        w0dram = W0.rearrange("c (u q) f -> q c u f", u=8, q=P)
-        nc.sync.dma_start(out=w0raw[:, 0, :, :], in_=w0dram[:, 0, :, :])
+        w0dram = W0.rearrange("c (t g q) f -> q c t g f", t=4, g=2, q=P)
+        w0rv = w0raw[:].rearrange("q c (t g) f -> q c t g f", t=4, g=2)
+
+        def load_w0(i):
+            c, gk = i // 2, i % 2
+            nc.sync.dma_start(out=w0rv[:, c, :, gk, :], in_=w0dram[:, c, :, gk, :])
+
+        load_x(0, PIECES0[0])
+        load_w0(0)
+        load_w0(1)
+        load_x(0, PIECES0[1])
+        load_w0(2)
+        load_w0(3)
         load_x(1)
         bz = const.tile([P, P], BF16, name="bz", tag="bz")
         nc.vector.memset(bz[:], 0.0)
         nc.sync.dma_start(out=bz[0:8, :], in_=b0.rearrange("c (t p) -> (c t) p", t=4, p=P))
-        nc.sync.dma_start(out=w0raw[:, 1, :, :], in_=w0dram[:, 1, :, :])
         w1raw = const.tile([P, 8, K1], BF16, name="w1raw", tag="w1raw")
         nc.sync.dma_start(out=w1raw[:], in_=W1.rearrange("c (t p) k -> p (c t) k", t=4, p=P))
         load_x(2)
@@ -129,35 +142,31 @@ def tile_shapeletencoder_pa_t_kernel(tc, x, W0, b0, W1, b1, out):
         w1sc = const.tile([P, C, K1], U8, name="w1sc", tag="w1sc", align_bytes=64)
         w1g = const.tile([P, C, K1, 4], BF16, name="w1g", tag="w1g", align_bytes=64)
 
-        def a_op(g, idx):
+        def a_op(g, idx, lo=0, hi=NA):
             xg = xs[g]
-            if idx == 0:
+            if g not in his:
                 his[g] = scr.tile([P, NA, SEG], BF16, name="hi", tag="hi")
                 los[g] = scr.tile([P, NA, SEG], BF16, name="lo", tag="lo")
             t = his[g] if idx % 2 == 0 else los[g]
             op = ALU.max if idx % 2 == 0 else ALU.min
-            if idx < 2 and g == 0:
-                for lo_a, hi_a in FIRST_PIECES if idx == 0 else ():
-                    for tt, oo in ((his[g], ALU.max), (los[g], ALU.min)):
-                        nc.vector.tensor_tensor(
-                            out=tt[:, lo_a:hi_a, :],
-                            in0=xg[:, lo_a:hi_a, 0:SEG],
-                            in1=xg[:, lo_a:hi_a, SEG : 2 * SEG],
-                            op=oo,
-                        )
-            elif idx < 2:
-                nc.vector.tensor_tensor(out=t[:], in0=xg[:, :, 0:SEG], in1=xg[:, :, SEG : 2 * SEG], op=op)
-            elif idx < 10:
+            if idx < 2:
+                nc.vector.tensor_tensor(
+                    out=t[:, lo:hi, :], in0=xg[:, lo:hi, 0:SEG], in1=xg[:, lo:hi, SEG : 2 * SEG], op=op
+                )
+            elif idx < LEVELS - 2:
                 h = SEG >> (idx // 2)
-                nc.vector.tensor_tensor(out=t[:, :, 0:h], in0=t[:, :, 0:h], in1=t[:, :, h : 2 * h], op=op)
+                nc.vector.tensor_tensor(
+                    out=t[:, lo:hi, 0:h], in0=t[:, lo:hi, 0:h], in1=t[:, lo:hi, h : 2 * h], op=op
+                )
             else:
-                st = stx if idx == 10 else stn
+                h = SEG >> (LEVELS // 2 - 2)
+                st = stx if idx % 2 == 0 else stn
                 nc.vector.tensor_reduce(
-                    out=st[:, 0:32].rearrange("p (a c) -> p a c", c=C),
-                    in_=t[:, :, 0:16].rearrange("p a (s c) -> p a c s", c=C),
+                    out=st[:, 2 * lo : 2 * hi].rearrange("p (a c) -> p a c", c=C),
+                    in_=t[:, lo:hi, 0:h].rearrange("p a (s c) -> p a c s", c=C),
                     axis=AX.X,
                     op=op,
-                    negate=(idx == 11),
+                    negate=(idx % 2 == 1),
                 )
 
         def chain1(g):
@@ -185,11 +194,11 @@ def tile_shapeletencoder_pa_t_kernel(tc, x, W0, b0, W1, b1, out):
             p2s[g] = ps_ch.tile([P, P], F32, name="p2", tag="ch")
             nc.tensor.transpose(out=p2s[g][:], in_=nsums[g][:].rearrange("q e t -> q (e t)"), identity=identf[:])
 
-        def chain4(g):
-            negmids[g] = small.tile([P, 32], F32, name="negmid", tag="negmid")
-            nc.vector.tensor_scalar(
-                out=negmids[g][:], in0=p2s[g][:, 0:32], scalar1=0.5, scalar2=None, op0=ALU.mult
-            )
+        def chain4(g, halves=(0, 1)):
+            nm = small.tile([P, 32], F32, name="negmid", tag="negmid")
+            nc.vector.tensor_scalar(out=nm[:], in0=p2s[g][:, 0:32], scalar1=0.5, scalar2=None, op0=ALU.mult)
+            for h in halves:
+                negmids[(g, h)] = nm
 
         def subtract(k):
             g, c, h = k // 4, (k // 2) % 2, k % 2
@@ -199,7 +208,7 @@ def tile_shapeletencoder_pa_t_kernel(tc, x, W0, b0, W1, b1, out):
             for i in range(8 - pe_rows(k)):
                 a = 8 * h + i
                 src = xs[g][:, a, :].rearrange("p (s c) -> p s c", c=C)[:, :, c]
-                bias = negmids[g][:, 2 * a + c : 2 * a + c + 1]
+                bias = negmids[(g, h)][:, 2 * a + c : 2 * a + c + 1]
                 if i < nv:
                     nc.vector.tensor_scalar(
                         out=nts[g][:, a, c, :], in0=src, scalar1=bias, scalar2=None, op0=ALU.add
@@ -232,7 +241,7 @@ def tile_shapeletencoder_pa_t_kernel(tc, x, W0, b0, W1, b1, out):
                     )
                     nc.tensor.matmul(
                         out=tp[:, i, :],
-                        lhsT=negmids[g][:, 2 * a + c : 2 * a + c + 1].to_broadcast([P, P]),
+                        lhsT=negmids[(g, h)][:, 2 * a + c : 2 * a + c + 1].to_broadcast([P, P]),
                         rhs=identf[:],
                         start=False,
                         stop=True,
@@ -249,115 +258,154 @@ def tile_shapeletencoder_pa_t_kernel(tc, x, W0, b0, W1, b1, out):
                         )
             tps[(k, j)] = tp
 
+        def parts(chi):
+            return 2 if chi == LAST else 1
+
+        def g_view(chi):
+            if parts(chi) == 2:
+                return gns[chi][:].rearrange("p (h g w) -> p g h w", h=2, g=2)
+            return gns[chi][:].rearrange("p (g h w) -> p g h w", h=2, g=2)
+
         def evacuate(k, j):
             chi, h = k // 2, k % 2
             if h == 0 and j == 0:
-                gns[chi] = gpool.tile([P, 2, 4 * CELLS], BF16, name="gn", tag="gn", align_bytes=64)
+                gns[chi] = gpool.tile([P, 8 * CELLS], BF16, name="gn", tag="gn", align_bytes=64)
             tp = tps[(k, j)]
+            gv = g_view(chi)
             if pe_rows(k) == 0:
-                nc.scalar.copy(out=gns[chi][:, j, 1024 * h : 1024 * (h + 1)], in_=tp[:])
+                nc.scalar.copy(out=gv[:, j, h, :], in_=tp[:])
             elif j < 2:
-                nc.scalar.copy(
-                    out=gns[chi][:, j, 1024 * h + 512 : 1024 * (h + 1)], in_=tp[:].rearrange("p i w -> p (i w)")
-                )
+                nc.scalar.copy(out=gv[:, j, h, 512:1024], in_=tp[:].rearrange("p i w -> p (i w)"))
             else:
-                nc.scalar.copy(
-                    out=gns[chi][:, :, 1024 * h : 1024 * h + 512], in_=tp[:].rearrange("p g i w -> p g (i w)")
-                )
+                nc.scalar.copy(out=gv[:, :, h, 0:512], in_=tp[:].rearrange("p g i w -> p g (i w)"))
 
-        def quantise_n(chi):
-            codes = gpool.tile([P, 2, CELLS], U32, name="ncodes", tag="ncodes", align_bytes=64)
-            sc = gpool.tile([P, 2, CELLS], U8, name="nsc", tag="nsc", align_bytes=64)
-            ncs[chi] = (codes, sc)
+        def quantise_n(chi, part=0):
+            n = 2 * CELLS // parts(chi)
+            if part == 0:
+                codes = gpool.tile([P, 2 * CELLS], U32, name="ncodes", tag="ncodes", align_bytes=64)
+                sc = gpool.tile([P, 2 * CELLS], U8, name="nsc", tag="nsc", align_bytes=64)
+                ncs[chi] = (codes, sc)
+            codes, sc = ncs[chi]
             nc.vector.quantize_mx(
-                out=codes[:].rearrange("p g w -> p (g w)").bitcast(FP8X4),
-                scales=sc[:].rearrange("p g w -> p (g w)"),
-                in_=gns[chi][:].rearrange("p g w -> p (g w)"),
+                out=codes[:, n * part : n * (part + 1)].bitcast(FP8X4),
+                scales=sc[:, n * part : n * (part + 1)],
+                in_=gns[chi][:, 4 * n * part : 4 * n * (part + 1)],
             )
 
-        def layer0(u):
+        def layer0(u, part=0, pool=None):
             chi, m = u // 4, u % 4
             c = chi % 2
+            n = CELLS // parts(chi)
             codes, sc = ncs[chi]
-            accs[u] = ps_acc.tile([P, CELLS], F32, name="acc", tag="acc")
+            if pool is None:
+                acc = ps_acc.tile([P, CELLS], F32, name="acc", tag="acc")
+            else:
+                acc = pool.tile([P, CELLS], F32, name="acc", tag="tp")
+            accs[(u, part)] = acc
             for gk in range(2):
+                o = n * (2 * part + gk)
                 nc.tensor.matmul_mx(
-                    out=accs[u][:],
+                    out=acc[:, 0:n],
                     lhsT=w0codes[:, c, gk, P * m : P * (m + 1)].bitcast(FP8X4),
                     lhsT_scale=w0sc[:, c, gk, P * m : P * (m + 1)],
-                    rhs=codes[:, gk, :].bitcast(FP8X4),
-                    rhs_scale=sc[:, gk, :],
+                    rhs=codes[:, o : o + n].bitcast(FP8X4),
+                    rhs_scale=sc[:, o : o + n],
                     start=(gk == 0),
                     stop=(gk == 1),
                 )
 
-        def relu0(u):
+        def relu0(u, part=0, on_vector=False):
             chi, m = u // 4, u % 4
             c = chi % 2
-            if m == 0:
+            n = CELLS // parts(chi)
+            if m == 0 and part == 0:
                 hps[chi] = hpool.tile([P, 4, CELLS], BF16, name="hp", tag="hp")
-            nc.scalar.activation(
-                out=hps[chi][:, m, :],
-                in_=accs[u][:],
-                func=ACT.Relu,
-                bias=b0col[:, 4 * c + m : 4 * c + m + 1],
-                scale=1.0,
-            )
+            bias = b0col[:, 4 * c + m : 4 * c + m + 1]
+            o = hps[chi][:, m, n * part : n * (part + 1)]
+            if on_vector:
+                nc.vector.tensor_scalar(
+                    out=o, in0=accs[(u, part)][:, 0:n], scalar1=bias, scalar2=0.0, op0=ALU.add, op1=ALU.max
+                )
+            else:
+                nc.scalar.activation(out=o, in_=accs[(u, part)][:, 0:n], func=ACT.Relu, bias=bias, scale=1.0)
 
-        def regroup_h(chi):
-            hgs[chi] = hpool.tile([P, CELLS, 4], BF16, name="hg", tag="hg", align_bytes=64)
+        def regroup_h(chi, part=0):
+            n = CELLS // parts(chi)
+            if part == 0:
+                hgs[chi] = hpool.tile([P, CELLS, 4], BF16, name="hg", tag="hg", align_bytes=64)
             nc.vector.tensor_copy(
-                out=hgs[chi][:].rearrange("p (w i) t -> p w t i", i=4),
-                in_=hps[chi][:].rearrange("p t (w i) -> p w t i", i=4),
+                out=hgs[chi][:, n * part : n * (part + 1), :].rearrange("p (w i) t -> p w t i", i=4),
+                in_=hps[chi][:, :, n * part : n * (part + 1)].rearrange("p t (w i) -> p w t i", i=4),
             )
 
-        def quantise_h(chi):
-            codes = hpool.tile([P, CELLS], U32, name="hcodes", tag="hcodes", align_bytes=64)
-            sc = hpool.tile([P, CELLS], U8, name="hsc", tag="hsc", align_bytes=64)
-            hcs[chi] = (codes, sc)
+        def quantise_h(chi, part=0):
+            n = CELLS // parts(chi)
+            if part == 0:
+                codes = hpool.tile([P, CELLS], U32, name="hcodes", tag="hcodes", align_bytes=64)
+                sc = hpool.tile([P, CELLS], U8, name="hsc", tag="hsc", align_bytes=64)
+                hcs[chi] = (codes, sc)
+            codes, sc = hcs[chi]
             nc.vector.quantize_mx(
-                out=codes[:].bitcast(FP8X4), scales=sc[:], in_=hgs[chi][:].rearrange("p w t -> p (w t)")
+                out=codes[:, n * part : n * (part + 1)].bitcast(FP8X4),
+                scales=sc[:, n * part : n * (part + 1)],
+                in_=hgs[chi][:, n * part : n * (part + 1), :].rearrange("p w t -> p (w t)"),
             )
 
-        def layer1(chi):
+        def layer1(chi, part=0, pool=None):
             c = chi % 2
             codes, sc = hcs[chi]
-            ops_[chi] = ps_o.tile([P, 4, K1], F32, name="o_ps", tag="o")
-            for jj in range(4):
+            nb = 4 // parts(chi)
+            if pool is None:
+                ops_[(chi, part)] = ps_o.tile([P, 4, K1], F32, name="o_ps", tag="o")
+            else:
+                ops_[(chi, part)] = pool.tile([P, 4, K1], F32, name="o_ps", tag="tp")
+            for jj in range(nb):
+                b = nb * part + jj
                 nc.tensor.matmul_mx(
-                    out=ops_[chi][:, jj, :],
-                    lhsT=codes[:, P * jj : P * (jj + 1)].bitcast(FP8X4),
-                    lhsT_scale=sc[:, P * jj : P * (jj + 1)],
+                    out=ops_[(chi, part)][:, jj, :],
+                    lhsT=codes[:, P * b : P * (b + 1)].bitcast(FP8X4),
+                    lhsT_scale=sc[:, P * b : P * (b + 1)],
                     rhs=w1codes[:, c, :].bitcast(FP8X4),
                     rhs_scale=w1sc[:, c, :],
                     start=True,
                     stop=True,
                 )
 
-        def bias1(chi):
+        def bias1(chi, part=0):
             g, c = chi // 2, chi % 2
+            nb = 4 // parts(chi)
             if c == 0:
                 osbs[g] = opool.tile([P, 4, C, K1], F32, name="osb", tag="osb")
             nc.vector.tensor_tensor(
-                out=osbs[g][:, :, c, :],
-                in0=ops_[chi][:],
-                in1=b1b[:, c, :].unsqueeze(1).to_broadcast([P, 4, K1]),
+                out=osbs[g][:, nb * part : nb * (part + 1), c, :],
+                in0=ops_[(chi, part)][:, 0:nb, :],
+                in1=b1b[:, c, :].unsqueeze(1).to_broadcast([P, nb, K1]),
                 op=ALU.add,
             )
 
-        def finish(chi):
+        def relu1(chi, part=0):
             g, c = chi // 2, chi % 2
-            part = osbs[g][:, :, c, :]
-            nc.vector.tensor_scalar_max(out=part, in0=part, scalar1=0.0)
-            nc.sync.dma_start(out=out[g].rearrange("(j p) c k -> p j c k", p=P)[:, :, c, :], in_=part)
+            nb = 4 // parts(chi)
+            o = osbs[g][:, nb * part : nb * (part + 1), c, :]
+            if relu1_on_scalar(chi):
+                nc.scalar.activation(out=o, in_=o, func=ACT.Relu)
+            else:
+                nc.vector.tensor_scalar_max(out=o, in0=o, scalar1=0.0)
+
+        def store(chi, part=0):
+            g, c = chi // 2, chi % 2
+            nb = 4 // parts(chi)
+            nc.sync.dma_start(
+                out=out[g].rearrange("(j p) c k -> p j c k", p=P)[:, nb * part : nb * (part + 1), c, :],
+                in_=osbs[g][:, nb * part : nb * (part + 1), c, :],
+            )
 
         def regroup_w0(i):
             c, gk = i // 2, i % 2
             w0gs[i] = wstage.tile([P, K0, 4], BF16, name="w0g", tag="w0g", align_bytes=64)
-            src = w0raw[:, c, :, :].rearrange("q (t g) f -> q t g f", t=4, g=2)[:, :, gk, :]
             nc.scalar.copy(
                 out=w0gs[i][:].rearrange("q (w i) t -> q w t i", i=4),
-                in_=src.rearrange("q t (w i) -> q w t i", i=4),
+                in_=w0rv[:, c, :, gk, :].rearrange("q t (w i) -> q w t i", i=4),
             )
 
         def quantise_w0(i):
@@ -368,9 +416,60 @@ def tile_shapeletencoder_pa_t_kernel(tc, x, W0, b0, W1, b1, out):
                 in_=w0gs[i][:].rearrange("q w t -> q (w t)"),
             )
 
-        for k in range(-LAG_A, NSLOT + LAG_I2 + 1):
-            gc = (k + 1) // 4
-            chain_now = (k + 1) % 4 == 0 and 0 <= gc < NG
+        def pairs(lo, hi):
+            a_op(0, 0, lo, hi)
+            a_op(0, 1, lo, hi)
+
+        def levels(lo, hi):
+            for idx in range(2, LEVELS):
+                a_op(0, idx, lo, hi)
+
+        regroup_w0(0)
+        for piece in PIECES0[0]:
+            pairs(*piece)
+        levels(0, 8)
+        chain1(0)
+        regroup_w0(1)
+        a_op(0, 0, 8, 12)
+        chain2a(0)
+        chain2b(0)
+        chain3(0)
+        a_op(0, 1, 8, 12)
+        chain4(0, (0,))
+        subtract(0)
+        for j in range(3):
+            fill(0, j)
+        quantise_w0(0)
+        regroup_w0(2)
+        pairs(12, 16)
+        levels(8, 16)
+        chain1(0)
+        for j in range(3):
+            evacuate(0, j)
+        quantise_w0(1)
+        chain2a(0)
+        chain2b(0)
+        chain3(0)
+        quantise_w0(2)
+        chain4(0, (1,))
+        regroup_w0(3)
+        a_op(1, 0)
+        a_op(1, 1)
+
+        for k in range(1, NSLOT):
+            gc = (k + 2) // 4
+            chain_now = k == 3 or ((k + 2) % 4 == 0 and 2 <= gc < NG)
+            if k == 3:
+                gc = 1
+            ga, j = (k + LAG_A) // 4, (k + LAG_A) % 4
+            tree_ops = [(ga, idx) for idx in A_PARTS[j]] if ga < NG else []
+            if k == 1:
+                tree_ops = [(1, 2), (1, 3), (1, 4)]
+            if k == 2:
+                tree_ops = [(1, idx) for idx in range(5, LEVELS)]
+            if k == 3:
+                tree_ops = [(2, 0), (2, 1), (2, 2)]
+            third = (len(tree_ops) + 2) // 3
             chi_q, chi_g, chi_l1, chi_i, chi_i2 = (
                 (k - LAG_Q) // 2,
                 (k - LAG_G) // 2,
@@ -378,71 +477,126 @@ def tile_shapeletencoder_pa_t_kernel(tc, x, W0, b0, W1, b1, out):
                 (k - LAG_I) // 2,
                 (k - LAG_I2) // 2,
             )
+            now_q = (k - LAG_Q) % 2 == 0 and chi_q >= 0
+            now_g = (k - LAG_G) % 2 == 0 and chi_g >= 0
+            now_l1 = (k - LAG_L1) % 2 == 0 and chi_l1 >= 0
+            now_i = (k - LAG_I) % 2 == 0 and chi_i >= 0
+            now_i2 = (k - LAG_I2) % 2 == 0 and chi_i2 >= 0
             u0 = 2 * (k - LAG_U)
             f0 = 2 * (k - LAG_F)
+
             if k % 4 == 0 and 3 <= k // 4 + 2 < NG:
                 load_x(k // 4 + 2)
-            if chain_now:
+            if k == 3:
+                chain2a(1)
+                chain2b(1)
+                chain3(1)
+                chain4(1)
+            if k > 1:
+                evacuate(k - 1, 0)
+            if now_i:
+                bias1(chi_i)
+            if chain_now and k > 3:
                 chain2a(gc)
-            if (k - LAG_I2) % 2 == 0 and 0 <= chi_i2 < 2 * NG:
-                finish(chi_i2)
-            if chain_now:
+            subtract(k)
+            if now_g:
+                regroup_h(chi_g)
+            if now_q:
+                quantise_n(chi_q)
+            if chain_now and k > 3:
                 chain2b(gc)
+            if now_l1:
+                layer1(chi_l1)
+            for g, idx in tree_ops[:third]:
+                a_op(g, idx)
+            if now_g:
+                quantise_h(chi_g)
+            fill(k, 0)
+            for g, idx in tree_ops[third : 2 * third]:
+                a_op(g, idx)
+            if k > 1:
+                evacuate(k - 1, 1)
+            fill(k, 1)
+            if f0 >= 0:
+                relu0(f0)
+            for g, idx in tree_ops[2 * third :]:
+                a_op(g, idx)
+            if chain_now and k > 3:
                 chain3(gc)
+            if u0 >= 0:
+                layer0(u0)
+                layer0(u0 + 1)
+            if now_i2:
+                relu1(chi_i2)
+                store(chi_i2)
+            if (ga < NG and j == 3 and k > 2) or k == 2:
+                chain1(1 if k == 2 else ga)
+            if f0 >= 0:
+                relu0(f0 + 1)
             if k == 1:
                 bzt = ps_ch.tile([P, P], BF16, name="bzt", tag="ch")
                 nc.tensor.transpose(out=bzt[:], in_=bz[:], identity=identb[:])
-            if 0 <= k - 1 < NSLOT:
-                evacuate(k - 1, 0)
-            if 0 <= k < NSLOT:
-                subtract(k)
-            if (k - LAG_Q) % 2 == 0 and 0 <= chi_q < 2 * NG:
-                quantise_n(chi_q)
-            if (k - LAG_L1) % 2 == 0 and 0 <= chi_l1 < 2 * NG:
-                layer1(chi_l1)
-            if chain_now:
-                chain4(gc)
-            if 0 <= k < NSLOT:
-                fill(k, 0)
-            if 0 <= u0 < 8 * NG:
-                layer0(u0)
-            ga, j = (k + LAG_A) // 4, (k + LAG_A) % 4
-            if ga < NG:
-                for idx in A_PARTS[j]:
-                    a_op(ga, idx)
-            if 0 <= f0 < 8 * NG:
-                relu0(f0)
-            if ga < NG and j == 3:
-                chain1(ga)
-            if k == 1:
+                quantise_w0(3)
                 nc.vector.tensor_copy(out=b0col[:], in_=bzt[:, 0:8])
-            if 0 <= k - 1 < NSLOT:
-                evacuate(k - 1, 1)
-            if 0 <= k < NSLOT:
-                fill(k, 1)
-            if 0 <= f0 < 8 * NG:
-                relu0(f0 + 1)
-            if 0 <= u0 < 8 * NG:
-                layer0(u0 + 1)
-            if (k - LAG_G) % 2 == 0 and 0 <= chi_g < 2 * NG:
-                regroup_h(chi_g)
-            if 0 <= k - 1 < NSLOT and pe_rows(k - 1) > 0:
-                evacuate(k - 1, 2)
-            if k in W_REGROUP_SLOTS:
-                regroup_w0(W_REGROUP_SLOTS.index(k))
-            if k == 3:
+            if k == 2:
                 nc.scalar.copy(out=w1g[:], in_=w1raw[:].rearrange("p (c t) k -> p c k t", c=C, t=4))
-            if 0 <= k < NSLOT and pe_rows(k) > 0:
-                fill(k, 2)
-            if (k - LAG_I) % 2 == 0 and 0 <= chi_i < 2 * NG:
-                bias1(chi_i)
-            if (k - LAG_G) % 2 == 0 and 0 <= chi_g < 2 * NG:
-                quantise_h(chi_g)
-            if k in W_QUANT_SLOTS:
-                quantise_w0(W_QUANT_SLOTS.index(k))
-            if k == 4:
+            if k == 3:
                 nc.vector.quantize_mx(
                     out=w1codes[:].rearrange("p c k -> p (c k)").bitcast(FP8X4),
                     scales=w1sc[:].rearrange("p c k -> p (c k)"),
                     in_=w1g[:].rearrange("p c k t -> p (c k t)"),
                 )
+            if k > 1 and pe_rows(k - 1) > 0:
+                evacuate(k - 1, 2)
+            if chain_now and k > 3:
+                chain4(gc)
+            if pe_rows(k) > 0:
+                fill(k, 2)
+
+        ul = 4 * LAST
+
+        evacuate(NSLOT - 1, 0)
+        quantise_n(LAST, 0)
+        layer0(ul - 2)
+        relu0(ul - 4)
+        evacuate(NSLOT - 1, 1)
+        relu0(ul - 3)
+        layer0(ul - 1)
+        for m in range(4):
+            layer0(ul + m, 0, ps_tp if m % 2 else None)
+        regroup_h(LAST - 2)
+        bias1(LAST - 3)
+        quantise_h(LAST - 2)
+        quantise_n(LAST, 1)
+        relu0(ul - 2)
+        relu0(ul - 1)
+        relu1(LAST - 3)
+        store(LAST - 3)
+        layer1(LAST - 2)
+        for m in range(4):
+            relu0(ul + m, 0, m == 3)
+        for m in range(4):
+            layer0(ul + m, 1, ps_tp if m % 2 else None)
+        regroup_h(LAST - 1)
+        bias1(LAST - 2)
+        quantise_h(LAST - 1)
+        regroup_h(LAST, 0)
+        relu1(LAST - 2)
+        store(LAST - 2)
+        for m in range(4):
+            relu0(ul + m, 1, m == 3)
+        quantise_h(LAST, 0)
+        layer1(LAST - 1)
+        layer1(LAST, 0, ps_tp)
+        regroup_h(LAST, 1)
+        bias1(LAST - 1)
+        quantise_h(LAST, 1)
+        relu1(LAST - 1)
+        store(LAST - 1)
+        bias1(LAST, 0)
+        layer1(LAST, 1, ps_tp)
+        relu1(LAST, 0)
+        store(LAST, 0)
+        bias1(LAST, 1)
+        relu1(LAST, 1)
+        store(LAST, 1)

@@ -19,8 +19,7 @@ L = 1024
 C = 2
 K0 = 512
 K1 = 128
-NA = 16
-SEG = 256
+NA = 4
 FLOPS = 2 * C * NG * CELLS * L * K0 + 2 * C * NG * CELLS * K0 * K1
 
 NSLOT = 4 * NG
@@ -35,15 +34,15 @@ LAG_I = 8
 LAG_I2 = 9
 LEVELS = 14
 A_PARTS = ((0,), (1, 2), (3,), tuple(range(4, LEVELS)))
-PIECES0 = (((0, 2), (2, 4), (4, 8)), ((8, 12), (12, 16)))
+PIECES0 = (((0, 1), (1, 2)), ((2, 3), (3, 4)))
 
 
 def b_on_vector(k):
-    return 7 if k >= 28 else 0
+    return 3 if k >= 28 else 0
 
 
-def pe_rows(k):
-    return 4 if k < NSLOT - 4 else 0
+def on_tensor(k):
+    return k < NSLOT - 4
 
 
 def relu1_on_scalar(chi):
@@ -71,10 +70,8 @@ def tile_shapeletencoder_pa_t_kernel(tc, x, W0, b0, W1, b1, out):
         xs = {}
         his = {}
         los = {}
-        p1s = {}
-        reds = {}
+        sts = {}
         nsums = {}
-        p2s = {}
         negmids = {}
         nts = {}
         tps = {}
@@ -89,21 +86,23 @@ def tile_shapeletencoder_pa_t_kernel(tc, x, W0, b0, W1, b1, out):
         w0gs = {}
 
         def x_view(g):
-            return x[g].rearrange("(a p s) c -> p a (s c)", a=NA, p=P, s=SEG)
+            return x[g].rearrange("(a p s) c -> p a (s c)", a=NA, p=P, s=L)
 
         def load_x(g, pieces=((0, NA),)):
             if g not in xs:
-                xs[g] = xpool.tile([P, NA, 2 * SEG], BF16, name="xg", tag="xg")
+                xs[g] = xpool.tile([P, NA, C * L], BF16, name="xg", tag="xg")
             for lo, hi in pieces:
                 nc.sync.dma_start(out=xs[g][:, lo:hi, :], in_=x_view(g)[:, lo:hi, :])
 
         w0raw = const.tile([P, C, 8, K0], BF16, name="w0raw", tag="w0raw")
-        w0dram = W0.rearrange("c (t g q) f -> q c t g f", t=4, g=2, q=P)
-        w0rv = w0raw[:].rearrange("q c (t g) f -> q c t g f", t=4, g=2)
+        w0dram = W0.rearrange("c (g j w e) f -> w c g j (e f)", g=2, j=2, w=P, e=2)
+        w0rv = w0raw[:].rearrange("w c (g t) f -> w c g t f", g=2, t=4)
 
         def load_w0(i):
             c, gk = i // 2, i % 2
-            nc.sync.dma_start(out=w0rv[:, c, :, gk, :], in_=w0dram[:, c, :, gk, :])
+            nc.sync.dma_start(
+                out=w0rv[:, c, gk, :, :].rearrange("w (j e) f -> w j (e f)", e=2), in_=w0dram[:, c, gk, :, :]
+            )
 
         load_x(0, PIECES0[0])
         load_w0(0)
@@ -131,10 +130,6 @@ def tile_shapeletencoder_pa_t_kernel(tc, x, W0, b0, W1, b1, out):
         make_identity(nc, identf[:])
         identb = const.tile([P, P], BF16, name="identb", tag="identb")
         make_identity(nc, identb[:])
-        stx = const.tile([P, P], F32, name="stx", tag="stx")
-        nc.vector.memset(stx[:], 0.0)
-        stn = const.tile([P, P], F32, name="stn", tag="stn")
-        nc.vector.memset(stn[:], 0.0)
         b0col = const.tile([P, 8], F32, name="b0col", tag="b0col")
         w0codes = const.tile([P, C, 2, K0], U32, name="w0codes", tag="w0codes", align_bytes=64)
         w0sc = const.tile([P, C, 2, K0], U8, name="w0sc", tag="w0sc", align_bytes=64)
@@ -145,117 +140,84 @@ def tile_shapeletencoder_pa_t_kernel(tc, x, W0, b0, W1, b1, out):
         def a_op(g, idx, lo=0, hi=NA):
             xg = xs[g]
             if g not in his:
-                his[g] = scr.tile([P, NA, SEG], BF16, name="hi", tag="hi")
-                los[g] = scr.tile([P, NA, SEG], BF16, name="lo", tag="lo")
+                his[g] = scr.tile([P, NA, L], BF16, name="hi", tag="hi")
+                los[g] = scr.tile([P, NA, L], BF16, name="lo", tag="lo")
+                sts[g] = small.tile([P, 2, NA, C], F32, name="st", tag="st")
             t = his[g] if idx % 2 == 0 else los[g]
             op = ALU.max if idx % 2 == 0 else ALU.min
+            h = L >> (idx // 2)
             if idx < 2:
-                nc.vector.tensor_tensor(
-                    out=t[:, lo:hi, :], in0=xg[:, lo:hi, 0:SEG], in1=xg[:, lo:hi, SEG : 2 * SEG], op=op
-                )
+                nc.vector.tensor_tensor(out=t[:, lo:hi, :], in0=xg[:, lo:hi, 0:L], in1=xg[:, lo:hi, L : 2 * L], op=op)
             elif idx < LEVELS - 2:
-                h = SEG >> (idx // 2)
-                nc.vector.tensor_tensor(
-                    out=t[:, lo:hi, 0:h], in0=t[:, lo:hi, 0:h], in1=t[:, lo:hi, h : 2 * h], op=op
-                )
+                nc.vector.tensor_tensor(out=t[:, lo:hi, 0:h], in0=t[:, lo:hi, 0:h], in1=t[:, lo:hi, h : 2 * h], op=op)
             else:
-                h = SEG >> (LEVELS // 2 - 2)
-                st = stx if idx % 2 == 0 else stn
                 nc.vector.tensor_reduce(
-                    out=st[:, 2 * lo : 2 * hi].rearrange("p (a c) -> p a c", c=C),
-                    in_=t[:, lo:hi, 0:h].rearrange("p a (s c) -> p a c s", c=C),
+                    out=sts[g][:, idx % 2, lo:hi, :],
+                    in_=t[:, lo:hi, 0 : 2 * h].rearrange("p a (s c) -> p a c s", c=C),
                     axis=AX.X,
                     op=op,
-                    negate=(idx % 2 == 1),
                 )
 
-        def chain1(g):
-            p1s[g] = ps_ch.tile([P, 2, P], F32, name="p1", tag="ch")
-            nc.tensor.transpose(out=p1s[g][:, 0, :], in_=stx[:], identity=identf[:])
-            nc.tensor.transpose(out=p1s[g][:, 1, :], in_=stn[:], identity=identf[:])
-
-        def chain2a(g):
-            reds[g] = small.tile([P, 2, 32], F32, name="red", tag="red")
-            nc.vector.tensor_reduce(
-                out=reds[g][:], in_=p1s[g][:].rearrange("q s (e t) -> q s e t", t=4), axis=AX.X, op=ALU.max
-            )
-
-        def chain2b(g):
-            red = reds[g]
-            nsums[g] = small.tile([P, 32, 4], F32, name="nsum", tag="nsum")
+        def mid_sum(g, lo=0, hi=NA):
+            nsums[(g, lo)] = small.tile([P, NA, C], F32, name="msum", tag="msum")
             nc.vector.tensor_tensor(
-                out=nsums[g][:],
-                in0=red[:, 1, :].unsqueeze(2).to_broadcast([P, 32, 4]),
-                in1=red[:, 0, :].unsqueeze(2).to_broadcast([P, 32, 4]),
-                op=ALU.subtract,
+                out=nsums[(g, lo)][:, lo:hi, :], in0=sts[g][:, 0, lo:hi, :], in1=sts[g][:, 1, lo:hi, :], op=ALU.add
             )
 
-        def chain3(g):
-            p2s[g] = ps_ch.tile([P, P], F32, name="p2", tag="ch")
-            nc.tensor.transpose(out=p2s[g][:], in_=nsums[g][:].rearrange("q e t -> q (e t)"), identity=identf[:])
-
-        def chain4(g, halves=(0, 1)):
-            nm = small.tile([P, 32], F32, name="negmid", tag="negmid")
-            nc.vector.tensor_scalar(out=nm[:], in0=p2s[g][:, 0:32], scalar1=0.5, scalar2=None, op0=ALU.mult)
-            for h in halves:
-                negmids[(g, h)] = nm
+        def mid_neg(g, lo=0, hi=NA):
+            nm = small.tile([P, NA, C], F32, name="negmid", tag="negmid")
+            nc.vector.tensor_scalar(
+                out=nm[:, lo:hi, :], in0=nsums[(g, lo)][:, lo:hi, :], scalar1=-0.5, scalar2=None, op0=ALU.mult
+            )
+            for a in range(lo, hi):
+                negmids[(g, a)] = nm
 
         def subtract(k):
             g, c, h = k // 4, (k // 2) % 2, k % 2
             if k % 4 == 0:
-                nts[g] = npool.tile([P, NA, C, SEG], BF16, name="nt", tag="nt")
-            nv = b_on_vector(k)
-            for i in range(8 - pe_rows(k)):
-                a = 8 * h + i
-                src = xs[g][:, a, :].rearrange("p (s c) -> p s c", c=C)[:, :, c]
-                bias = negmids[(g, h)][:, 2 * a + c : 2 * a + c + 1]
-                if i < nv:
-                    nc.vector.tensor_scalar(
-                        out=nts[g][:, a, c, :], in0=src, scalar1=bias, scalar2=None, op0=ALU.add
-                    )
+                nts[g] = npool.tile([P, NA, C, L], BF16, name="nt", tag="nt")
+            pieces = [(a, q) for a in (2 * h, 2 * h + 1) for q in ((1,) if on_tensor(k) else (0, 1))]
+            for i, (a, q) in enumerate(pieces):
+                src = xs[g][:, a, :].rearrange("p (s c) -> p s c", c=C)[:, L // 2 * q : L // 2 * (q + 1), c]
+                dst = nts[g][:, a, c, L // 2 * q : L // 2 * (q + 1)]
+                bias = negmids[(g, a)][:, a, c : c + 1]
+                if i < b_on_vector(k):
+                    nc.vector.tensor_scalar(out=dst, in0=src, scalar1=bias, scalar2=None, op0=ALU.add)
                 else:
-                    nc.scalar.activation(
-                        out=nts[g][:, a, c, :], in_=src, func=ACT.Identity, bias=bias, scale=1.0
-                    )
+                    nc.scalar.activation(out=dst, in_=src, func=ACT.Identity, bias=bias, scale=1.0)
+
+        def word_transposes(tp, g, c, a, q, i):
+            words = nts[g][:, a, c, :].bitcast(F32)
+            for j in range(2):
+                o = 256 * q + P * j
+                nc.tensor.transpose(out=tp[:, i, j, :], in_=words[:, o : o + P], identity=identf[:])
 
         def fill(k, j):
             g, c, h = k // 4, (k // 2) % 2, k % 2
-            if pe_rows(k) == 0:
-                tp = ps_tp.tile([P, 8 * P], BF16, name="tp", tag="tp")
-                for i in range(8):
-                    nc.tensor.transpose(
-                        out=tp[:, P * i : P * (i + 1)],
-                        in_=nts[g][:, 8 * h + i, c, P * j : P * (j + 1)],
-                        identity=identb[:],
-                    )
+            if not on_tensor(k):
+                tp = ps_tp.tile([P, 2, 2, P], F32, name="tp", tag="tp")
+                for q in range(2):
+                    word_transposes(tp, g, c, 2 * h + j, q, q)
             elif j < 2:
                 tp = ps_tp.tile([P, 4, P], F32, name="pb", tag="tp")
-                for i in range(4):
-                    a = 8 * h + 4 + i
+                a = 2 * h + j
+                xv = xs[g][:, a, 0:L].rearrange("p (j w e c) -> p j e c w", j=2, w=P, e=2, c=C)
+                for t in range(4):
                     nc.tensor.matmul(
-                        out=tp[:, i, :],
-                        lhsT=xs[g][:, a, :].rearrange("p (s c) -> p s c", c=C)[:, P * j : P * (j + 1), c],
-                        rhs=identb[:],
-                        start=True,
-                        stop=False,
+                        out=tp[:, t, :], lhsT=xv[:, t // 2, t % 2, c, :], rhs=identb[:], start=True, stop=False
                     )
                     nc.tensor.matmul(
-                        out=tp[:, i, :],
-                        lhsT=negmids[(g, h)][:, 2 * a + c : 2 * a + c + 1].to_broadcast([P, P]),
+                        out=tp[:, t, :],
+                        lhsT=negmids[(g, a)][:, a, c : c + 1].to_broadcast([P, P]),
                         rhs=identf[:],
                         start=False,
                         stop=True,
                         is_transpose=True,
                     )
             else:
-                tp = ps_tp.tile([P, 2, 4, P], BF16, name="tq", tag="tp")
-                for gk in range(2):
-                    for i in range(4):
-                        nc.tensor.transpose(
-                            out=tp[:, gk, i, :],
-                            in_=nts[g][:, 8 * h + i, c, P * gk : P * (gk + 1)],
-                            identity=identb[:],
-                        )
+                tp = ps_tp.tile([P, 2, 2, P], F32, name="tq", tag="tp")
+                for i in range(2):
+                    word_transposes(tp, g, c, 2 * h + i, 1, i)
             tps[(k, j)] = tp
 
         def parts(chi):
@@ -272,12 +234,19 @@ def tile_shapeletencoder_pa_t_kernel(tc, x, W0, b0, W1, b1, out):
                 gns[chi] = gpool.tile([P, 8 * CELLS], BF16, name="gn", tag="gn", align_bytes=64)
             tp = tps[(k, j)]
             gv = g_view(chi)
-            if pe_rows(k) == 0:
-                nc.scalar.copy(out=gv[:, j, h, :], in_=tp[:])
+            if not on_tensor(k):
+                o = gv[:, :, h, 512 * j : 512 * (j + 1)].bitcast(F32)
+                nc.scalar.copy(
+                    out=o.rearrange("p q (x j) -> p q x j", j=2), in_=tp[:].rearrange("p q j x -> p q x j")
+                )
             elif j < 2:
-                nc.scalar.copy(out=gv[:, j, h, 512:1024], in_=tp[:].rearrange("p i w -> p (i w)"))
+                o = gv[:, 0, h, 512 * j : 512 * (j + 1)]
+                nc.scalar.copy(out=o.rearrange("p (x t) -> p x t", t=4), in_=tp[:].rearrange("p t x -> p x t"))
             else:
-                nc.scalar.copy(out=gv[:, :, h, 0:512], in_=tp[:].rearrange("p g i w -> p g (i w)"))
+                o = gv[:, 1, h, :].bitcast(F32)
+                nc.scalar.copy(
+                    out=o.rearrange("p (i x j) -> p i x j", i=2, j=2), in_=tp[:].rearrange("p i j x -> p i x j")
+                )
 
         def quantise_n(chi, part=0):
             n = 2 * CELLS // parts(chi)
@@ -405,7 +374,7 @@ def tile_shapeletencoder_pa_t_kernel(tc, x, W0, b0, W1, b1, out):
             w0gs[i] = wstage.tile([P, K0, 4], BF16, name="w0g", tag="w0g", align_bytes=64)
             nc.scalar.copy(
                 out=w0gs[i][:].rearrange("q (w i) t -> q w t i", i=4),
-                in_=w0rv[:, c, :, gk, :].rearrange("q t (w i) -> q w t i", i=4),
+                in_=w0rv[:, c, gk, :, :].rearrange("q t (w i) -> q w t i", i=4),
             )
 
         def quantise_w0(i):
@@ -427,31 +396,25 @@ def tile_shapeletencoder_pa_t_kernel(tc, x, W0, b0, W1, b1, out):
         regroup_w0(0)
         for piece in PIECES0[0]:
             pairs(*piece)
-        levels(0, 8)
-        chain1(0)
+        levels(0, 2)
         regroup_w0(1)
-        a_op(0, 0, 8, 12)
-        chain2a(0)
-        chain2b(0)
-        chain3(0)
-        a_op(0, 1, 8, 12)
-        chain4(0, (0,))
+        a_op(0, 0, 2, 3)
+        mid_sum(0, 0, 2)
+        a_op(0, 1, 2, 3)
+        mid_neg(0, 0, 2)
         subtract(0)
         for j in range(3):
             fill(0, j)
         quantise_w0(0)
         regroup_w0(2)
-        pairs(12, 16)
-        levels(8, 16)
-        chain1(0)
+        pairs(3, 4)
+        levels(2, 4)
         for j in range(3):
             evacuate(0, j)
         quantise_w0(1)
-        chain2a(0)
-        chain2b(0)
-        chain3(0)
+        mid_sum(0, 2, 4)
         quantise_w0(2)
-        chain4(0, (1,))
+        mid_neg(0, 2, 4)
         regroup_w0(3)
         a_op(1, 0)
         a_op(1, 1)
@@ -487,24 +450,19 @@ def tile_shapeletencoder_pa_t_kernel(tc, x, W0, b0, W1, b1, out):
 
             if k % 4 == 0 and 3 <= k // 4 + 2 < NG:
                 load_x(k // 4 + 2)
-            if k == 3:
-                chain2a(1)
-                chain2b(1)
-                chain3(1)
-                chain4(1)
             if k > 1:
                 evacuate(k - 1, 0)
             if now_i:
                 bias1(chi_i)
-            if chain_now and k > 3:
-                chain2a(gc)
+            if chain_now:
+                mid_sum(gc)
             subtract(k)
             if now_g:
                 regroup_h(chi_g)
             if now_q:
                 quantise_n(chi_q)
-            if chain_now and k > 3:
-                chain2b(gc)
+            if chain_now:
+                mid_neg(gc)
             if now_l1:
                 layer1(chi_l1)
             for g, idx in tree_ops[:third]:
@@ -521,16 +479,12 @@ def tile_shapeletencoder_pa_t_kernel(tc, x, W0, b0, W1, b1, out):
                 relu0(f0)
             for g, idx in tree_ops[2 * third :]:
                 a_op(g, idx)
-            if chain_now and k > 3:
-                chain3(gc)
             if u0 >= 0:
                 layer0(u0)
                 layer0(u0 + 1)
             if now_i2:
                 relu1(chi_i2)
                 store(chi_i2)
-            if (ga < NG and j == 3 and k > 2) or k == 2:
-                chain1(1 if k == 2 else ga)
             if f0 >= 0:
                 relu0(f0 + 1)
             if k == 1:
@@ -546,11 +500,9 @@ def tile_shapeletencoder_pa_t_kernel(tc, x, W0, b0, W1, b1, out):
                     scales=w1sc[:].rearrange("p c k -> p (c k)"),
                     in_=w1g[:].rearrange("p c k t -> p (c k t)"),
                 )
-            if k > 1 and pe_rows(k - 1) > 0:
+            if k > 1 and on_tensor(k - 1):
                 evacuate(k - 1, 2)
-            if chain_now and k > 3:
-                chain4(gc)
-            if pe_rows(k) > 0:
+            if on_tensor(k):
                 fill(k, 2)
 
         ul = 4 * LAST

@@ -33,12 +33,10 @@ LAG_L1 = 7
 LAG_I = 8
 LAG_I2 = 9
 LEVELS = 14
+TAIL = [("b1", -3, 0), ("ev", 0), ("L0", -2, 0, 0), ("R0", -4, 0, 0), ("qn", 0), ("ev", 1), ("L0", -1, 0, 0), ("R0", -3, 0, 0), ("rg", -2, 0), ("qn", 1), ("R0", -1, 0, 1), ("R0", -2, 0, 0), ("qh", -2, 0), ("L0", 0, 0, 1), ("L0", 1, 0, 1), ("L0", 2, 0, 1), ("R0", 0, 0, 0), ("L0", 3, 0, 1), ("R0", 1, 0, 0), ("L0", 0, 1, 0), ("R0", 2, 0, 0), ("L0", 1, 1, 0), ("R0", 3, 0, 0), ("rg", -1, 0), ("l1", -2, 0, 1), ("R0", 0, 1, 0), ("L0", 2, 1, 0), ("R0", 1, 1, 0), ("L0", 3, 1, 0), ("r1", -3, 0, 1), ("R0", 2, 1, 0), ("b1", -2, 0), ("R0", 3, 1, 0), ("qh", -1, 0), ("rg", 0, 0), ("l1", -1, 0, 1), ("qh", 0, 0), ("rg", 0, 1), ("l1", 0, 0, 1), ("b1", -1, 0), ("r1", -2, 0, 1), ("qh", 0, 1), ("l1", 0, 1, 1), ("b1", 0, 0), ("r1", -1, 0, 1), ("r1", 0, 0, 0), ("b1", 0, 1), ("r1", 0, 1, 0)]
+ORDER = ["x", "ev0", "sub", "qn", "ms", "ev1", "rg", "f0", "mn", "ev2", "T0", "f1", "l1", "R0a", "W", "L0a", "R0b", "qh", "f2", "T1", "b1", "T2", "r1", "L0b"]
 A_PARTS = ((0,), (1, 2), (3,), tuple(range(4, LEVELS)))
 PIECES0 = (((0, 1), (1, 2)), ((2, 3), (3, 4)))
-
-
-def b_on_vector(k):
-    return 3 if k >= 28 else 0
 
 
 def on_tensor(k):
@@ -176,35 +174,28 @@ def tile_shapeletencoder_pa_t_kernel(tc, x, W0, b0, W1, b1, out):
             g, c, h = k // 4, (k // 2) % 2, k % 2
             if k % 4 == 0:
                 nts[g] = npool.tile([P, NA, C, L], BF16, name="nt", tag="nt")
-            pieces = [(a, q) for a in (2 * h, 2 * h + 1) for q in ((1,) if on_tensor(k) else (0, 1))]
-            for i, (a, q) in enumerate(pieces):
-                src = xs[g][:, a, :].rearrange("p (s c) -> p s c", c=C)[:, L // 2 * q : L // 2 * (q + 1), c]
-                dst = nts[g][:, a, c, L // 2 * q : L // 2 * (q + 1)]
+            if on_tensor(k):
+                pieces = ((2 * h + 1, 0, L, False),)
+            else:
+                pieces = ((2 * h, 0, L, True), (2 * h + 1, 0, L // 2, True), (2 * h + 1, L // 2, L, False))
+            for a, s0, s1, on_vector in pieces:
+                src = xs[g][:, a, :].rearrange("p (s c) -> p s c", c=C)[:, s0:s1, c]
+                dst = nts[g][:, a, c, s0:s1]
                 bias = negmids[(g, a)][:, a, c : c + 1]
-                if i < b_on_vector(k):
+                if on_vector:
                     nc.vector.tensor_scalar(out=dst, in0=src, scalar1=bias, scalar2=None, op0=ALU.add)
                 else:
                     nc.scalar.activation(out=dst, in_=src, func=ACT.Identity, bias=bias, scale=1.0)
 
-        def word_transposes(tp, g, c, a, q, i):
-            words = nts[g][:, a, c, :].bitcast(F32)
-            for j in range(2):
-                o = 256 * q + P * j
-                nc.tensor.transpose(out=tp[:, i, j, :], in_=words[:, o : o + P], identity=identf[:])
-
         def fill(k, j):
             g, c, h = k // 4, (k // 2) % 2, k % 2
-            if not on_tensor(k):
-                tp = ps_tp.tile([P, 2, 2, P], F32, name="tp", tag="tp")
-                for q in range(2):
-                    word_transposes(tp, g, c, 2 * h + j, q, q)
-            elif j < 2:
+            if on_tensor(k) and j < 2:
                 tp = ps_tp.tile([P, 4, P], F32, name="pb", tag="tp")
-                a = 2 * h + j
-                xv = xs[g][:, a, 0:L].rearrange("p (j w e c) -> p j e c w", j=2, w=P, e=2, c=C)
+                a = 2 * h
+                xv = xs[g][:, a, :].rearrange("p (q j w e c) -> p q j e c w", q=2, j=2, w=P, e=2, c=C)
                 for t in range(4):
                     nc.tensor.matmul(
-                        out=tp[:, t, :], lhsT=xv[:, t // 2, t % 2, c, :], rhs=identb[:], start=True, stop=False
+                        out=tp[:, t, :], lhsT=xv[:, j, t // 2, t % 2, c, :], rhs=identb[:], start=True, stop=False
                     )
                     nc.tensor.matmul(
                         out=tp[:, t, :],
@@ -215,9 +206,13 @@ def tile_shapeletencoder_pa_t_kernel(tc, x, W0, b0, W1, b1, out):
                         is_transpose=True,
                     )
             else:
-                tp = ps_tp.tile([P, 2, 2, P], F32, name="tq", tag="tp")
-                for i in range(2):
-                    word_transposes(tp, g, c, 2 * h + i, 1, i)
+                a = 2 * h + min(j, 1)
+                tp = ps_tp.tile([P, 2, 2, P], F32, name="tp", tag="tp")
+                words = nts[g][:, a, c, :].bitcast(F32)
+                for q in range(2):
+                    for w in range(2):
+                        o = 256 * q + P * w
+                        nc.tensor.transpose(out=tp[:, q, w, :], in_=words[:, o : o + P], identity=identf[:])
             tps[(k, j)] = tp
 
         def parts(chi):
@@ -234,18 +229,14 @@ def tile_shapeletencoder_pa_t_kernel(tc, x, W0, b0, W1, b1, out):
                 gns[chi] = gpool.tile([P, 8 * CELLS], BF16, name="gn", tag="gn", align_bytes=64)
             tp = tps[(k, j)]
             gv = g_view(chi)
-            if not on_tensor(k):
-                o = gv[:, :, h, 512 * j : 512 * (j + 1)].bitcast(F32)
-                nc.scalar.copy(
-                    out=o.rearrange("p q (x j) -> p q x j", j=2), in_=tp[:].rearrange("p q j x -> p q x j")
-                )
-            elif j < 2:
-                o = gv[:, 0, h, 512 * j : 512 * (j + 1)]
+            if on_tensor(k) and j < 2:
+                o = gv[:, j, h, 0:512]
                 nc.scalar.copy(out=o.rearrange("p (x t) -> p x t", t=4), in_=tp[:].rearrange("p t x -> p x t"))
             else:
-                o = gv[:, 1, h, :].bitcast(F32)
+                i = min(j, 1)
+                o = gv[:, :, h, 512 * i : 512 * (i + 1)].bitcast(F32)
                 nc.scalar.copy(
-                    out=o.rearrange("p (i x j) -> p i x j", i=2, j=2), in_=tp[:].rearrange("p i j x -> p i x j")
+                    out=o.rearrange("p q (x j) -> p q x j", j=2), in_=tp[:].rearrange("p q j x -> p q x j")
                 )
 
         def quantise_n(chi, part=0):
@@ -352,11 +343,11 @@ def tile_shapeletencoder_pa_t_kernel(tc, x, W0, b0, W1, b1, out):
                 op=ALU.add,
             )
 
-        def relu1(chi, part=0):
+        def relu1(chi, part=0, on_scalar=None):
             g, c = chi // 2, chi % 2
             nb = 4 // parts(chi)
             o = osbs[g][:, nb * part : nb * (part + 1), c, :]
-            if relu1_on_scalar(chi):
+            if relu1_on_scalar(chi) if on_scalar is None else on_scalar:
                 nc.scalar.activation(out=o, in_=o, func=ACT.Relu)
             else:
                 nc.vector.tensor_scalar_max(out=o, in0=o, scalar1=0.0)
@@ -413,13 +404,12 @@ def tile_shapeletencoder_pa_t_kernel(tc, x, W0, b0, W1, b1, out):
             evacuate(0, j)
         quantise_w0(1)
         mid_sum(0, 2, 4)
-        quantise_w0(2)
+        a_op(1, 0)
         mid_neg(0, 2, 4)
         regroup_w0(3)
-        a_op(1, 0)
         a_op(1, 1)
 
-        for k in range(1, NSLOT):
+        def act(name, k):
             gc = (k + 2) // 4
             chain_now = k == 3 or ((k + 2) % 4 == 0 and 2 <= gc < NG)
             if k == 3:
@@ -433,6 +423,7 @@ def tile_shapeletencoder_pa_t_kernel(tc, x, W0, b0, W1, b1, out):
             if k == 3:
                 tree_ops = [(2, 0), (2, 1), (2, 2)]
             third = (len(tree_ops) + 2) // 3
+            cut = (0, third, 2 * third, len(tree_ops))
             chi_q, chi_g, chi_l1, chi_i, chi_i2 = (
                 (k - LAG_Q) // 2,
                 (k - LAG_G) // 2,
@@ -447,108 +438,101 @@ def tile_shapeletencoder_pa_t_kernel(tc, x, W0, b0, W1, b1, out):
             now_i2 = (k - LAG_I2) % 2 == 0 and chi_i2 >= 0
             u0 = 2 * (k - LAG_U)
             f0 = 2 * (k - LAG_F)
-
-            if k % 4 == 0 and 3 <= k // 4 + 2 < NG:
+            if name == "x" and k % 4 == 0 and 3 <= k // 4 + 2 < NG:
                 load_x(k // 4 + 2)
-            if k > 1:
+            if name == "ev0" and k > 1:
                 evacuate(k - 1, 0)
-            if now_i:
-                bias1(chi_i)
-            if chain_now:
-                mid_sum(gc)
-            subtract(k)
-            if now_g:
-                regroup_h(chi_g)
-            if now_q:
-                quantise_n(chi_q)
-            if chain_now:
-                mid_neg(gc)
-            if now_l1:
-                layer1(chi_l1)
-            for g, idx in tree_ops[:third]:
-                a_op(g, idx)
-            if now_g:
-                quantise_h(chi_g)
-            fill(k, 0)
-            for g, idx in tree_ops[third : 2 * third]:
-                a_op(g, idx)
-            if k > 1:
+            if name == "ev1" and k > 1:
                 evacuate(k - 1, 1)
-            fill(k, 1)
-            if f0 >= 0:
-                relu0(f0)
-            for g, idx in tree_ops[2 * third :]:
-                a_op(g, idx)
-            if u0 >= 0:
-                layer0(u0)
-                layer0(u0 + 1)
-            if now_i2:
+            if name == "ev2" and k > 1 and on_tensor(k - 1):
+                evacuate(k - 1, 2)
+            if name == "ms" and chain_now:
+                mid_sum(gc)
+            if name == "mn" and chain_now:
+                mid_neg(gc)
+            if name == "sub":
+                subtract(k)
+                done.add(k)
+            if name in ("f0", "f1"):
+                assert on_tensor(k) or k in done
+                fill(k, int(name[1]))
+            if name == "f2" and on_tensor(k):
+                assert k in done
+                fill(k, 2)
+            if name == "qn" and now_q:
+                quantise_n(chi_q)
+            if name == "rg" and now_g:
+                regroup_h(chi_g)
+                done.add(("rg", chi_g))
+            if name == "qh" and now_g:
+                assert ("rg", chi_g) in done
+                quantise_h(chi_g)
+            if name == "l1" and now_l1:
+                layer1(chi_l1)
+            if name == "b1" and now_i:
+                bias1(chi_i)
+                done.add(("b1", chi_i))
+            if name == "r1" and now_i2:
                 relu1(chi_i2)
                 store(chi_i2)
-            if f0 >= 0:
+            if name in ("T0", "T1", "T2"):
+                q = int(name[1])
+                assert q == 0 or ("T%d" % (q - 1), k, "s") in done
+                done.add((name, k, "s"))
+                for g, idx in tree_ops[cut[q] : cut[q + 1]]:
+                    a_op(g, idx)
+            if name == "R0a" and f0 >= 0:
+                relu0(f0)
+            if name == "R0b" and f0 >= 0:
                 relu0(f0 + 1)
-            if k == 1:
-                bzt = ps_ch.tile([P, P], BF16, name="bzt", tag="ch")
-                nc.tensor.transpose(out=bzt[:], in_=bz[:], identity=identb[:])
-                quantise_w0(3)
-                nc.vector.tensor_copy(out=b0col[:], in_=bzt[:, 0:8])
-            if k == 2:
-                nc.scalar.copy(out=w1g[:], in_=w1raw[:].rearrange("p (c t) k -> p c k t", c=C, t=4))
-            if k == 3:
-                nc.vector.quantize_mx(
-                    out=w1codes[:].rearrange("p c k -> p (c k)").bitcast(FP8X4),
-                    scales=w1sc[:].rearrange("p c k -> p (c k)"),
-                    in_=w1g[:].rearrange("p c k t -> p (c k t)"),
-                )
-            if k > 1 and on_tensor(k - 1):
-                evacuate(k - 1, 2)
-            if on_tensor(k):
-                fill(k, 2)
+            if name == "L0a" and u0 >= 0:
+                layer0(u0)
+            if name == "L0b" and u0 >= 0:
+                layer0(u0 + 1)
+            if name == "W":
+                if k == 1:
+                    bzt = ps_ch.tile([P, P], BF16, name="bzt", tag="ch")
+                    nc.tensor.transpose(out=bzt[:], in_=bz[:], identity=identb[:])
+                    nc.vector.tensor_copy(out=b0col[:], in_=bzt[:, 0:8])
+                if k == 2:
+                    nc.scalar.copy(out=w1g[:], in_=w1raw[:].rearrange("p (c t) k -> p c k t", c=C, t=4))
+                if k in (3, 4):
+                    quantise_w0(k - 1)
+                if k == 5:
+                    nc.vector.quantize_mx(
+                        out=w1codes[:].rearrange("p c k -> p (c k)").bitcast(FP8X4),
+                        scales=w1sc[:].rearrange("p c k -> p (c k)"),
+                        in_=w1g[:].rearrange("p c k t -> p (c k t)"),
+                    )
+
+        done = set()
+        for k in range(1, NSLOT):
+            for name in ORDER:
+                act(name, k)
 
         ul = 4 * LAST
 
-        evacuate(NSLOT - 1, 0)
-        quantise_n(LAST, 0)
-        layer0(ul - 2)
-        relu0(ul - 4)
-        evacuate(NSLOT - 1, 1)
-        relu0(ul - 3)
-        layer0(ul - 1)
-        for m in range(4):
-            layer0(ul + m, 0, ps_tp if m % 2 else None)
-        regroup_h(LAST - 2)
-        bias1(LAST - 3)
-        quantise_h(LAST - 2)
-        quantise_n(LAST, 1)
-        relu0(ul - 2)
-        relu0(ul - 1)
-        relu1(LAST - 3)
-        store(LAST - 3)
-        layer1(LAST - 2)
-        for m in range(4):
-            relu0(ul + m, 0, m == 3)
-        for m in range(4):
-            layer0(ul + m, 1, ps_tp if m % 2 else None)
-        regroup_h(LAST - 1)
-        bias1(LAST - 2)
-        quantise_h(LAST - 1)
-        regroup_h(LAST, 0)
-        relu1(LAST - 2)
-        store(LAST - 2)
-        for m in range(4):
-            relu0(ul + m, 1, m == 3)
-        quantise_h(LAST, 0)
-        layer1(LAST - 1)
-        layer1(LAST, 0, ps_tp)
-        regroup_h(LAST, 1)
-        bias1(LAST - 1)
-        quantise_h(LAST, 1)
-        relu1(LAST - 1)
-        store(LAST - 1)
-        bias1(LAST, 0)
-        layer1(LAST, 1, ps_tp)
-        relu1(LAST, 0)
-        store(LAST, 0)
-        bias1(LAST, 1)
-        relu1(LAST, 1)
-        store(LAST, 1)
+        def tact(t):
+            n = t[0]
+            if n == "ev":
+                evacuate(NSLOT - 1, t[1])
+            elif n == "qn":
+                quantise_n(LAST, t[1])
+            elif n == "L0":
+                layer0(ul + t[1], t[2], ps_tp if t[3] else None)
+            elif n == "R0":
+                relu0(ul + t[1], t[2], t[3])
+            elif n == "rg":
+                regroup_h(LAST + t[1], t[2])
+            elif n == "qh":
+                quantise_h(LAST + t[1], t[2])
+            elif n == "l1":
+                layer1(LAST + t[1], t[2], ps_tp if t[3] else None)
+            elif n == "b1":
+                bias1(LAST + t[1], t[2])
+            elif n == "r1":
+                relu1(LAST + t[1], t[2], t[3])
+                store(LAST + t[1], t[2])
+
+        for t in TAIL:
+            tact(t)

@@ -195,14 +195,15 @@ def tile_shapeletencoder_pa_t_kernel(tc, x, W0, b0, W1, b1, out):
                 xv = xs[g][:, a, :].rearrange("p (q j w e c) -> p q j e c w", q=2, j=2, w=P, e=2, c=C)
                 for t in range(4):
                     nc.tensor.matmul(
-                        out=tp[:, t, :], lhsT=xv[:, j, t // 2, t % 2, c, :], rhs=identb[:], start=True, stop=False
+                        out=tp[:, t, :], lhsT=xv[:, j, t // 2, t % 2, c, :], rhs=identb[:], start=(t == 0), stop=False
                     )
+                for t in range(4):
                     nc.tensor.matmul(
                         out=tp[:, t, :],
                         lhsT=negmids[(g, a)][:, a, c : c + 1].to_broadcast([P, P]),
                         rhs=identf[:],
                         start=False,
-                        stop=True,
+                        stop=(t == 3),
                         is_transpose=True,
                     )
             else:

@@ -32,9 +32,9 @@ LAG_G = 6
 LAG_L1 = 7
 LAG_I = 8
 LAG_I2 = 9
-LEVELS = 14
+LEVELS = 12
 TAIL = [("b1", -3, 0), ("ev", 0), ("L0", -2, 0, 0), ("R0", -4, 0, 0), ("qn", 0), ("ev", 1), ("L0", -1, 0, 0), ("R0", -3, 0, 0), ("rg", -2, 0), ("qn", 1), ("R0", -1, 0, 1), ("R0", -2, 0, 0), ("qh", -2, 0), ("L0", 0, 0, 1), ("L0", 1, 0, 1), ("L0", 2, 0, 1), ("R0", 0, 0, 0), ("L0", 3, 0, 1), ("R0", 1, 0, 0), ("L0", 0, 1, 0), ("R0", 2, 0, 0), ("L0", 1, 1, 0), ("R0", 3, 0, 0), ("rg", -1, 0), ("l1", -2, 0, 1), ("R0", 0, 1, 0), ("L0", 2, 1, 0), ("R0", 1, 1, 0), ("L0", 3, 1, 0), ("r1", -3, 0, 1), ("R0", 2, 1, 0), ("b1", -2, 0), ("R0", 3, 1, 0), ("qh", -1, 0), ("rg", 0, 0), ("l1", -1, 0, 1), ("qh", 0, 0), ("rg", 0, 1), ("l1", 0, 0, 1), ("b1", -1, 0), ("r1", -2, 0, 1), ("qh", 0, 1), ("l1", 0, 1, 1), ("b1", 0, 0), ("r1", -1, 0, 1), ("r1", 0, 0, 0), ("b1", 0, 1), ("r1", 0, 1, 0)]
-ORDER = ["x", "ev0", "sub", "qn", "ms", "ev1", "rg", "f0", "mn", "ev2", "T0", "f1", "l1", "R0a", "W", "L0a", "R0b", "qh", "f2", "T1", "b1", "T2", "r1", "L0b"]
+ORDER = ["x", "ev0", "sub", "qn", "ev1", "rg", "ms", "f0", "ev2", "T0", "mn", "f1", "l1", "R0a", "W", "L0a", "R0b", "qh", "f2", "T1", "b1", "T2", "r1", "L0b"]
 A_PARTS = ((0,), (1, 2), (3,), tuple(range(4, LEVELS)))
 PIECES0 = (((0, 1), (1, 2)), ((2, 3), (3, 4)))
 

@@ -24,7 +24,7 @@ FLOPS = 2 * C * NG * CELLS * L * K0 + 2 * C * NG * CELLS * K0 * K1
 
 NSLOT = 4 * NG
 LAST = 2 * NG - 1
-LAG_A = 6
+LAG_A = 5
 LAG_Q = 3
 LAG_U = 3
 LAG_F = 4
@@ -34,13 +34,21 @@ LAG_I = 8
 LAG_I2 = 9
 LEVELS = 12
 TAIL = [("b1", -3, 0), ("ev", 0), ("L0", -2, 0, 0), ("R0", -4, 0, 0), ("qn", 0), ("ev", 1), ("L0", -1, 0, 0), ("R0", -3, 0, 0), ("rg", -2, 0), ("qn", 1), ("R0", -1, 0, 1), ("R0", -2, 0, 0), ("qh", -2, 0), ("L0", 0, 0, 1), ("L0", 1, 0, 1), ("L0", 2, 0, 1), ("R0", 0, 0, 0), ("L0", 3, 0, 1), ("R0", 1, 0, 0), ("L0", 0, 1, 0), ("R0", 2, 0, 0), ("L0", 1, 1, 0), ("R0", 3, 0, 0), ("rg", -1, 0), ("l1", -2, 0, 1), ("R0", 0, 1, 0), ("L0", 2, 1, 0), ("R0", 1, 1, 0), ("L0", 3, 1, 0), ("r1", -3, 0, 1), ("R0", 2, 1, 0), ("b1", -2, 0), ("R0", 3, 1, 0), ("qh", -1, 0), ("rg", 0, 0), ("l1", -1, 0, 1), ("qh", 0, 0), ("rg", 0, 1), ("l1", 0, 0, 1), ("b1", -1, 0), ("r1", -2, 0, 1), ("qh", 0, 1), ("l1", 0, 1, 1), ("b1", 0, 0), ("r1", -1, 0, 1), ("r1", 0, 0, 0), ("b1", 0, 1), ("r1", 0, 1, 0)]
-ORDER = ["x", "ev0", "sub", "qn", "ev1", "rg", "ms", "f0", "ev2", "T0", "mn", "f1", "l1", "R0a", "W", "L0a", "R0b", "qh", "f2", "T1", "b1", "T2", "r1", "L0b"]
-A_PARTS = ((0,), (1, 2), (3,), tuple(range(4, LEVELS)))
+ORDER = ["x", "ev0", "bt", "sub", "qn", "ev1", "rg", "ms", "l1", "f0", "zt", "T0", "b1", "mn", "R0a", "W", "L0a", "R0b", "qh", "f1", "x1", "zc", "T1", "T2", "r1", "L0b"]
+A_PARTS = ((0,), (1,), (2, 3, 4, 5, 6, 7), tuple(range(8, LEVELS)))
 PIECES0 = (((0, 1), (1, 2)), ((2, 3), (3, 4)))
 
 
+def sub_on_vector(k):
+    return L if k >= 28 else 0
+
+
+def swapped(chi):
+    return chi <= 8 and chi % 2 == 0
+
+
 def on_tensor(k):
-    return k < NSLOT - 4
+    return k >= 4
 
 
 def relu1_on_scalar(chi):
@@ -54,8 +62,8 @@ def tile_shapeletencoder_pa_t_kernel(tc, x, W0, b0, W1, b1, out):
         xpool = ctx.enter_context(tc.tile_pool(name="xpool", bufs=3))
         scr = ctx.enter_context(tc.tile_pool(name="scr", bufs=1))
         small = ctx.enter_context(tc.tile_pool(name="small", bufs=2))
-        npool = ctx.enter_context(tc.tile_pool(name="npool", bufs=2))
-        gpool = ctx.enter_context(tc.tile_pool(name="gpool", bufs=3))
+        npool = ctx.enter_context(tc.tile_pool(name="npool", bufs=3))
+        gpool = ctx.enter_context(tc.tile_pool(name="gpool", bufs=2))
         hpool = ctx.enter_context(tc.tile_pool(name="hpool", bufs=2))
         opool = ctx.enter_context(tc.tile_pool(name="opool", bufs=2))
         wstage = ctx.enter_context(tc.tile_pool(name="wstage", bufs=2))
@@ -79,7 +87,10 @@ def tile_shapeletencoder_pa_t_kernel(tc, x, W0, b0, W1, b1, out):
         hps = {}
         hgs = {}
         hcs = {}
+        zps = {}
         ops_ = {}
+        ots = {}
+        xps = {}
         osbs = {}
         w0gs = {}
 
@@ -91,6 +102,53 @@ def tile_shapeletencoder_pa_t_kernel(tc, x, W0, b0, W1, b1, out):
                 xs[g] = xpool.tile([P, NA, C * L], BF16, name="xg", tag="xg")
             for lo, hi in pieces:
                 nc.sync.dma_start(out=xs[g][:, lo:hi, :], in_=x_view(g)[:, lo:hi, :])
+
+        def load_y(g, hs=(0, 1)):
+            for h in hs:
+                for e in range(2):
+                    cells = x[g].rearrange("t c -> (t c)")[2 * e : 2 * e + 3 * P * C * L]
+                    cells = cells.rearrange("(a s z i m) -> a z i s m", a=3, s=2, z=2, i=32, m=C * L)
+                    for z in range(2):
+                        p0 = 64 * z + 32 * e
+                        nc.sync.dma_start(out=ys[(2 * g + h) % 3][p0 : p0 + 32, z, :, :], in_=cells[2 * h, z])
+
+        ys = []
+        for i in range(3):
+            y = const.tile([P, 2, 2, C * L], BF16, name="y%d" % i, tag="y%d" % i)
+            ys.append(y)
+
+        identf = const.tile([P, P], F32, name="identf", tag="identf")
+        make_identity(nc, identf[:])
+        identb = const.tile([P, P], BF16, name="identb", tag="identb")
+        make_identity(nc, identb[:])
+        def ones(i, z, engine):
+            rows = slice(64 * (1 - z), 64 * (2 - z))
+            for s in range(2):
+                for o in range(0, C * L, L):
+                    engine.memset(ys[i][rows, z, s, o : o + L], 1.0)
+
+        ones(2, 0, nc.gpsimd)
+        ones(2, 1, nc.gpsimd)
+        zs = []
+        zts = []
+        for i in range(2):
+            z = const.tile([P, 4, P], BF16, name="z%d" % i, tag="z%d" % i)
+            nc.gpsimd.memset(z[:], 0.0)
+            zs.append(z)
+            zt = const.tile([P, 4, 4, 64], BF16, name="zt%d" % i, tag="zt%d" % i)
+            nc.gpsimd.memset(zt[:], 0.0)
+            zts.append(zt)
+        for i in (0, 1):
+            for z in range(2):
+                ones(i, z, nc.gpsimd)
+
+        def unit_blocks(i):
+            for z in range(2):
+                rows = slice(64 * z, 64 * (z + 1))
+                nc.vector.tensor_copy(
+                    out=zts[i][rows].rearrange("p b (s z) n -> p z (b s) n", z=2)[:, z],
+                    in_=identb[rows, 64 * z : 64 * (z + 1)].unsqueeze(1).to_broadcast([64, 8, 64]),
+                )
 
         w0raw = const.tile([P, C, 8, K0], BF16, name="w0raw", tag="w0raw")
         w0dram = W0.rearrange("c (g j w e) f -> w c g j (e f)", g=2, j=2, w=P, e=2)
@@ -112,9 +170,11 @@ def tile_shapeletencoder_pa_t_kernel(tc, x, W0, b0, W1, b1, out):
         bz = const.tile([P, P], BF16, name="bz", tag="bz")
         nc.vector.memset(bz[:], 0.0)
         nc.sync.dma_start(out=bz[0:8, :], in_=b0.rearrange("c (t p) -> (c t) p", t=4, p=P))
+        nc.sync.dma_start(out=bz[8:10, :], in_=b1)
         w1raw = const.tile([P, 8, K1], BF16, name="w1raw", tag="w1raw")
         nc.sync.dma_start(out=w1raw[:], in_=W1.rearrange("c (t p) k -> p (c t) k", t=4, p=P))
         load_x(2)
+        load_y(1)
         b1b = const.tile([P, C, K1], BF16, name="b1b", tag="b1b")
         nc.sync.dma_start(
             out=b1b[:].rearrange("p c k -> p (c k)"),
@@ -124,11 +184,7 @@ def tile_shapeletencoder_pa_t_kernel(tc, x, W0, b0, W1, b1, out):
         warm = const.tile([P, 1], F32, name="warm", tag="warm")
         nc.vector.memset(warm[:], 0.0)
         nc.scalar.activation(out=warm[:], in_=warm[:], func=ACT.Identity)
-        identf = const.tile([P, P], F32, name="identf", tag="identf")
-        make_identity(nc, identf[:])
-        identb = const.tile([P, P], BF16, name="identb", tag="identb")
-        make_identity(nc, identb[:])
-        b0col = const.tile([P, 8], F32, name="b0col", tag="b0col")
+        b0col = const.tile([P, 10], F32, name="b0col", tag="b0col")
         w0codes = const.tile([P, C, 2, K0], U32, name="w0codes", tag="w0codes", align_bytes=64)
         w0sc = const.tile([P, C, 2, K0], U8, name="w0sc", tag="w0sc", align_bytes=64)
         w1codes = const.tile([P, C, K1], U32, name="w1codes", tag="w1codes", align_bytes=64)
@@ -170,17 +226,39 @@ def tile_shapeletencoder_pa_t_kernel(tc, x, W0, b0, W1, b1, out):
             for a in range(lo, hi):
                 negmids[(g, a)] = nm
 
+        def mid_cols(g):
+            for col in (0, 96):
+                nc.vector.tensor_scalar(
+                    out=zs[g % 2][:, :, col : col + 2].rearrange("p (h c) m -> p h c m", c=C),
+                    in0=sts[g][:].rearrange("p m (h two) c -> p two h c m", two=2)[:, 0],
+                    scalar1=-0.5,
+                    scalar2=None,
+                    op0=ALU.mult,
+                )
+
+        def turn_mid(g):
+            zps[g] = ps_tp.tile([P, 4, P], BF16, name="zp", tag="tp")
+            for i in range(4):
+                nc.tensor.transpose(out=zps[g][:, i, :], in_=zs[g % 2][:, i, :], identity=identb[:])
+
+        def copy_mid(g):
+            zpv = zps[g][:].rearrange("p b (s z i) -> p z b s i", s=2, z=2)
+            ztv = zts[g % 2][:].rearrange("p b (s z) (e i) -> p z e b s i", z=2, e=2)
+            for z, p0 in ((0, 96), (1, 0)):
+                for e in range(2):
+                    nc.scalar.copy(out=ztv[p0 : p0 + 32, z, e], in_=zpv[p0 : p0 + 32, z])
+
         def subtract(k):
             g, c, h = k // 4, (k // 2) % 2, k % 2
-            if k % 4 == 0:
-                nts[g] = npool.tile([P, NA, C, L], BF16, name="nt", tag="nt")
+            nts[k] = npool.tile([P, 2, L], BF16, name="nt", tag="nt")
             if on_tensor(k):
-                pieces = ((2 * h + 1, 0, L, False),)
+                v = sub_on_vector(k)
+                pieces = [p for p in ((2 * h + 1, 0, v, True), (2 * h + 1, v, L, False)) if p[1] < p[2]]
             else:
-                pieces = ((2 * h, 0, L, True), (2 * h + 1, 0, L // 2, True), (2 * h + 1, L // 2, L, False))
+                pieces = ((2 * h, 0, L, False), (2 * h + 1, 0, L, False))
             for a, s0, s1, on_vector in pieces:
                 src = xs[g][:, a, :].rearrange("p (s c) -> p s c", c=C)[:, s0:s1, c]
-                dst = nts[g][:, a, c, s0:s1]
+                dst = nts[k][:, a % 2, s0:s1]
                 bias = negmids[(g, a)][:, a, c : c + 1]
                 if on_vector:
                     nc.vector.tensor_scalar(out=dst, in0=src, scalar1=bias, scalar2=None, op0=ALU.add)
@@ -189,27 +267,24 @@ def tile_shapeletencoder_pa_t_kernel(tc, x, W0, b0, W1, b1, out):
 
         def fill(k, j):
             g, c, h = k // 4, (k // 2) % 2, k % 2
-            if on_tensor(k) and j < 2:
-                tp = ps_tp.tile([P, 4, P], F32, name="pb", tag="tp")
-                a = 2 * h
-                xv = xs[g][:, a, :].rearrange("p (q j w e c) -> p q j e c w", q=2, j=2, w=P, e=2, c=C)
-                for t in range(4):
-                    nc.tensor.matmul(
-                        out=tp[:, t, :], lhsT=xv[:, j, t // 2, t % 2, c, :], rhs=identb[:], start=(t == 0), stop=False
-                    )
-                for t in range(4):
-                    nc.tensor.matmul(
-                        out=tp[:, t, :],
-                        lhsT=negmids[(g, a)][:, a, c : c + 1].to_broadcast([P, P]),
-                        rhs=identf[:],
-                        start=False,
-                        stop=(t == 3),
-                        is_transpose=True,
-                    )
+            if on_tensor(k) and j == 0:
+                tp = ps_tp.tile([P, 2, P, 4], BF16, name="pb", tag="tp")
+                yv = ys[(2 * g + h) % 3][:].rearrange("p z s (q j w e c) -> p z s q j e c w", q=2, j=2, w=P, e=2, c=C)
+                ztv = zts[g % 2][:].rearrange("p b r (e i) -> p b r e i", e=2)
+                for q in range(2):
+                    for j2 in range(2):
+                        for r in range(4):
+                            nc.tensor.matmul(
+                                out=tp[:, q, 32 * r : 32 * (r + 1), 2 * j2 : 2 * j2 + 2].rearrange("p i e -> p e i"),
+                                lhsT=yv[:, r % 2, r // 2, q, j2, 0, c, :],
+                                rhs=ztv[:, 2 * h + c, r],
+                                start=True,
+                                stop=True,
+                            )
             else:
                 a = 2 * h + min(j, 1)
                 tp = ps_tp.tile([P, 2, 2, P], F32, name="tp", tag="tp")
-                words = nts[g][:, a, c, :].bitcast(F32)
+                words = nts[k][:, a % 2, :].bitcast(F32)
                 for q in range(2):
                     for w in range(2):
                         o = 256 * q + P * w
@@ -230,9 +305,8 @@ def tile_shapeletencoder_pa_t_kernel(tc, x, W0, b0, W1, b1, out):
                 gns[chi] = gpool.tile([P, 8 * CELLS], BF16, name="gn", tag="gn", align_bytes=64)
             tp = tps[(k, j)]
             gv = g_view(chi)
-            if on_tensor(k) and j < 2:
-                o = gv[:, j, h, 0:512]
-                nc.scalar.copy(out=o.rearrange("p (x t) -> p x t", t=4), in_=tp[:].rearrange("p t x -> p x t"))
+            if on_tensor(k) and j == 0:
+                nc.scalar.copy(out=gv[:, :, h, 0:512], in_=tp[:].rearrange("p q x t -> p q (x t)"))
             else:
                 i = min(j, 1)
                 o = gv[:, :, h, 512 * i : 512 * (i + 1)].bitcast(F32)
@@ -332,6 +406,38 @@ def tile_shapeletencoder_pa_t_kernel(tc, x, W0, b0, W1, b1, out):
                     stop=True,
                 )
 
+        def layer1_t(chi):
+            c = chi % 2
+            codes, sc = hcs[chi]
+            ops_[chi] = ps_o.tile([P, CELLS], F32, name="ot_ps", tag="o")
+            nc.tensor.matmul_mx(
+                out=ops_[chi][:],
+                lhsT=w1codes[:, c, :].bitcast(FP8X4),
+                lhsT_scale=w1sc[:, c, :],
+                rhs=codes[:].bitcast(FP8X4),
+                rhs_scale=sc[:],
+                start=True,
+                stop=True,
+            )
+
+        def bias_relu_t(chi):
+            c = chi % 2
+            ots[chi] = opool.tile([P, CELLS], F32, name="ot", tag="ot")
+            nc.scalar.activation(
+                out=ots[chi][:], in_=ops_[chi][:], func=ACT.Relu, bias=b0col[:, 8 + c : 9 + c], scale=1.0
+            )
+
+        def turn_back(chi):
+            xps[chi] = ps_ch.tile([P, 4, P], F32, name="ox", tag="ch")
+            for j in range(4):
+                nc.tensor.transpose(out=xps[chi][:, j, :], in_=ots[chi][:, P * j : P * (j + 1)], identity=identf[:])
+
+        def copy_out(chi):
+            g, c = chi // 2, chi % 2
+            if c == 0:
+                osbs[g] = opool.tile([P, 4, C, K1], F32, name="osb", tag="osb")
+            nc.scalar.copy(out=osbs[g][:, :, c, :], in_=xps[chi][:])
+
         def bias1(chi, part=0):
             g, c = chi // 2, chi % 2
             nb = 4 // parts(chi)
@@ -395,13 +501,13 @@ def tile_shapeletencoder_pa_t_kernel(tc, x, W0, b0, W1, b1, out):
         a_op(0, 1, 2, 3)
         mid_neg(0, 0, 2)
         subtract(0)
-        for j in range(3):
+        for j in range(2):
             fill(0, j)
         quantise_w0(0)
         regroup_w0(2)
         pairs(3, 4)
         levels(2, 4)
-        for j in range(3):
+        for j in range(2):
             evacuate(0, j)
         quantise_w0(1)
         mid_sum(0, 2, 4)
@@ -411,18 +517,16 @@ def tile_shapeletencoder_pa_t_kernel(tc, x, W0, b0, W1, b1, out):
         a_op(1, 1)
 
         def act(name, k):
-            gc = (k + 2) // 4
-            chain_now = k == 3 or ((k + 2) % 4 == 0 and 2 <= gc < NG)
-            if k == 3:
-                gc = 1
+            gc = (k + 1) // 4
+            chain_now = (k + 1) % 4 == 0 and gc < NG
             ga, j = (k + LAG_A) // 4, (k + LAG_A) % 4
             tree_ops = [(ga, idx) for idx in A_PARTS[j]] if ga < NG else []
             if k == 1:
                 tree_ops = [(1, 2), (1, 3), (1, 4)]
             if k == 2:
                 tree_ops = [(1, idx) for idx in range(5, LEVELS)]
-            if k == 3:
-                tree_ops = [(2, 0), (2, 1), (2, 2)]
+            gz = (k + 1) // 4
+            z_now = (k + 1) % 4 == 0 and gz < NG
             third = (len(tree_ops) + 2) // 3
             cut = (0, third, 2 * third, len(tree_ops))
             chi_q, chi_g, chi_l1, chi_i, chi_i2 = (
@@ -439,27 +543,32 @@ def tile_shapeletencoder_pa_t_kernel(tc, x, W0, b0, W1, b1, out):
             now_i2 = (k - LAG_I2) % 2 == 0 and chi_i2 >= 0
             u0 = 2 * (k - LAG_U)
             f0 = 2 * (k - LAG_F)
+            if name == "x" and k % 4 in (0, 3) and 2 <= k // 4 + 1 < NG:
+                load_y(k // 4 + 1, (k % 4 // 3,))
             if name == "x" and k % 4 == 0 and 3 <= k // 4 + 2 < NG:
                 load_x(k // 4 + 2)
             if name == "ev0" and k > 1:
                 evacuate(k - 1, 0)
             if name == "ev1" and k > 1:
                 evacuate(k - 1, 1)
-            if name == "ev2" and k > 1 and on_tensor(k - 1):
-                evacuate(k - 1, 2)
             if name == "ms" and chain_now:
                 mid_sum(gc)
-            if name == "mn" and chain_now:
+                if k == 3:
+                    quantise_w0(2)
+                    mid_neg(gc)
+                mid_cols(gc)
+            if name == "mn" and chain_now and k != 3:
                 mid_neg(gc)
             if name == "sub":
                 subtract(k)
                 done.add(k)
             if name in ("f0", "f1"):
-                assert on_tensor(k) or k in done
+                assert (on_tensor(k) and name == "f0") or k in done
                 fill(k, int(name[1]))
-            if name == "f2" and on_tensor(k):
-                assert k in done
-                fill(k, 2)
+            if name == "zt" and z_now:
+                turn_mid(gz)
+            if name == "zc" and z_now:
+                copy_mid(gz)
             if name == "qn" and now_q:
                 quantise_n(chi_q)
             if name == "rg" and now_g:
@@ -469,12 +578,21 @@ def tile_shapeletencoder_pa_t_kernel(tc, x, W0, b0, W1, b1, out):
                 assert ("rg", chi_g) in done
                 quantise_h(chi_g)
             if name == "l1" and now_l1:
-                layer1(chi_l1)
-            if name == "b1" and now_i:
+                if swapped(chi_l1):
+                    layer1_t(chi_l1)
+                else:
+                    layer1(chi_l1)
+            if name == "bt" and now_i and swapped(chi_i):
+                bias_relu_t(chi_i)
+            if name == "x1" and now_i and swapped(chi_i):
+                turn_back(chi_i)
+            if name == "b1" and now_i and not swapped(chi_i):
                 bias1(chi_i)
-                done.add(("b1", chi_i))
             if name == "r1" and now_i2:
-                relu1(chi_i2)
+                if swapped(chi_i2):
+                    copy_out(chi_i2)
+                else:
+                    relu1(chi_i2)
                 store(chi_i2)
             if name in ("T0", "T1", "T2"):
                 q = int(name[1])
@@ -491,14 +609,16 @@ def tile_shapeletencoder_pa_t_kernel(tc, x, W0, b0, W1, b1, out):
             if name == "L0b" and u0 >= 0:
                 layer0(u0 + 1)
             if name == "W":
+                if k in (1, 2):
+                    unit_blocks(2 - k)
                 if k == 1:
                     bzt = ps_ch.tile([P, P], BF16, name="bzt", tag="ch")
                     nc.tensor.transpose(out=bzt[:], in_=bz[:], identity=identb[:])
-                    nc.vector.tensor_copy(out=b0col[:], in_=bzt[:, 0:8])
+                    nc.vector.tensor_copy(out=b0col[:], in_=bzt[:, 0:10])
                 if k == 2:
                     nc.scalar.copy(out=w1g[:], in_=w1raw[:].rearrange("p (c t) k -> p c k t", c=C, t=4))
-                if k in (3, 4):
-                    quantise_w0(k - 1)
+                if k == 4:
+                    quantise_w0(3)
                 if k == 5:
                     nc.vector.quantize_mx(
                         out=w1codes[:].rearrange("p c k -> p (c k)").bitcast(FP8X4),

@@ -44,7 +44,7 @@ def sub_on_vector(k):
 
 
 def swapped(chi):
-    return chi <= 8 and chi % 2 == 0
+    return chi <= 8 and chi % 4 != 1
 
 
 def on_tensor(k):
@@ -105,49 +105,48 @@ def tile_shapeletencoder_pa_t_kernel(tc, x, W0, b0, W1, b1, out):
 
         def load_y(g, hs=(0, 1)):
             for h in hs:
+                y = ys[(2 * g + h) % 3]
                 for e in range(2):
                     cells = x[g].rearrange("t c -> (t c)")[2 * e : 2 * e + 3 * P * C * L]
-                    cells = cells.rearrange("(a s z i m) -> a z i s m", a=3, s=2, z=2, i=32, m=C * L)
-                    for z in range(2):
-                        p0 = 64 * z + 32 * e
-                        nc.sync.dma_start(out=ys[(2 * g + h) % 3][p0 : p0 + 32, z, :, :], in_=cells[2 * h, z])
+                    cells = cells.rearrange("(a n m) -> a n m", a=3, n=P, m=C * L)[2 * h]
+                    nc.sync.dma_start(
+                        out=y[e:96:2, 0:2, :], in_=cells[0:96, :].rearrange("(s i) m -> i s m", s=2)
+                    )
+                    nc.sync.dma_start(out=y[e:64:2, 2, :], in_=cells[96:P, :])
 
         ys = []
         for i in range(3):
-            y = const.tile([P, 2, 2, C * L], BF16, name="y%d" % i, tag="y%d" % i)
+            y = const.tile([P, 3, C * L], BF16, name="y%d" % i, tag="y%d" % i)
             ys.append(y)
 
         identf = const.tile([P, P], F32, name="identf", tag="identf")
         make_identity(nc, identf[:])
         identb = const.tile([P, P], BF16, name="identb", tag="identb")
         make_identity(nc, identb[:])
-        def ones(i, z, engine):
-            rows = slice(64 * (1 - z), 64 * (2 - z))
-            for s in range(2):
-                for o in range(0, C * L, L):
-                    engine.memset(ys[i][rows, z, s, o : o + L], 1.0)
+        def ones(i, engine):
+            pair = 1.0 + 0x3F80 / 2.0**23
+            engine.memset(ys[i][96:P, 0:2, :].bitcast(F32), pair)
+            engine.memset(ys[i][64:P, 2, :].bitcast(F32), pair)
 
-        ones(2, 0, nc.gpsimd)
-        ones(2, 1, nc.gpsimd)
+        warm = const.tile([P, 1], F32, name="warm", tag="warm")
+        nc.vector.memset(warm[:], 0.0)
+        nc.scalar.activation(out=warm[:], in_=warm[:], func=ACT.Identity)
+        ones(2, nc.vector)
+        ones(0, nc.vector)
         zs = []
         zts = []
         for i in range(2):
-            z = const.tile([P, 4, P], BF16, name="z%d" % i, tag="z%d" % i)
+            z = const.tile([P, 4, P], F32, name="z%d" % i, tag="z%d" % i)
             nc.gpsimd.memset(z[:], 0.0)
             zs.append(z)
-            zt = const.tile([P, 4, 4, 64], BF16, name="zt%d" % i, tag="zt%d" % i)
-            nc.gpsimd.memset(zt[:], 0.0)
+            zt = const.tile([P, 4, 2 * P], BF16, name="zt%d" % i, tag="zt%d" % i)
             zts.append(zt)
-        for i in (0, 1):
-            for z in range(2):
-                ones(i, z, nc.gpsimd)
+        ones(1, nc.gpsimd)
 
         def unit_blocks(i):
-            for z in range(2):
-                rows = slice(64 * z, 64 * (z + 1))
+            for s, n in ((0, 96), (96, 96), (192, 64)):
                 nc.vector.tensor_copy(
-                    out=zts[i][rows].rearrange("p b (s z) n -> p z (b s) n", z=2)[:, z],
-                    in_=identb[rows, 64 * z : 64 * (z + 1)].unsqueeze(1).to_broadcast([64, 8, 64]),
+                    out=zts[i][0:96, :, s : s + n], in_=identb[0:96, 0:n].unsqueeze(1).to_broadcast([96, 4, n])
                 )
 
         w0raw = const.tile([P, C, 8, K0], BF16, name="w0raw", tag="w0raw")
@@ -181,9 +180,6 @@ def tile_shapeletencoder_pa_t_kernel(tc, x, W0, b0, W1, b1, out):
             in_=b1.rearrange("c k -> (c k)").partition_broadcast(P),
         )
 
-        warm = const.tile([P, 1], F32, name="warm", tag="warm")
-        nc.vector.memset(warm[:], 0.0)
-        nc.scalar.activation(out=warm[:], in_=warm[:], func=ACT.Identity)
         b0col = const.tile([P, 10], F32, name="b0col", tag="b0col")
         w0codes = const.tile([P, C, 2, K0], U32, name="w0codes", tag="w0codes", align_bytes=64)
         w0sc = const.tile([P, C, 2, K0], U8, name="w0sc", tag="w0sc", align_bytes=64)
@@ -227,9 +223,10 @@ def tile_shapeletencoder_pa_t_kernel(tc, x, W0, b0, W1, b1, out):
                 negmids[(g, a)] = nm
 
         def mid_cols(g):
-            for col in (0, 96):
+            pairs_ = zs[g % 2][:].bitcast(BF16).rearrange("p (h c) (k d) -> p d h c k", c=C, d=2)
+            for e in range(2):
                 nc.vector.tensor_scalar(
-                    out=zs[g % 2][:, :, col : col + 2].rearrange("p (h c) m -> p h c m", c=C),
+                    out=pairs_[:, e, :, :, 96:98],
                     in0=sts[g][:].rearrange("p m (h two) c -> p two h c m", two=2)[:, 0],
                     scalar1=-0.5,
                     scalar2=None,
@@ -237,16 +234,12 @@ def tile_shapeletencoder_pa_t_kernel(tc, x, W0, b0, W1, b1, out):
                 )
 
         def turn_mid(g):
-            zps[g] = ps_tp.tile([P, 4, P], BF16, name="zp", tag="tp")
+            zps[g] = ps_tp.tile([P, 4, P], F32, name="zp", tag="tp")
             for i in range(4):
-                nc.tensor.transpose(out=zps[g][:, i, :], in_=zs[g % 2][:, i, :], identity=identb[:])
+                nc.tensor.transpose(out=zps[g][:, i, :], in_=zs[g % 2][:, i, :], identity=identf[:])
 
         def copy_mid(g):
-            zpv = zps[g][:].rearrange("p b (s z i) -> p z b s i", s=2, z=2)
-            ztv = zts[g % 2][:].rearrange("p b (s z) (e i) -> p z e b s i", z=2, e=2)
-            for z, p0 in ((0, 96), (1, 0)):
-                for e in range(2):
-                    nc.scalar.copy(out=ztv[p0 : p0 + 32, z, e], in_=zpv[p0 : p0 + 32, z])
+            nc.scalar.copy(out=zts[g % 2][96:P].bitcast(F32), in_=zps[g][96:P])
 
         def subtract(k):
             g, c, h = k // 4, (k // 2) % 2, k % 2
@@ -269,15 +262,14 @@ def tile_shapeletencoder_pa_t_kernel(tc, x, W0, b0, W1, b1, out):
             g, c, h = k // 4, (k // 2) % 2, k % 2
             if on_tensor(k) and j == 0:
                 tp = ps_tp.tile([P, 2, P, 4], BF16, name="pb", tag="tp")
-                yv = ys[(2 * g + h) % 3][:].rearrange("p z s (q j w e c) -> p z s q j e c w", q=2, j=2, w=P, e=2, c=C)
-                ztv = zts[g % 2][:].rearrange("p b r (e i) -> p b r e i", e=2)
+                yv = ys[(2 * g + h) % 3][:].rearrange("p s (q j w e c) -> p s q j e c w", q=2, j=2, w=P, e=2, c=C)
                 for q in range(2):
                     for j2 in range(2):
-                        for r in range(4):
+                        for s, i0, i1 in ((0, 0, 48), (1, 48, 96), (2, 96, P)):
                             nc.tensor.matmul(
-                                out=tp[:, q, 32 * r : 32 * (r + 1), 2 * j2 : 2 * j2 + 2].rearrange("p i e -> p e i"),
-                                lhsT=yv[:, r % 2, r // 2, q, j2, 0, c, :],
-                                rhs=ztv[:, 2 * h + c, r],
+                                out=tp[:, q, i0:i1, 2 * j2 : 2 * j2 + 2],
+                                lhsT=yv[:, s, q, j2, 0, c, :],
+                                rhs=zts[g % 2][:, 2 * h + c, 2 * i0 : 2 * i1].rearrange("p (i e) -> p i e", e=2),
                                 start=True,
                                 stop=True,
                             )

@@ -36,19 +36,20 @@ LEVELS = 12
 TAIL = [("b1", -3, 0), ("ev", 0), ("L0", -2, 0, 0), ("R0", -4, 0, 0), ("qn", 0), ("ev", 1), ("L0", -1, 0, 0), ("R0", -3, 0, 0), ("rg", -2, 0), ("qn", 1), ("R0", -1, 0, 1), ("R0", -2, 0, 0), ("qh", -2, 0), ("L0", 0, 0, 1), ("L0", 1, 0, 1), ("L0", 2, 0, 1), ("R0", 0, 0, 0), ("L0", 3, 0, 1), ("R0", 1, 0, 0), ("L0", 0, 1, 0), ("R0", 2, 0, 0), ("L0", 1, 1, 0), ("R0", 3, 0, 0), ("rg", -1, 0), ("l1", -2, 0, 1), ("R0", 0, 1, 0), ("L0", 2, 1, 0), ("R0", 1, 1, 0), ("L0", 3, 1, 0), ("r1", -3, 0, 1), ("R0", 2, 1, 0), ("b1", -2, 0), ("R0", 3, 1, 0), ("qh", -1, 0), ("rg", 0, 0), ("l1", -1, 0, 1), ("qh", 0, 0), ("rg", 0, 1), ("l1", 0, 0, 1), ("b1", -1, 0), ("r1", -2, 0, 1), ("qh", 0, 1), ("l1", 0, 1, 1), ("b1", 0, 0), ("r1", -1, 0, 1), ("r1", 0, 0, 0), ("b1", 0, 1), ("r1", 0, 1, 0)]
 ORDER = ["x", "ev0", "bt", "sub", "qn", "ev1", "rg", "ms", "l1", "f0", "zt", "T0", "b1", "mn", "R0a", "W", "L0a", "R0b", "qh", "f1", "x1", "zc", "T1", "T2", "r1", "L0b"]
 A_PARTS = ((0,), (1,), (2, 3, 4, 5, 6, 7), tuple(range(8, LEVELS)))
+SLOTS = ((0, 0, 48), (1, 48, 96), (2, 96, 128))
 PIECES0 = (((0, 1), (1, 2)), ((2, 3), (3, 4)))
 
 
 def sub_on_vector(k):
-    return L if k >= 28 else 0
+    return k >= NSLOT - 4
 
 
 def swapped(chi):
-    return chi <= 8 and chi % 4 != 1
+    return chi <= 11 and chi % 4 != 1
 
 
 def on_tensor(k):
-    return k >= 4
+    return 4 <= k < NSLOT - 4
 
 
 def relu1_on_scalar(chi):
@@ -104,19 +105,16 @@ def tile_shapeletencoder_pa_t_kernel(tc, x, W0, b0, W1, b1, out):
                 nc.sync.dma_start(out=xs[g][:, lo:hi, :], in_=x_view(g)[:, lo:hi, :])
 
         def load_y(g, hs=(0, 1)):
+            cells = x[g].rearrange("(a n q d s) c -> a d n q (s c)", a=NA, n=P, q=2, d=2, s=L // 4)
             for h in hs:
-                y = ys[(2 * g + h) % 3]
-                for e in range(2):
-                    cells = x[g].rearrange("t c -> (t c)")[2 * e : 2 * e + 3 * P * C * L]
-                    cells = cells.rearrange("(a n m) -> a n m", a=3, n=P, m=C * L)[2 * h]
-                    nc.sync.dma_start(
-                        out=y[e:96:2, 0:2, :], in_=cells[0:96, :].rearrange("(s i) m -> i s m", s=2)
-                    )
-                    nc.sync.dma_start(out=y[e:64:2, 2, :], in_=cells[96:P, :])
+                y = ys[(2 * g + h) % 3][:].rearrange("p s (q m) -> p s q m", q=2)
+                for s, i0, i1 in SLOTS:
+                    for e in range(2):
+                        nc.sync.dma_start(out=y[e : 2 * (i1 - i0) : 2, s, :, :], in_=cells[2 * h, e, i0:i1])
 
         ys = []
         for i in range(3):
-            y = const.tile([P, 3, C * L], BF16, name="y%d" % i, tag="y%d" % i)
+            y = const.tile([P, 3, C * L // 2], BF16, name="y%d" % i, tag="y%d" % i)
             ys.append(y)
 
         identf = const.tile([P, P], F32, name="identf", tag="identf")
@@ -133,6 +131,7 @@ def tile_shapeletencoder_pa_t_kernel(tc, x, W0, b0, W1, b1, out):
         nc.scalar.activation(out=warm[:], in_=warm[:], func=ACT.Identity)
         ones(2, nc.vector)
         ones(0, nc.vector)
+        ones(1, nc.vector)
         zs = []
         zts = []
         for i in range(2):
@@ -141,7 +140,6 @@ def tile_shapeletencoder_pa_t_kernel(tc, x, W0, b0, W1, b1, out):
             zs.append(z)
             zt = const.tile([P, 4, 2 * P], BF16, name="zt%d" % i, tag="zt%d" % i)
             zts.append(zt)
-        ones(1, nc.gpsimd)
 
         def unit_blocks(i):
             for s, n in ((0, 96), (96, 96), (192, 64)):
@@ -150,14 +148,13 @@ def tile_shapeletencoder_pa_t_kernel(tc, x, W0, b0, W1, b1, out):
                 )
 
         w0raw = const.tile([P, C, 8, K0], BF16, name="w0raw", tag="w0raw")
-        w0dram = W0.rearrange("c (g j w e) f -> w c g j (e f)", g=2, j=2, w=P, e=2)
+        w0dram = W0.rearrange("c (g d j w) f -> w c g j d f", g=2, d=2, j=2, w=P)
         w0rv = w0raw[:].rearrange("w c (g t) f -> w c g t f", g=2, t=4)
 
         def load_w0(i):
             c, gk = i // 2, i % 2
-            nc.sync.dma_start(
-                out=w0rv[:, c, gk, :, :].rearrange("w (j e) f -> w j (e f)", e=2), in_=w0dram[:, c, gk, :, :]
-            )
+            for j in range(2):
+                nc.sync.dma_start(out=w0rv[:, c, gk, 2 * j : 2 * j + 2, :], in_=w0dram[:, c, gk, j, :, :])
 
         load_x(0, PIECES0[0])
         load_w0(0)
@@ -244,16 +241,11 @@ def tile_shapeletencoder_pa_t_kernel(tc, x, W0, b0, W1, b1, out):
         def subtract(k):
             g, c, h = k // 4, (k // 2) % 2, k % 2
             nts[k] = npool.tile([P, 2, L], BF16, name="nt", tag="nt")
-            if on_tensor(k):
-                v = sub_on_vector(k)
-                pieces = [p for p in ((2 * h + 1, 0, v, True), (2 * h + 1, v, L, False)) if p[1] < p[2]]
-            else:
-                pieces = ((2 * h, 0, L, False), (2 * h + 1, 0, L, False))
-            for a, s0, s1, on_vector in pieces:
-                src = xs[g][:, a, :].rearrange("p (s c) -> p s c", c=C)[:, s0:s1, c]
-                dst = nts[k][:, a % 2, s0:s1]
+            for a in (2 * h + 1,) if on_tensor(k) else (2 * h, 2 * h + 1):
+                src = xs[g][:, a, :].rearrange("p (q d m c) -> p c q m d", q=2, d=2, c=C)[:, c]
+                dst = nts[k][:, a % 2, :].rearrange("p (q m d) -> p q m d", q=2, d=2)
                 bias = negmids[(g, a)][:, a, c : c + 1]
-                if on_vector:
+                if sub_on_vector(k):
                     nc.vector.tensor_scalar(out=dst, in0=src, scalar1=bias, scalar2=None, op0=ALU.add)
                 else:
                     nc.scalar.activation(out=dst, in_=src, func=ACT.Identity, bias=bias, scale=1.0)
@@ -262,13 +254,13 @@ def tile_shapeletencoder_pa_t_kernel(tc, x, W0, b0, W1, b1, out):
             g, c, h = k // 4, (k // 2) % 2, k % 2
             if on_tensor(k) and j == 0:
                 tp = ps_tp.tile([P, 2, P, 4], BF16, name="pb", tag="tp")
-                yv = ys[(2 * g + h) % 3][:].rearrange("p s (q j w e c) -> p s q j e c w", q=2, j=2, w=P, e=2, c=C)
+                yv = ys[(2 * g + h) % 3][:].rearrange("p s (q j w c) -> p s q j c w", q=2, j=2, w=P, c=C)
                 for q in range(2):
                     for j2 in range(2):
-                        for s, i0, i1 in ((0, 0, 48), (1, 48, 96), (2, 96, P)):
+                        for s, i0, i1 in SLOTS:
                             nc.tensor.matmul(
                                 out=tp[:, q, i0:i1, 2 * j2 : 2 * j2 + 2],
-                                lhsT=yv[:, s, q, j2, 0, c, :],
+                                lhsT=yv[:, s, q, j2, c, :],
                                 rhs=zts[g % 2][:, 2 * h + c, 2 * i0 : 2 * i1].rearrange("p (i e) -> p i e", e=2),
                                 start=True,
                                 stop=True,
@@ -518,7 +510,7 @@ def tile_shapeletencoder_pa_t_kernel(tc, x, W0, b0, W1, b1, out):
             if k == 2:
                 tree_ops = [(1, idx) for idx in range(5, LEVELS)]
             gz = (k + 1) // 4
-            z_now = (k + 1) % 4 == 0 and gz < NG
+            z_now = (k + 1) % 4 == 0 and gz < NG - 1
             third = (len(tree_ops) + 2) // 3
             cut = (0, third, 2 * third, len(tree_ops))
             chi_q, chi_g, chi_l1, chi_i, chi_i2 = (
@@ -535,7 +527,7 @@ def tile_shapeletencoder_pa_t_kernel(tc, x, W0, b0, W1, b1, out):
             now_i2 = (k - LAG_I2) % 2 == 0 and chi_i2 >= 0
             u0 = 2 * (k - LAG_U)
             f0 = 2 * (k - LAG_F)
-            if name == "x" and k % 4 in (0, 3) and 2 <= k // 4 + 1 < NG:
+            if name == "x" and k % 4 in (0, 3) and 2 <= k // 4 + 1 < NG - 1:
                 load_y(k // 4 + 1, (k % 4 // 3,))
             if name == "x" and k % 4 == 0 and 3 <= k // 4 + 2 < NG:
                 load_x(k // 4 + 2)
@@ -548,7 +540,8 @@ def tile_shapeletencoder_pa_t_kernel(tc, x, W0, b0, W1, b1, out):
                 if k == 3:
                     quantise_w0(2)
                     mid_neg(gc)
-                mid_cols(gc)
+                if gc < NG - 1:
+                    mid_cols(gc)
             if name == "mn" and chain_now and k != 3:
                 mid_neg(gc)
             if name == "sub":

from contextlib import ExitStack

import concourse.mybir as mybir
from concourse.masks import make_identity

BF16 = mybir.dt.bfloat16
F32 = mybir.dt.float32
U32 = mybir.dt.uint32
U8 = mybir.dt.uint8
FP8X4 = mybir.dt.float8_e4m3fn_x4
ALU = mybir.AluOpType
ACT = mybir.ActivationFunctionType
AX = mybir.AxisListType

P = 128
NG = 8
CELLS = 512
L = 1024
C = 2
K0 = 512
K1 = 128
NA = 4
FLOPS = 2 * C * NG * CELLS * L * K0 + 2 * C * NG * CELLS * K0 * K1

NSLOT = 4 * NG
LAST = 2 * NG - 1
LAG_A = 5
LAG_Q = 3
LAG_U = 3
LAG_F = 4
LAG_G = 6
LAG_L1 = 7
LAG_I = 8
LAG_I2 = 9
LEVELS = 12
TAIL = [("b1", -3, 0), ("ev", 0), ("L0", -2, 0, 0), ("R0", -4, 0, 0), ("qn", 0), ("ev", 1), ("L0", -1, 0, 0), ("R0", -3, 0, 0), ("rg", -2, 0), ("qn", 1), ("R0", -1, 0, 1), ("R0", -2, 0, 0), ("qh", -2, 0), ("L0", 0, 0, 1), ("L0", 1, 0, 1), ("L0", 2, 0, 1), ("R0", 0, 0, 0), ("L0", 3, 0, 1), ("R0", 1, 0, 0), ("L0", 0, 1, 0), ("R0", 2, 0, 0), ("L0", 1, 1, 0), ("R0", 3, 0, 0), ("rg", -1, 0), ("l1", -2, 0, 1), ("R0", 0, 1, 0), ("L0", 2, 1, 0), ("R0", 1, 1, 0), ("L0", 3, 1, 0), ("r1", -3, 0, 1), ("R0", 2, 1, 0), ("b1", -2, 0), ("R0", 3, 1, 0), ("qh", -1, 0), ("rg", 0, 0), ("l1", -1, 0, 1), ("qh", 0, 0), ("rg", 0, 1), ("l1", 0, 0, 1), ("b1", -1, 0), ("r1", -2, 0, 1), ("qh", 0, 1), ("l1", 0, 1, 1), ("b1", 0, 0), ("r1", -1, 0, 1), ("r1", 0, 0, 0), ("b1", 0, 1), ("r1", 0, 1, 0)]
ORDER = ["x", "ev0", "bt", "sub", "qn", "ev1", "rg", "ms", "l1", "f0", "zt", "T0", "b1", "mn", "R0a", "W", "L0a", "R0b", "qh", "f1", "x1", "zc", "T1", "T2", "r1", "L0b"]
A_PARTS = ((0,), (1,), (2, 3, 4, 5, 6, 7), tuple(range(8, LEVELS)))
SLOTS = ((0, 0, 48), (1, 48, 96), (2, 96, 128))
PIECES0 = (((0, 1), (1, 2)), ((2, 3), (3, 4)))


def sub_on_vector(k):
    return k >= NSLOT - 4


def swapped(chi):
    return chi <= 11 and chi % 4 != 1


def on_tensor(k):
    return 4 <= k < NSLOT - 4


def relu1_on_scalar(chi):
    return chi % 2 == 0 or chi < 4


def tile_shapeletencoder_pa_t_kernel(tc, x, W0, b0, W1, b1, out):
    nc = tc.nc
    with ExitStack() as ctx:
        const = ctx.enter_context(tc.tile_pool(name="const", bufs=1))
        xpool = ctx.enter_context(tc.tile_pool(name="xpool", bufs=3))
        scr = ctx.enter_context(tc.tile_pool(name="scr", bufs=1))
        small = ctx.enter_context(tc.tile_pool(name="small", bufs=2))
        npool = ctx.enter_context(tc.tile_pool(name="npool", bufs=3))
        gpool = ctx.enter_context(tc.tile_pool(name="gpool", bufs=2))
        hpool = ctx.enter_context(tc.tile_pool(name="hpool", bufs=2))
        opool = ctx.enter_context(tc.tile_pool(name="opool", bufs=2))
        wstage = ctx.enter_context(tc.tile_pool(name="wstage", bufs=2))
        ps_tp = ctx.enter_context(tc.psum_pool(name="ps_tp", bufs=3))
        ps_acc = ctx.enter_context(tc.psum_pool(name="ps_acc", bufs=3))
        ps_o = ctx.enter_context(tc.psum_pool(name="ps_o", bufs=1))
        ps_ch = ctx.enter_context(tc.psum_pool(name="ps_ch", bufs=1))
        ctx.enter_context(tc.manual_schedule())

        xs = {}
        his = {}
        los = {}
        sts = {}
        nsums = {}
        negmids = {}
        nts = {}
        tps = {}
        gns = {}
        ncs = {}
        accs = {}
        hps = {}
        hgs = {}
        hcs = {}
        zps = {}
        ops_ = {}
        ots = {}
        xps = {}
        osbs = {}
        w0gs = {}

        def x_view(g):
            return x[g].rearrange("(a p s) c -> p a (s c)", a=NA, p=P, s=L)

        def load_x(g, pieces=((0, NA),)):
            if g not in xs:
                xs[g] = xpool.tile([P, NA, C * L], BF16, name="xg", tag="xg")
            for lo, hi in pieces:
                nc.sync.dma_start(out=xs[g][:, lo:hi, :], in_=x_view(g)[:, lo:hi, :])

        def load_y(g, hs=(0, 1)):
            cells = x[g].rearrange("(a n q d s) c -> a d n q (s c)", a=NA, n=P, q=2, d=2, s=L // 4)
            for h in hs:
                y = ys[(2 * g + h) % 3][:].rearrange("p s (q m) -> p s q m", q=2)
                for s, i0, i1 in SLOTS:
                    for e in range(2):
                        nc.sync.dma_start(out=y[e : 2 * (i1 - i0) : 2, s, :, :], in_=cells[2 * h, e, i0:i1])

        ys = []
        for i in range(3):
            y = const.tile([P, 3, C * L // 2], BF16, name="y%d" % i, tag="y%d" % i)
            ys.append(y)

        identf = const.tile([P, P], F32, name="identf", tag="identf")
        make_identity(nc, identf[:])
        identb = const.tile([P, P], BF16, name="identb", tag="identb")
        make_identity(nc, identb[:])
        def ones(i, engine):
            pair = 1.0 + 0x3F80 / 2.0**23
            engine.memset(ys[i][96:P, 0:2, :].bitcast(F32), pair)
            engine.memset(ys[i][64:P, 2, :].bitcast(F32), pair)

        warm = const.tile([P, 1], F32, name="warm", tag="warm")
        nc.vector.memset(warm[:], 0.0)
        nc.scalar.activation(out=warm[:], in_=warm[:], func=ACT.Identity)
        ones(2, nc.vector)
        ones(0, nc.vector)
        ones(1, nc.vector)
        zs = []
        zts = []
        for i in range(2):
            z = const.tile([P, 4, P], F32, name="z%d" % i, tag="z%d" % i)
            nc.gpsimd.memset(z[:], 0.0)
            zs.append(z)
            zt = const.tile([P, 4, 2 * P], BF16, name="zt%d" % i, tag="zt%d" % i)
            zts.append(zt)

        def unit_blocks(i):
            for s, n in ((0, 96), (96, 96), (192, 64)):
                nc.vector.tensor_copy(
                    out=zts[i][0:96, :, s : s + n], in_=identb[0:96, 0:n].unsqueeze(1).to_broadcast([96, 4, n])
                )

        w0raw = const.tile([P, C, 8, K0], BF16, name="w0raw", tag="w0raw")
        w0dram = W0.rearrange("c (g d j w) f -> w c g j d f", g=2, d=2, j=2, w=P)
        w0rv = w0raw[:].rearrange("w c (g t) f -> w c g t f", g=2, t=4)

        def load_w0(i):
            c, gk = i // 2, i % 2
            for j in range(2):
                nc.sync.dma_start(out=w0rv[:, c, gk, 2 * j : 2 * j + 2, :], in_=w0dram[:, c, gk, j, :, :])

        load_x(0, PIECES0[0])
        load_w0(0)
        load_w0(1)
        load_x(0, PIECES0[1])
        load_w0(2)
        load_w0(3)
        load_x(1)
        bz = const.tile([P, P], BF16, name="bz", tag="bz")
        nc.vector.memset(bz[:], 0.0)
        nc.sync.dma_start(out=bz[0:8, :], in_=b0.rearrange("c (t p) -> (c t) p", t=4, p=P))
        nc.sync.dma_start(out=bz[8:10, :], in_=b1)
        w1raw = const.tile([P, 8, K1], BF16, name="w1raw", tag="w1raw")
        nc.sync.dma_start(out=w1raw[:], in_=W1.rearrange("c (t p) k -> p (c t) k", t=4, p=P))
        load_x(2)
        load_y(1)
        b1b = const.tile([P, C, K1], BF16, name="b1b", tag="b1b")
        nc.sync.dma_start(
            out=b1b[:].rearrange("p c k -> p (c k)"),
            in_=b1.rearrange("c k -> (c k)").partition_broadcast(P),
        )

        b0col = const.tile([P, 10], F32, name="b0col", tag="b0col")
        w0codes = const.tile([P, C, 2, K0], U32, name="w0codes", tag="w0codes", align_bytes=64)
        w0sc = const.tile([P, C, 2, K0], U8, name="w0sc", tag="w0sc", align_bytes=64)
        w1codes = const.tile([P, C, K1], U32, name="w1codes", tag="w1codes", align_bytes=64)
        w1sc = const.tile([P, C, K1], U8, name="w1sc", tag="w1sc", align_bytes=64)
        w1g = const.tile([P, C, K1, 4], BF16, name="w1g", tag="w1g", align_bytes=64)

        def a_op(g, idx, lo=0, hi=NA):
            xg = xs[g]
            if g not in his:
                his[g] = scr.tile([P, NA, L], BF16, name="hi", tag="hi")
                los[g] = scr.tile([P, NA, L], BF16, name="lo", tag="lo")
                sts[g] = small.tile([P, 2, NA, C], F32, name="st", tag="st")
            t = his[g] if idx % 2 == 0 else los[g]
            op = ALU.max if idx % 2 == 0 else ALU.min
            h = L >> (idx // 2)
            if idx < 2:
                nc.vector.tensor_tensor(out=t[:, lo:hi, :], in0=xg[:, lo:hi, 0:L], in1=xg[:, lo:hi, L : 2 * L], op=op)
            elif idx < LEVELS - 2:
                nc.vector.tensor_tensor(out=t[:, lo:hi, 0:h], in0=t[:, lo:hi, 0:h], in1=t[:, lo:hi, h : 2 * h], op=op)
            else:
                nc.vector.tensor_reduce(
                    out=sts[g][:, idx % 2, lo:hi, :],
                    in_=t[:, lo:hi, 0 : 2 * h].rearrange("p a (s c) -> p a c s", c=C),
                    axis=AX.X,
                    op=op,
                )

        def mid_sum(g, lo=0, hi=NA):
            nsums[(g, lo)] = small.tile([P, NA, C], F32, name="msum", tag="msum")
            nc.vector.tensor_tensor(
                out=nsums[(g, lo)][:, lo:hi, :], in0=sts[g][:, 0, lo:hi, :], in1=sts[g][:, 1, lo:hi, :], op=ALU.add
            )

        def mid_neg(g, lo=0, hi=NA):
            nm = small.tile([P, NA, C], F32, name="negmid", tag="negmid")
            nc.vector.tensor_scalar(
                out=nm[:, lo:hi, :], in0=nsums[(g, lo)][:, lo:hi, :], scalar1=-0.5, scalar2=None, op0=ALU.mult
            )
            for a in range(lo, hi):
                negmids[(g, a)] = nm

        def mid_cols(g):
            pairs_ = zs[g % 2][:].bitcast(BF16).rearrange("p (h c) (k d) -> p d h c k", c=C, d=2)
            for e in range(2):
                nc.vector.tensor_scalar(
                    out=pairs_[:, e, :, :, 96:98],
                    in0=sts[g][:].rearrange("p m (h two) c -> p two h c m", two=2)[:, 0],
                    scalar1=-0.5,
                    scalar2=None,
                    op0=ALU.mult,
                )

        def turn_mid(g):
            zps[g] = ps_tp.tile([P, 4, P], F32, name="zp", tag="tp")
            for i in range(4):
                nc.tensor.transpose(out=zps[g][:, i, :], in_=zs[g % 2][:, i, :], identity=identf[:])

        def copy_mid(g):
            nc.scalar.copy(out=zts[g % 2][96:P].bitcast(F32), in_=zps[g][96:P])

        def subtract(k):
            g, c, h = k // 4, (k // 2) % 2, k % 2
            nts[k] = npool.tile([P, 2, L], BF16, name="nt", tag="nt")
            for a in (2 * h + 1,) if on_tensor(k) else (2 * h, 2 * h + 1):
                src = xs[g][:, a, :].rearrange("p (q d m c) -> p c q m d", q=2, d=2, c=C)[:, c]
                dst = nts[k][:, a % 2, :].rearrange("p (q m d) -> p q m d", q=2, d=2)
                bias = negmids[(g, a)][:, a, c : c + 1]
                if sub_on_vector(k):
                    nc.vector.tensor_scalar(out=dst, in0=src, scalar1=bias, scalar2=None, op0=ALU.add)
                else:
                    nc.scalar.activation(out=dst, in_=src, func=ACT.Identity, bias=bias, scale=1.0)

        def fill(k, j):
            g, c, h = k // 4, (k // 2) % 2, k % 2
            if on_tensor(k) and j == 0:
                tp = ps_tp.tile([P, 2, P, 4], BF16, name="pb", tag="tp")
                yv = ys[(2 * g + h) % 3][:].rearrange("p s (q j w c) -> p s q j c w", q=2, j=2, w=P, c=C)
                for q in range(2):
                    for j2 in range(2):
                        for s, i0, i1 in SLOTS:
                            nc.tensor.matmul(
                                out=tp[:, q, i0:i1, 2 * j2 : 2 * j2 + 2],
                                lhsT=yv[:, s, q, j2, c, :],
                                rhs=zts[g % 2][:, 2 * h + c, 2 * i0 : 2 * i1].rearrange("p (i e) -> p i e", e=2),
                                start=True,
                                stop=True,
                            )
            else:
                a = 2 * h + min(j, 1)
                tp = ps_tp.tile([P, 2, 2, P], F32, name="tp", tag="tp")
                words = nts[k][:, a % 2, :].bitcast(F32)
                for q in range(2):
                    for w in range(2):
                        o = 256 * q + P * w
                        nc.tensor.transpose(out=tp[:, q, w, :], in_=words[:, o : o + P], identity=identf[:])
            tps[(k, j)] = tp

        def parts(chi):
            return 2 if chi == LAST else 1

        def g_view(chi):
            if parts(chi) == 2:
                return gns[chi][:].rearrange("p (h g w) -> p g h w", h=2, g=2)
            return gns[chi][:].rearrange("p (g h w) -> p g h w", h=2, g=2)

        def evacuate(k, j):
            chi, h = k // 2, k % 2
            if h == 0 and j == 0:
                gns[chi] = gpool.tile([P, 8 * CELLS], BF16, name="gn", tag="gn", align_bytes=64)
            tp = tps[(k, j)]
            gv = g_view(chi)
            if on_tensor(k) and j == 0:
                nc.scalar.copy(out=gv[:, :, h, 0:512], in_=tp[:].rearrange("p q x t -> p q (x t)"))
            else:
                i = min(j, 1)
                o = gv[:, :, h, 512 * i : 512 * (i + 1)].bitcast(F32)
                nc.scalar.copy(
                    out=o.rearrange("p q (x j) -> p q x j", j=2), in_=tp[:].rearrange("p q j x -> p q x j")
                )

        def quantise_n(chi, part=0):
            n = 2 * CELLS // parts(chi)
            if part == 0:
                codes = gpool.tile([P, 2 * CELLS], U32, name="ncodes", tag="ncodes", align_bytes=64)
                sc = gpool.tile([P, 2 * CELLS], U8, name="nsc", tag="nsc", align_bytes=64)
                ncs[chi] = (codes, sc)
            codes, sc = ncs[chi]
            nc.vector.quantize_mx(
                out=codes[:, n * part : n * (part + 1)].bitcast(FP8X4),
                scales=sc[:, n * part : n * (part + 1)],
                in_=gns[chi][:, 4 * n * part : 4 * n * (part + 1)],
            )

        def layer0(u, part=0, pool=None):
            chi, m = u // 4, u % 4
            c = chi % 2
            n = CELLS // parts(chi)
            codes, sc = ncs[chi]
            if pool is None:
                acc = ps_acc.tile([P, CELLS], F32, name="acc", tag="acc")
            else:
                acc = pool.tile([P, CELLS], F32, name="acc", tag="tp")
            accs[(u, part)] = acc
            for gk in range(2):
                o = n * (2 * part + gk)
                nc.tensor.matmul_mx(
                    out=acc[:, 0:n],
                    lhsT=w0codes[:, c, gk, P * m : P * (m + 1)].bitcast(FP8X4),
                    lhsT_scale=w0sc[:, c, gk, P * m : P * (m + 1)],
                    rhs=codes[:, o : o + n].bitcast(FP8X4),
                    rhs_scale=sc[:, o : o + n],
                    start=(gk == 0),
                    stop=(gk == 1),
                )

        def relu0(u, part=0, on_vector=False):
            chi, m = u // 4, u % 4
            c = chi % 2
            n = CELLS // parts(chi)
            if m == 0 and part == 0:
                hps[chi] = hpool.tile([P, 4, CELLS], BF16, name="hp", tag="hp")
            bias = b0col[:, 4 * c + m : 4 * c + m + 1]
            o = hps[chi][:, m, n * part : n * (part + 1)]
            if on_vector:
                nc.vector.tensor_scalar(
                    out=o, in0=accs[(u, part)][:, 0:n], scalar1=bias, scalar2=0.0, op0=ALU.add, op1=ALU.max
                )
            else:
                nc.scalar.activation(out=o, in_=accs[(u, part)][:, 0:n], func=ACT.Relu, bias=bias, scale=1.0)

        def regroup_h(chi, part=0):
            n = CELLS // parts(chi)
            if part == 0:
                hgs[chi] = hpool.tile([P, CELLS, 4], BF16, name="hg", tag="hg", align_bytes=64)
            nc.vector.tensor_copy(
                out=hgs[chi][:, n * part : n * (part + 1), :].rearrange("p (w i) t -> p w t i", i=4),
                in_=hps[chi][:, :, n * part : n * (part + 1)].rearrange("p t (w i) -> p w t i", i=4),
            )

        def quantise_h(chi, part=0):
            n = CELLS // parts(chi)
            if part == 0:
                codes = hpool.tile([P, CELLS], U32, name="hcodes", tag="hcodes", align_bytes=64)
                sc = hpool.tile([P, CELLS], U8, name="hsc", tag="hsc", align_bytes=64)
                hcs[chi] = (codes, sc)
            codes, sc = hcs[chi]
            nc.vector.quantize_mx(
                out=codes[:, n * part : n * (part + 1)].bitcast(FP8X4),
                scales=sc[:, n * part : n * (part + 1)],
                in_=hgs[chi][:, n * part : n * (part + 1), :].rearrange("p w t -> p (w t)"),
            )

        def layer1(chi, part=0, pool=None):
            c = chi % 2
            codes, sc = hcs[chi]
            nb = 4 // parts(chi)
            if pool is None:
                ops_[(chi, part)] = ps_o.tile([P, 4, K1], F32, name="o_ps", tag="o")
            else:
                ops_[(chi, part)] = pool.tile([P, 4, K1], F32, name="o_ps", tag="tp")
            for jj in range(nb):
                b = nb * part + jj
                nc.tensor.matmul_mx(
                    out=ops_[(chi, part)][:, jj, :],
                    lhsT=codes[:, P * b : P * (b + 1)].bitcast(FP8X4),
                    lhsT_scale=sc[:, P * b : P * (b + 1)],
                    rhs=w1codes[:, c, :].bitcast(FP8X4),
                    rhs_scale=w1sc[:, c, :],
                    start=True,
                    stop=True,
                )

        def layer1_t(chi):
            c = chi % 2
            codes, sc = hcs[chi]
            ops_[chi] = ps_o.tile([P, CELLS], F32, name="ot_ps", tag="o")
            nc.tensor.matmul_mx(
                out=ops_[chi][:],
                lhsT=w1codes[:, c, :].bitcast(FP8X4),
                lhsT_scale=w1sc[:, c, :],
                rhs=codes[:].bitcast(FP8X4),
                rhs_scale=sc[:],
                start=True,
                stop=True,
            )

        def bias_relu_t(chi):
            c = chi % 2
            ots[chi] = opool.tile([P, CELLS], F32, name="ot", tag="ot")
            nc.scalar.activation(
                out=ots[chi][:], in_=ops_[chi][:], func=ACT.Relu, bias=b0col[:, 8 + c : 9 + c], scale=1.0
            )

        def turn_back(chi):
            xps[chi] = ps_ch.tile([P, 4, P], F32, name="ox", tag="ch")
            for j in range(4):
                nc.tensor.transpose(out=xps[chi][:, j, :], in_=ots[chi][:, P * j : P * (j + 1)], identity=identf[:])

        def copy_out(chi):
            g, c = chi // 2, chi % 2
            if c == 0:
                osbs[g] = opool.tile([P, 4, C, K1], F32, name="osb", tag="osb")
            nc.scalar.copy(out=osbs[g][:, :, c, :], in_=xps[chi][:])

        def bias1(chi, part=0):
            g, c = chi // 2, chi % 2
            nb = 4 // parts(chi)
            if c == 0:
                osbs[g] = opool.tile([P, 4, C, K1], F32, name="osb", tag="osb")
            nc.vector.tensor_tensor(
                out=osbs[g][:, nb * part : nb * (part + 1), c, :],
                in0=ops_[(chi, part)][:, 0:nb, :],
                in1=b1b[:, c, :].unsqueeze(1).to_broadcast([P, nb, K1]),
                op=ALU.add,
            )

        def relu1(chi, part=0, on_scalar=None):
            g, c = chi // 2, chi % 2
            nb = 4 // parts(chi)
            o = osbs[g][:, nb * part : nb * (part + 1), c, :]
            if relu1_on_scalar(chi) if on_scalar is None else on_scalar:
                nc.scalar.activation(out=o, in_=o, func=ACT.Relu)
            else:
                nc.vector.tensor_scalar_max(out=o, in0=o, scalar1=0.0)

        def store(chi, part=0):
            g, c = chi // 2, chi % 2
            nb = 4 // parts(chi)
            nc.sync.dma_start(
                out=out[g].rearrange("(j p) c k -> p j c k", p=P)[:, nb * part : nb * (part + 1), c, :],
                in_=osbs[g][:, nb * part : nb * (part + 1), c, :],
            )

        def regroup_w0(i):
            c, gk = i // 2, i % 2
            w0gs[i] = wstage.tile([P, K0, 4], BF16, name="w0g", tag="w0g", align_bytes=64)
            nc.scalar.copy(
                out=w0gs[i][:].rearrange("q (w i) t -> q w t i", i=4),
                in_=w0rv[:, c, gk, :, :].rearrange("q t (w i) -> q w t i", i=4),
            )

        def quantise_w0(i):
            c, gk = i // 2, i % 2
            nc.vector.quantize_mx(
                out=w0codes[:, c, gk, :].bitcast(FP8X4),
                scales=w0sc[:, c, gk, :],
                in_=w0gs[i][:].rearrange("q w t -> q (w t)"),
            )

        def pairs(lo, hi):
            a_op(0, 0, lo, hi)
            a_op(0, 1, lo, hi)

        def levels(lo, hi):
            for idx in range(2, LEVELS):
                a_op(0, idx, lo, hi)

        regroup_w0(0)
        for piece in PIECES0[0]:
            pairs(*piece)
        levels(0, 2)
        regroup_w0(1)
        a_op(0, 0, 2, 3)
        mid_sum(0, 0, 2)
        a_op(0, 1, 2, 3)
        mid_neg(0, 0, 2)
        subtract(0)
        for j in range(2):
            fill(0, j)
        quantise_w0(0)
        regroup_w0(2)
        pairs(3, 4)
        levels(2, 4)
        for j in range(2):
            evacuate(0, j)
        quantise_w0(1)
        mid_sum(0, 2, 4)
        a_op(1, 0)
        mid_neg(0, 2, 4)
        regroup_w0(3)
        a_op(1, 1)

        def act(name, k):
            gc = (k + 1) // 4
            chain_now = (k + 1) % 4 == 0 and gc < NG
            ga, j = (k + LAG_A) // 4, (k + LAG_A) % 4
            tree_ops = [(ga, idx) for idx in A_PARTS[j]] if ga < NG else []
            if k == 1:
                tree_ops = [(1, 2), (1, 3), (1, 4)]
            if k == 2:
                tree_ops = [(1, idx) for idx in range(5, LEVELS)]
            gz = (k + 1) // 4
            z_now = (k + 1) % 4 == 0 and gz < NG - 1
            third = (len(tree_ops) + 2) // 3
            cut = (0, third, 2 * third, len(tree_ops))
            chi_q, chi_g, chi_l1, chi_i, chi_i2 = (
                (k - LAG_Q) // 2,
                (k - LAG_G) // 2,
                (k - LAG_L1) // 2,
                (k - LAG_I) // 2,
                (k - LAG_I2) // 2,
            )
            now_q = (k - LAG_Q) % 2 == 0 and chi_q >= 0
            now_g = (k - LAG_G) % 2 == 0 and chi_g >= 0
            now_l1 = (k - LAG_L1) % 2 == 0 and chi_l1 >= 0
            now_i = (k - LAG_I) % 2 == 0 and chi_i >= 0
            now_i2 = (k - LAG_I2) % 2 == 0 and chi_i2 >= 0
            u0 = 2 * (k - LAG_U)
            f0 = 2 * (k - LAG_F)
            if name == "x" and k % 4 in (0, 3) and 2 <= k // 4 + 1 < NG - 1:
                load_y(k // 4 + 1, (k % 4 // 3,))
            if name == "x" and k % 4 == 0 and 3 <= k // 4 + 2 < NG:
                load_x(k // 4 + 2)
            if name == "ev0" and k > 1:
                evacuate(k - 1, 0)
            if name == "ev1" and k > 1:
                evacuate(k - 1, 1)
            if name == "ms" and chain_now:
                mid_sum(gc)
                if k == 3:
                    quantise_w0(2)
                    mid_neg(gc)
                if gc < NG - 1:
                    mid_cols(gc)
            if name == "mn" and chain_now and k != 3:
                mid_neg(gc)
            if name == "sub":
                subtract(k)
                done.add(k)
            if name in ("f0", "f1"):
                assert (on_tensor(k) and name == "f0") or k in done
                fill(k, int(name[1]))
            if name == "zt" and z_now:
                turn_mid(gz)
            if name == "zc" and z_now:
                copy_mid(gz)
            if name == "qn" and now_q:
                quantise_n(chi_q)
            if name == "rg" and now_g:
                regroup_h(chi_g)
                done.add(("rg", chi_g))
            if name == "qh" and now_g:
                assert ("rg", chi_g) in done
                quantise_h(chi_g)
            if name == "l1" and now_l1:
                if swapped(chi_l1):
                    layer1_t(chi_l1)
                else:
                    layer1(chi_l1)
            if name == "bt" and now_i and swapped(chi_i):
                bias_relu_t(chi_i)
            if name == "x1" and now_i and swapped(chi_i):
                turn_back(chi_i)
            if name == "b1" and now_i and not swapped(chi_i):
                bias1(chi_i)
            if name == "r1" and now_i2:
                if swapped(chi_i2):
                    copy_out(chi_i2)
                else:
                    relu1(chi_i2)
                store(chi_i2)
            if name in ("T0", "T1", "T2"):
                q = int(name[1])
                assert q == 0 or ("T%d" % (q - 1), k, "s") in done
                done.add((name, k, "s"))
                for g, idx in tree_ops[cut[q] : cut[q + 1]]:
                    a_op(g, idx)
            if name == "R0a" and f0 >= 0:
                relu0(f0)
            if name == "R0b" and f0 >= 0:
                relu0(f0 + 1)
            if name == "L0a" and u0 >= 0:
                layer0(u0)
            if name == "L0b" and u0 >= 0:
                layer0(u0 + 1)
            if name == "W":
                if k in (1, 2):
                    unit_blocks(2 - k)
                if k == 1:
                    bzt = ps_ch.tile([P, P], BF16, name="bzt", tag="ch")
                    nc.tensor.transpose(out=bzt[:], in_=bz[:], identity=identb[:])
                    nc.vector.tensor_copy(out=b0col[:], in_=bzt[:, 0:10])
                if k == 2:
                    nc.scalar.copy(out=w1g[:], in_=w1raw[:].rearrange("p (c t) k -> p c k t", c=C, t=4))
                if k == 4:
                    quantise_w0(3)
                if k == 5:
                    nc.vector.quantize_mx(
                        out=w1codes[:].rearrange("p c k -> p (c k)").bitcast(FP8X4),
                        scales=w1sc[:].rearrange("p c k -> p (c k)"),
                        in_=w1g[:].rearrange("p c k t -> p (c k t)"),
                    )

        done = set()
        for k in range(1, NSLOT):
            for name in ORDER:
                act(name, k)

        ul = 4 * LAST

        def tact(t):
            n = t[0]
            if n == "ev":
                evacuate(NSLOT - 1, t[1])
            elif n == "qn":
                quantise_n(LAST, t[1])
            elif n == "L0":
                layer0(ul + t[1], t[2], ps_tp if t[3] else None)
            elif n == "R0":
                relu0(ul + t[1], t[2], t[3])
            elif n == "rg":
                regroup_h(LAST + t[1], t[2])
            elif n == "qh":
                quantise_h(LAST + t[1], t[2])
            elif n == "l1":
                layer1(LAST + t[1], t[2], ps_tp if t[3] else None)
            elif n == "b1":
                bias1(LAST + t[1], t[2])
            elif n == "r1":
                relu1(LAST + t[1], t[2], t[3])
                store(LAST + t[1], t[2])

        for t in TAIL:
            tact(t)
